import numpy as np
import ml_dtypes


def mxq(x, axis, fmt="e4m3"):
    dtype, down = {"e4m3": (ml_dtypes.float8_e4m3fn, 7), "e5m2": (ml_dtypes.float8_e5m2, 14)}[fmt]
    v = np.moveaxis(np.asarray(x, np.float32).astype(ml_dtypes.bfloat16).astype(np.float64), axis, -1)
    blocks = v.reshape(v.shape[:-1] + (-1, 32))
    amax = np.abs(blocks).max(-1, keepdims=True)
    byte = np.maximum(np.where(amax > 0, np.frexp(amax)[1] - 1 + 127, 0) - down, 1)
    scale = np.exp2(byte - 127.0)
    codes = (blocks / scale).astype(np.float32).astype(dtype).astype(np.float64)
    return np.moveaxis((codes * scale).reshape(v.shape), -1, axis)


WIDE = False


def mx_kscale(k):
    if not WIDE:
        return np.ones(k)
    levels = np.array([10, -10, 5, -5, 0])
    if k % 512:
        return np.exp2(np.random.permutation(np.resize(levels, k // 32))).repeat(32)
    a = np.empty((k // 512, 16))
    for p in range(k // 512):
        a[p, :8] = np.random.permutation(np.resize(levels, 8))
        for g in range(8):
            far = levels[np.abs(levels - a[p, g]) >= 10]
            a[p, g + 8] = far[np.random.randint(len(far))]
    return np.exp2(a.ravel()).repeat(32)


BF16 = ml_dtypes.bfloat16


def bf(x):
    return np.asarray(x, np.float32).astype(BF16)


def f64(x):
    return np.asarray(x).astype(np.float64)


E2M1 = np.array([0.0, 0.5, 1.0, 1.5, 2.0, 3.0, 4.0, 6.0, -0.0, -0.5, -1.0, -1.5, -2.0, -3.0, -4.0, -6.0])


def pack_weight(w, fmt):
    k, n = w.shape
    w = f64(bf(w)).reshape(k // 32, 32, n)
    amax = np.abs(w).max(1)
    if fmt == "e4m3":
        byte = np.frexp(amax)[1] - 1 + 127 - 7
    else:
        mant, ex = np.frexp(amax / 6.0)
        byte = np.where(mant > 0.5, ex, ex - 1) + 127
    byte = np.clip(np.where(amax > 0, byte, 1), 1, 254)
    scaled = (w * np.exp2(127.0 - byte)[:, None, :]).reshape(k, n).astype(np.float32)
    by_word = np.ascontiguousarray(scaled.reshape(k // 512, 128, 4, n).transpose(0, 1, 3, 2))
    if fmt == "e4m3":
        words = by_word.astype(ml_dtypes.float8_e4m3fn).view(np.uint8)
    else:
        c = by_word.astype(ml_dtypes.float4_e2m1fn).view(np.uint8) & 0xF
        words = c[..., 0::2] | (c[..., 1::2] << 4)
    return np.ascontiguousarray(words), np.ascontiguousarray(byte.astype(np.uint8).reshape(k // 512, 16, n))


def unpack_weight(words, scales, fmt):
    g, p, n, _ = words.shape
    if fmt == "e4m3":
        vals = np.ascontiguousarray(words).view(ml_dtypes.float8_e4m3fn).astype(np.float64)
    else:
        nib = np.empty((g, p, n, 4), np.uint8)
        nib[..., 0::2] = words & 0xF
        nib[..., 1::2] = words >> 4
        vals = E2M1[nib]
    vals = vals * np.repeat(np.exp2(scales.astype(np.float64) - 127.0), 8, axis=1)[..., None]
    return vals.transpose(0, 1, 3, 2).reshape(g * 512, n)
def pack4(w):
    words, scales = pack_weight(w, "e2m1")
    return words.reshape(words.shape[0], 128, -1), scales


def unpack4(words, scales):
    return unpack_weight(words.reshape(words.shape[0], 128, -1, 2), scales, "e2m1")


B, S, D, N, A, F = 64, 64, 512, 128, 128, 512


def draw0():
    s, t, u = mx_kscale(D), mx_kscale(F), mx_kscale(F)
    slots = bf(np.random.standard_normal((B, S, D)) * s)
    ident = bf(np.random.standard_normal((N, F)) * t)
    Wq = np.random.standard_normal((F, D)) / np.sqrt(D) / s[None, :] * u[:, None]
    Wk = np.random.standard_normal((F, F)) * 2.0 / np.sqrt(F) / t[None, :] / u[:, None]
    Wq_words, Wq_scales = pack4(Wq.T)
    Wk_words, Wk_scales = pack4(Wk.T)
    return {
        "slots": slots,
        "ident": ident,
        "Wq_words": Wq_words,
        "Wq_scales": Wq_scales,
        "Wk_words": Wk_words,
        "Wk_scales": Wk_scales,
    }


def core(slots, ident, Wq_words, Wq_scales, Wk_words, Wk_scales):
    q = mxq(f64(slots), 2, "e4m3") @ unpack4(Wq_words, Wq_scales)
    k = mxq(f64(ident), 1, "e4m3") @ unpack4(Wk_words, Wk_scales)
    logits = D ** (-0.5) * (mxq(k, 1, "e4m3") @ mxq(q, 2, "e4m3").transpose(0, 2, 1))
    e = np.exp(logits - logits.max(-1, keepdims=True))
    return e / e.sum(-1, keepdims=True)


def e4m3fn_bytes(y):
    return np.clip(np.asarray(y, np.float64), -448.0, 448.0).astype(np.float32).astype(ml_dtypes.float8_e4m3fn).view(np.uint8)


def e4m3fn_values(b):
    return np.asarray(b, np.uint8).view(ml_dtypes.float8_e4m3fn).astype(np.float64)


def setup_inputs():
    d = draw0()
    x0 = np.asarray(d['slots']).astype(np.float64)
    s = (np.max(np.abs(x0), axis=(0, 1), keepdims=True) / 448.0).astype(np.float32)
    out = {}
    for k, v in d.items():
        if k == 'slots':
            out['slots_bytes'] = e4m3fn_bytes(x0 / s.astype(np.float64))
            out['slots_scale'] = s
        else:
            out[k] = v
    return out


def reference(slots_bytes, slots_scale, ident, Wq_words, Wq_scales, Wk_words, Wk_scales):
    return core(e4m3fn_values(slots_bytes) * slots_scale.astype(np.float64), ident, Wq_words, Wq_scales, Wk_words, Wk_scales)

@@ -1,0 +1,392 @@
+from contextlib import ExitStack
+
+import concourse.mybir as mybir
+from concourse.masks import make_identity
+
+F32 = mybir.dt.float32
+BF16 = mybir.dt.bfloat16
+I32 = mybir.dt.int32
+U32 = mybir.dt.uint32
+U8 = mybir.dt.uint8
+FP8 = mybir.dt.float8_e4m3fn
+FP8X4 = mybir.dt.float8_e4m3fn_x4
+FP4X4 = mybir.dt.float4_e2m1fn_x4
+MULT = mybir.AluOpType.mult
+MAX = mybir.AluOpType.max
+AXIS_X = mybir.AxisListType.X
+COPY = mybir.ActivationFunctionType.Copy
+EXP = mybir.ActivationFunctionType.Exp
+
+P = 128
+PACK = 4
+SAMPLES, SLOTS, FEATURES, OBJECTS = 64, 64, 512, 128
+FLOPS = 2 * SAMPLES * SLOTS * FEATURES**2 + 2 * OBJECTS * FEATURES**2 + 2 * SAMPLES * OBJECTS * SLOTS * FEATURES
+LOGIT_SCALE = float(FEATURES) ** -0.5
+
+PAIRS = SAMPLES * SLOTS // (2 * P)
+LAST = PAIRS - 1
+UNITS = [(4 * u, 4) for u in range(7)] + [(28, 2), (30, 1), (31, 1)]
+Q, K = 0, 1
+
+
+def tile_actionbindingattention_pb_w4_kernel(
+    tc, slots_bytes, slots_scale, ident, Wq_words, Wq_scales, Wk_words, Wk_scales, out
+):
+    nc = tc.nc
+    with ExitStack() as ctx:
+        keep = ctx.enter_context(tc.tile_pool(name="keep", bufs=1))
+        work = ctx.enter_context(tc.tile_pool(name="work", bufs=4))
+        soft = ctx.enter_context(tc.tile_pool(name="soft", bufs=len(UNITS)))
+        turn_psum = ctx.enter_context(tc.psum_pool(name="turn_psum", bufs=2))
+        proj_psum = ctx.enter_context(tc.psum_pool(name="proj_psum", bufs=4))
+        logit_psum = ctx.enter_context(tc.psum_pool(name="logit_psum", bufs=2))
+        ctx.enter_context(tc.manual_schedule())
+
+        scale4 = keep.tile([P, PACK], F32, name="scale4")
+        nc.scalar.dma_start(out=scale4[:], in_=slots_scale.rearrange("a b (p t) -> p (a b t)", t=PACK))
+        ident_rows = keep.tile([P, FEATURES], BF16, name="ident_rows", align_bytes=64)
+        nc.scalar.dma_start(out=ident_rows[:], in_=ident)
+
+        warm = keep.tile([P, 1], F32, name="warm")
+        nc.vector.memset(warm[:], 0.0)
+        nc.scalar.activation(out=warm[:], in_=warm[:], func=EXP)
+        eye = keep.tile([P, P], F32, name="eye", align_bytes=64)
+        make_identity(nc, eye[:])
+
+        raw_bytes = []
+        rows = slots_bytes.rearrange("b s k -> (b s) k")
+
+        def load_slots(first, pairs):
+            t = keep.tile([P, 2 * pairs, FEATURES], U8, name="slots_%d" % first, align_bytes=64)
+            src = rows[first * 2 * P : (first + pairs) * 2 * P, :]
+            nc.sync.dma_start(out=t[:], in_=src.rearrange("(j p) k -> p j k", p=P))
+            for i in range(pairs):
+                raw_bytes.append(t[:, 2 * i : 2 * i + 2, :])
+
+        words_in = keep.tile([P, 2, 2 * FEATURES], U8, name="words_in", align_bytes=64)
+        scales_in = keep.tile([P, 2, FEATURES], U8, name="scales_in", align_bytes=64)
+        words = keep.tile([P, 2, 2 * FEATURES], U8, name="words", align_bytes=64)
+        scales = keep.tile([P, 2, FEATURES], U8, name="scales", align_bytes=64)
+        nc.vector.memset(scales_in[:].rearrange("p w n -> p (w n)").bitcast(I32), 0)
+
+        def load_weight(w, w_words, w_scales):
+            nc.sync.dma_start(out=words_in[:, w, :].bitcast(I32), in_=w_words[0].bitcast(I32))
+            for b in range(4):
+                nc.sync.dma_start(
+                    out=scales_in[32 * b : 32 * b + 4, w, :].bitcast(I32),
+                    in_=w_scales[0, 4 * b : 4 * b + 4, :].bitcast(I32),
+                )
+
+        load_slots(0, 1)
+        load_weight(Q, Wq_words, Wq_scales)
+        load_slots(1, 1)
+        load_weight(K, Wk_words, Wk_scales)
+        for first in range(2, PAIRS, 2):
+            load_slots(first, 2)
+
+        def permute_words(w):
+            nc.vector.tensor_copy(
+                out=words[:, w, :].bitcast(I32).rearrange("p (t g e) -> p t g e", t=PACK, e=2),
+                in_=words_in[:, w, :].bitcast(I32).rearrange("p (g t e) -> p t g e", t=PACK, e=2),
+            )
+
+        def permute_scales(w):
+            nc.vector.tensor_copy(
+                out=scales[:, w, :].bitcast(I32).rearrange("p (t g) -> p t g", t=PACK),
+                in_=scales_in[:, w, :].bitcast(I32).rearrange("p (g t) -> p t g", t=PACK),
+            )
+
+        scaled, turned, slots4, slots_q, proj, query4, query_q = {}, {}, {}, {}, {}, {}, {}
+        logits, tops, biases, exps, sums, inverses = {}, {}, {}, {}, {}, {}
+
+        scale_rows = keep.tile([P, 2, FEATURES], F32, name="scale_rows", align_bytes=64)
+
+        def scale_slots(i, tiles=(0, 1)):
+            if i not in scaled:
+                scaled[i] = work.tile([P, 2, FEATURES], BF16, name="scaled", align_bytes=64)
+            if i < 2:
+                for j in tiles:
+                    nc.vector.tensor_tensor(
+                        out=scaled[i][:, j, :],
+                        in0=raw_bytes[i][:, j, :].bitcast(FP8),
+                        in1=scale_rows[:, 0, :],
+                        op=MULT,
+                    )
+            else:
+                nc.vector.tensor_tensor(
+                    out=scaled[i][:].rearrange("p j k -> p (j k)"),
+                    in0=raw_bytes[i].rearrange("p j k -> p (j k)").bitcast(FP8),
+                    in1=scale_rows[:].rearrange("p j k -> p (j k)"),
+                    op=MULT,
+                )
+
+        def turn_rows(dst, src):
+            src_words = src.bitcast(F32)
+            for u in range(2):
+                nc.tensor.transpose(dst[:, u, :], src_words[:, u::2], eye[:])
+
+        def lay_rows(dst, src):
+            nc.scalar.copy(
+                out=dst.rearrange("p r t -> p (r t)").bitcast(F32).rearrange("p (r u) -> p r u", u=2),
+                in_=src.rearrange("p u r -> p r u"),
+            )
+
+        def turn_slots(i):
+            turned[i] = turn_psum.tile([P, 2, 2, P], F32, name="turned")
+            for j in range(2):
+                turn_rows(turned[i][:, j], scaled[i][:, j, :])
+
+        def lay_slots(i):
+            slots4[i] = work.tile([P, 2, P, PACK], BF16, name="slots4", align_bytes=64)
+            nc.scalar.copy(
+                out=slots4[i][:]
+                .rearrange("p j r t -> p j (r t)")
+                .bitcast(F32)
+                .rearrange("p j (r u) -> p j r u", u=2),
+                in_=turned[i][:].rearrange("p j u r -> p j r u"),
+            )
+
+        def turn_and_lay_first_pair():
+            slots4[0] = work.tile([P, 2, P, PACK], BF16, name="slots4", align_bytes=64)
+            for j in range(2):
+                bank = turn_psum.tile([P, 2, P], F32, name="turned")
+                turn_rows(bank, scaled[0][:, j, :])
+                lay_rows(slots4[0][:, j], bank[:])
+
+        def quantize_slots(i, lo=0, hi=2):
+            if i not in slots_q:
+                slots_q[i] = (
+                    work.tile([P, 2 * P], U32, name="slot_codes", align_bytes=64),
+                    work.tile([P, 2 * P], U8, name="slot_scales", align_bytes=64),
+                )
+            codes, code_scales = slots_q[i]
+            cols = slice(P * lo, P * hi)
+            nc.vector.quantize_mx(
+                out=codes[:, cols].bitcast(FP8X4),
+                scales=code_scales[:, cols],
+                in_=slots4[i][:, lo:hi].rearrange("p j r t -> p (j r t)"),
+            )
+
+        def project(w, codes, code_scales, fill=False):
+            bank = proj_psum.tile([P, PACK, P], F32, name="proj")
+            if fill:
+                nc.tensor.matmul(
+                    bank[:].rearrange("p t r -> p (t r)"),
+                    lhsT=ident_rows[:, :P],
+                    rhs=ident_rows[:],
+                    start=True,
+                    stop=True,
+                )
+            for t in range(PACK):
+                nc.tensor.matmul_mx(
+                    out=bank[:, t, :],
+                    lhsT=words[:, w, 2 * P * t : 2 * P * (t + 1)].bitcast(FP4X4),
+                    lhsT_scale=scales[:, w, P * t : P * (t + 1)],
+                    rhs=codes.bitcast(FP8X4),
+                    rhs_scale=code_scales,
+                    start=True,
+                    stop=True,
+                )
+            return bank
+
+        def queries(i, tiles=(0, 1), fill=True):
+            codes, code_scales = slots_q[i]
+            for j in tiles:
+                cols = slice(P * j, P * (j + 1))
+                proj[i, j] = project(Q, codes[:, cols], code_scales[:, cols], fill and j == 0)
+
+        def lay_query(i, j, copy):
+            if i not in query4:
+                query4[i] = work.tile([P, 2, P, PACK], BF16, name="query4", align_bytes=64)
+            copy(out=query4[i][:, j], in_=proj[i, j][:].rearrange("p t r -> p r t"))
+
+        def quantize_queries(i, lo=0, hi=2):
+            if i // 2 not in query_q:
+                query_q[i // 2] = (
+                    work.tile([P, 4 * P], U32, name="query_codes", align_bytes=64),
+                    work.tile([P, 4 * P], U8, name="query_scales", align_bytes=64),
+                )
+            codes, code_scales = query_q[i // 2]
+            first = 2 * (i % 2)
+            cols = slice(P * (first + lo), P * (first + hi))
+            nc.vector.quantize_mx(
+                out=codes[:, cols].bitcast(FP8X4),
+                scales=code_scales[:, cols],
+                in_=query4[i][:, lo:hi].rearrange("p j r t -> p (j r t)"),
+            )
+
+        def multiply_keys(u, pool=logit_psum, name="logits"):
+            first, tiles = UNITS[u]
+            logits[u] = pool.tile([P, 2 * tiles, SLOTS], F32, name=name)
+            codes, code_scales = query_q[first // 4]
+            cols = slice(P * (first % 4), P * (first % 4 + tiles))
+            nc.tensor.matmul_mx(
+                out=logits[u][:].rearrange("p b s -> p (b s)"),
+                lhsT=key_codes[:].bitcast(FP8X4),
+                lhsT_scale=key_scales[:],
+                rhs=codes[:, cols].bitcast(FP8X4),
+                rhs_scale=code_scales[:, cols],
+                start=True,
+                stop=True,
+            )
+
+        def find_tops(u):
+            tops[u] = soft.tile([P, 2 * UNITS[u][1]], F32, name="tops")
+            nc.vector.tensor_reduce(out=tops[u][:], in_=logits[u][:], axis=AXIS_X, op=MAX)
+
+        def negate_tops(u, on_scalar):
+            biases[u] = soft.tile([P, 2 * UNITS[u][1]], F32, name="biases")
+            if on_scalar:
+                nc.scalar.activation(out=biases[u][:], in_=tops[u][:], func=COPY, scale=-LOGIT_SCALE)
+            else:
+                nc.vector.tensor_scalar(
+                    out=biases[u][:], in0=tops[u][:], scalar1=-LOGIT_SCALE, scalar2=None, op0=MULT
+                )
+
+        def exponentiate(u, samples):
+            if u not in exps:
+                exps[u] = soft.tile([P, 2 * UNITS[u][1], SLOTS], F32, name="exps")
+                sums[u] = soft.tile([P, 2 * UNITS[u][1]], F32, name="sums")
+            for b in samples:
+                nc.scalar.activation(
+                    out=exps[u][:, b, :],
+                    in_=logits[u][:, b, :],
+                    func=EXP,
+                    bias=biases[u][:, b : b + 1],
+                    scale=LOGIT_SCALE,
+                    accum_out=sums[u][:, b : b + 1],
+                )
+
+        def invert_sums(u):
+            inverses[u] = soft.tile([P, 2 * UNITS[u][1]], F32, name="inverses")
+            nc.vector.reciprocal(out=inverses[u][:], in_=sums[u][:])
+
+        def divide_and_store(u, on_scalar=False):
+            first, tiles = UNITS[u]
+            samples = 2 * tiles
+            shares = soft.tile([P, samples, SLOTS], F32, name="shares")
+            if on_scalar:
+                for b in range(samples):
+                    nc.scalar.activation(
+                        out=shares[:, b, :], in_=exps[u][:, b, :], func=COPY, scale=inverses[u][:, b : b + 1]
+                    )
+            else:
+                nc.vector.tensor_tensor(
+                    out=shares[:],
+                    in0=exps[u][:],
+                    in1=inverses[u][:].unsqueeze(2).to_broadcast([P, samples, SLOTS]),
+                    op=MULT,
+                )
+            nc.sync.dma_start(
+                out=out[2 * first : 2 * first + samples].rearrange("b n s -> n b s"), in_=shares[:]
+            )
+
+        scale_bank = logit_psum.tile([P, PACK, P], F32, name="logits")
+        for t in range(PACK):
+            nc.tensor.transpose(scale_bank[:, t, :], scale4[:, t : t + 1].to_broadcast([P, P]), eye[:])
+        for j in range(2):
+            nc.scalar.copy(
+                out=scale_rows[:, j, :].rearrange("p (n t) -> p n t", t=PACK),
+                in_=scale_bank[:].rearrange("p t n -> p n t"),
+            )
+        ident4 = keep.tile([P, P, PACK], BF16, name="ident4", align_bytes=64)
+        ident_bank = logit_psum.tile([P, 2, P], F32, name="logits")
+        turn_rows(ident_bank, ident_rows[:])
+        lay_rows(ident4[:], ident_bank[:])
+
+        permute_words(Q)
+        scale_slots(0)
+        turn_and_lay_first_pair()
+        permute_scales(Q)
+        scale_slots(1, (0,))
+        quantize_slots(0, 0, 1)
+        queries(0, (0,))
+        scale_slots(1, (1,))
+        quantize_slots(0, 1, 2)
+        queries(0, (1,))
+        turn_slots(1)
+
+        permute_words(K)
+        permute_scales(K)
+        ident_codes = keep.tile([P, P], U32, name="ident_codes", align_bytes=64)
+        ident_scales = keep.tile([P, P], U8, name="ident_scales", align_bytes=64)
+        nc.vector.quantize_mx(
+            out=ident_codes[:].bitcast(FP8X4), scales=ident_scales[:], in_=ident4[:].rearrange("p r t -> p (r t)")
+        )
+        key_bank = project(K, ident_codes[:], ident_scales[:])
+        for j in range(2):
+            lay_query(0, j, nc.scalar.copy)
+        lay_slots(1)
+        scale_slots(2)
+        key4 = keep.tile([P, P, PACK], BF16, name="key4", align_bytes=64)
+        nc.scalar.copy(out=key4[:], in_=key_bank[:].rearrange("p t r -> p r t"))
+        key_codes = keep.tile([P, P], U32, name="key_codes", align_bytes=64)
+        key_scales = keep.tile([P, P], U8, name="key_scales", align_bytes=64)
+
+        for i in range(1, LAST):
+            u = i // 2
+            even = i % 2 == 0
+            if even and u >= 3:
+                invert_sums(u - 3)
+            if i + 2 <= LAST:
+                scale_slots(i + 2)
+            turn_slots(i + 1)
+            if even and u >= 2:
+                negate_tops(u - 2, on_scalar=True)
+            if i > 1:
+                lay_query(i - 1, 0, nc.scalar.copy)
+                lay_query(i - 1, 1, nc.scalar.copy if i + 2 <= LAST else nc.vector.tensor_copy)
+            quantize_slots(i)
+            queries(i)
+            if not even and u >= 1:
+                find_tops(u - 1)
+            quantize_queries(i - 1)
+            if i == 1:
+                nc.vector.quantize_mx(
+                    out=key_codes[:].bitcast(FP8X4), scales=key_scales[:], in_=key4[:].rearrange("p r t -> p (r t)")
+                )
+            if even:
+                multiply_keys(u - 1)
+                if u >= 2:
+                    exponentiate(u - 2, range(0, 4))
+                if u >= 3:
+                    divide_and_store(u - 3)
+            elif u >= 2:
+                exponentiate(u - 2, range(4, 8))
+            lay_slots(i + 1)
+
+        quantize_slots(15)
+        find_tops(6)
+        queries(15, fill=False)
+        lay_query(14, 0, nc.scalar.copy)
+        lay_query(14, 1, nc.scalar.copy)
+        lay_query(15, 0, nc.scalar.copy)
+        quantize_queries(14)
+        negate_tops(6, on_scalar=False)
+        multiply_keys(7, turn_psum, "turned")
+        lay_query(15, 1, nc.vector.tensor_copy)
+        quantize_queries(15, 0, 1)
+        find_tops(7)
+        exponentiate(5, range(4, 8))
+        quantize_queries(15, 1, 2)
+        invert_sums(5)
+        multiply_keys(8, turn_psum, "turned")
+        multiply_keys(9)
+        find_tops(8)
+        negate_tops(7, on_scalar=False)
+        exponentiate(6, range(8))
+        find_tops(9)
+        negate_tops(8, on_scalar=False)
+        divide_and_store(5)
+        exponentiate(7, range(4))
+        invert_sums(6)
+        exponentiate(8, range(2))
+        negate_tops(9, on_scalar=False)
+        invert_sums(7)
+        invert_sums(8)
+        divide_and_store(7, on_scalar=True)
+        divide_and_store(6)
+        exponentiate(9, range(2))
+        invert_sums(9)
+        divide_and_store(8)
+        divide_and_store(9)

@@ -47,9 +47,6 @@ def tile_actionbindingattention_pb_w4_kernel(
         ident_rows = keep.tile([P, FEATURES], BF16, name="ident_rows", align_bytes=64)
         nc.scalar.dma_start(out=ident_rows[:], in_=ident)
 
-        warm = keep.tile([P, 1], F32, name="warm")
-        nc.vector.memset(warm[:], 0.0)
-        nc.scalar.activation(out=warm[:], in_=warm[:], func=EXP)
         eye = keep.tile([P, P], F32, name="eye", align_bytes=64)
         make_identity(nc, eye[:])
 
@@ -167,16 +164,8 @@ def tile_actionbindingattention_pb_w4_kernel(
                 in_=slots4[i][:, lo:hi].rearrange("p j r t -> p (j r t)"),
             )
 
-        def project(w, codes, code_scales, fill=False):
+        def project(w, codes, code_scales):
             bank = proj_psum.tile([P, PACK, P], F32, name="proj")
-            if fill:
-                nc.tensor.matmul(
-                    bank[:].rearrange("p t r -> p (t r)"),
-                    lhsT=ident_rows[:, :P],
-                    rhs=ident_rows[:],
-                    start=True,
-                    stop=True,
-                )
             for t in range(PACK):
                 nc.tensor.matmul_mx(
                     out=bank[:, t, :],
@@ -189,11 +178,11 @@ def tile_actionbindingattention_pb_w4_kernel(
                 )
             return bank
 
-        def queries(i, tiles=(0, 1), fill=True):
+        def queries(i, tiles=(0, 1)):
             codes, code_scales = slots_q[i]
             for j in tiles:
                 cols = slice(P * j, P * (j + 1))
-                proj[i, j] = project(Q, codes[:, cols], code_scales[:, cols], fill and j == 0)
+                proj[i, j] = project(Q, codes[:, cols], code_scales[:, cols])
 
         def lay_query(i, j, copy):
             if i not in query4:
@@ -357,7 +346,7 @@ def tile_actionbindingattention_pb_w4_kernel(
 
         quantize_slots(15)
         find_tops(6)
-        queries(15, fill=False)
+        queries(15)
         lay_query(14, 0, nc.scalar.copy)
         lay_query(14, 1, nc.scalar.copy)
         lay_query(15, 0, nc.scalar.copy)

@@ -23,9 +23,20 @@ SAMPLES, SLOTS, FEATURES, OBJECTS = 64, 64, 512, 128
 FLOPS = 2 * SAMPLES * SLOTS * FEATURES**2 + 2 * OBJECTS * FEATURES**2 + 2 * SAMPLES * OBJECTS * SLOTS * FEATURES
 LOGIT_SCALE = float(FEATURES) ** -0.5
 
-PAIRS = SAMPLES * SLOTS // (2 * P)
-LAST = PAIRS - 1
-UNITS = [(4 * u, 4) for u in range(7)] + [(28, 2), (30, 1), (31, 1)]
+TILES = SAMPLES * SLOTS // P
+UNIT = 4
+STARTS = [0] + list(range(2, TILES, UNIT))
+GROUPS = len(STARTS)
+
+
+def place(tile):
+    return (0, tile) if tile < 2 else ((tile + 2) // UNIT, (tile + 2) % UNIT)
+
+
+def size(g):
+    return 2 if g in (0, GROUPS - 1) else UNIT
+
+
 Q, K = 0, 1
 
 
@@ -35,30 +46,22 @@ def tile_actionbindingattention_pb_w4_kernel(
     nc = tc.nc
     with ExitStack() as ctx:
         keep = ctx.enter_context(tc.tile_pool(name="keep", bufs=1))
-        work = ctx.enter_context(tc.tile_pool(name="work", bufs=4))
-        soft = ctx.enter_context(tc.tile_pool(name="soft", bufs=len(UNITS)))
+        work = ctx.enter_context(tc.tile_pool(name="work", bufs=3))
+        soft = ctx.enter_context(tc.tile_pool(name="soft", bufs=12))
         turn_psum = ctx.enter_context(tc.psum_pool(name="turn_psum", bufs=2))
         proj_psum = ctx.enter_context(tc.psum_pool(name="proj_psum", bufs=4))
         logit_psum = ctx.enter_context(tc.psum_pool(name="logit_psum", bufs=2))
         ctx.enter_context(tc.manual_schedule())
 
-        scale4 = keep.tile([P, PACK], F32, name="scale4")
-        nc.scalar.dma_start(out=scale4[:], in_=slots_scale.rearrange("a b (p t) -> p (a b t)", t=PACK))
-        ident_rows = keep.tile([P, FEATURES], BF16, name="ident_rows", align_bytes=64)
-        nc.scalar.dma_start(out=ident_rows[:], in_=ident)
-
-        eye = keep.tile([P, P], F32, name="eye", align_bytes=64)
-        make_identity(nc, eye[:])
-
-        raw_bytes = []
+        raw_bytes = {}
         rows = slots_bytes.rearrange("b s k -> (b s) k")
 
-        def load_slots(first, pairs):
-            t = keep.tile([P, 2 * pairs, FEATURES], U8, name="slots_%d" % first, align_bytes=64)
-            src = rows[first * 2 * P : (first + pairs) * 2 * P, :]
+        def load_slots(first, tiles):
+            t = keep.tile([P, tiles, FEATURES], U8, name="slots_%d" % first, align_bytes=64)
+            src = rows[first * P : (first + tiles) * P, :]
             nc.sync.dma_start(out=t[:], in_=src.rearrange("(j p) k -> p j k", p=P))
-            for i in range(pairs):
-                raw_bytes.append(t[:, 2 * i : 2 * i + 2, :])
+            for j in range(tiles):
+                raw_bytes[first + j] = (t, j)
 
         words_in = keep.tile([P, 2, 2 * FEATURES], U8, name="words_in", align_bytes=64)
         scales_in = keep.tile([P, 2, FEATURES], U8, name="scales_in", align_bytes=64)
@@ -66,20 +69,34 @@ def tile_actionbindingattention_pb_w4_kernel(
         scales = keep.tile([P, 2, FEATURES], U8, name="scales", align_bytes=64)
         nc.vector.memset(scales_in[:].rearrange("p w n -> p (w n)").bitcast(I32), 0)
 
-        def load_weight(w, w_words, w_scales):
+        def load_words(w, w_words):
             nc.sync.dma_start(out=words_in[:, w, :].bitcast(I32), in_=w_words[0].bitcast(I32))
+
+        def load_scales(w, w_scales):
             for b in range(4):
                 nc.sync.dma_start(
                     out=scales_in[32 * b : 32 * b + 4, w, :].bitcast(I32),
                     in_=w_scales[0, 4 * b : 4 * b + 4, :].bitcast(I32),
                 )
 
-        load_slots(0, 1)
-        load_weight(Q, Wq_words, Wq_scales)
-        load_slots(1, 1)
-        load_weight(K, Wk_words, Wk_scales)
-        for first in range(2, PAIRS, 2):
-            load_slots(first, 2)
+        scale4 = keep.tile([P, PACK], F32, name="scale4")
+        ident_rows = keep.tile([P, FEATURES], BF16, name="ident_rows", align_bytes=64)
+        load_slots(0, 2)
+        nc.scalar.dma_start(out=scale4[:], in_=slots_scale.rearrange("a b (p t) -> p (a b t)", t=PACK))
+        load_slots(2, 2)
+        load_words(Q, Wq_words)
+        load_slots(4, 4)
+        load_scales(Q, Wq_scales)
+        load_slots(8, 2)
+        nc.sync.dma_start(out=ident_rows[:], in_=ident)
+        load_words(K, Wk_words)
+        load_slots(10, 4)
+        load_scales(K, Wk_scales)
+        for g in range(4, GROUPS):
+            load_slots(STARTS[g], size(g))
+
+        eye = keep.tile([P, P], F32, name="eye", align_bytes=64)
+        make_identity(nc, eye[:])
 
         def permute_words(w):
             nc.vector.tensor_copy(
@@ -93,79 +110,68 @@ def tile_actionbindingattention_pb_w4_kernel(
                 in_=scales_in[:, w, :].bitcast(I32).rearrange("p (g t) -> p t g", t=PACK),
             )
 
-        scaled, turned, slots4, slots_q, proj, query4, query_q = {}, {}, {}, {}, {}, {}, {}
+        wide, turned, slots4, slots_q, proj, query4, query_q = {}, {}, {}, {}, {}, {}, {}
         logits, tops, biases, exps, sums, inverses = {}, {}, {}, {}, {}, {}
 
-        scale_rows = keep.tile([P, 2, FEATURES], F32, name="scale_rows", align_bytes=64)
+        planes = [keep.tile([P, UNIT * FEATURES], BF16, name="plane_%d" % n, align_bytes=64) for n in range(6)]
+        for g in range(GROUPS):
+            query4[g] = planes[g % 3][:].rearrange("p (r t) -> p r t", t=PACK)
+            slots4[g] = planes[3 if g == 0 else 4 + g % 2][:].rearrange("p (r t) -> p r t", t=PACK)
 
-        def scale_slots(i, tiles=(0, 1)):
-            if i not in scaled:
-                scaled[i] = work.tile([P, 2, FEATURES], BF16, name="scaled", align_bytes=64)
-            if i < 2:
-                for j in tiles:
-                    nc.vector.tensor_tensor(
-                        out=scaled[i][:, j, :],
-                        in0=raw_bytes[i][:, j, :].bitcast(FP8),
-                        in1=scale_rows[:, 0, :],
-                        op=MULT,
-                    )
-            else:
-                nc.vector.tensor_tensor(
-                    out=scaled[i][:].rearrange("p j k -> p (j k)"),
-                    in0=raw_bytes[i].rearrange("p j k -> p (j k)").bitcast(FP8),
-                    in1=scale_rows[:].rearrange("p j k -> p (j k)"),
-                    op=MULT,
-                )
+        def widen(first, tiles, copy, t=None):
+            if t is None:
+                t = keep.tile([P, tiles * FEATURES], BF16, name="wide_%d" % first, align_bytes=64)
+            src, j = raw_bytes[first]
+            copy(out=t[:, : tiles * FEATURES], in_=src[:, j : j + tiles, :].rearrange("p j k -> p (j k)").bitcast(FP8))
+            for i in range(tiles):
+                wide[first + i] = t[:, i * FEATURES : (i + 1) * FEATURES]
+
+        def widen_on_scalar(out, in_):
+            nc.scalar.activation(out=out, in_=in_, func=COPY)
 
         def turn_rows(dst, src):
             src_words = src.bitcast(F32)
             for u in range(2):
                 nc.tensor.transpose(dst[:, u, :], src_words[:, u::2], eye[:])
 
-        def lay_rows(dst, src):
-            nc.scalar.copy(
-                out=dst.rearrange("p r t -> p (r t)").bitcast(F32).rearrange("p (r u) -> p r u", u=2),
-                in_=src.rearrange("p u r -> p r u"),
+        def turn(first, tiles=2, pool=turn_psum, name="turned"):
+            turned[first] = pool.tile([P, 2, tiles, P], F32, name=name)
+            for j in range(tiles):
+                turn_rows(turned[first][:, :, j, :], wide[first + j])
+
+        def scale_slots(first, tiles=2):
+            u, j = place(first)
+            n = tiles * P
+            nc.vector.tensor_tensor(
+                out=slots4[u][:, j * P : j * P + n, :].rearrange("p r (h e) -> p r h e", e=2),
+                in0=turned[first][:].rearrange("p h j r -> p h (j r)").bitcast(BF16).rearrange("p h (r e) -> p r h e", e=2),
+                in1=scale4[:].rearrange("p (h e) -> p h e", e=2).unsqueeze(1).to_broadcast([P, n, 2, 2]),
+                op=MULT,
             )
 
-        def turn_slots(i):
-            turned[i] = turn_psum.tile([P, 2, 2, P], F32, name="turned")
-            for j in range(2):
-                turn_rows(turned[i][:, j], scaled[i][:, j, :])
-
-        def lay_slots(i):
-            slots4[i] = work.tile([P, 2, P, PACK], BF16, name="slots4", align_bytes=64)
-            nc.scalar.copy(
-                out=slots4[i][:]
-                .rearrange("p j r t -> p j (r t)")
-                .bitcast(F32)
-                .rearrange("p j (r u) -> p j r u", u=2),
-                in_=turned[i][:].rearrange("p j u r -> p j r u"),
-            )
-
-        def turn_and_lay_first_pair():
-            slots4[0] = work.tile([P, 2, P, PACK], BF16, name="slots4", align_bytes=64)
-            for j in range(2):
-                bank = turn_psum.tile([P, 2, P], F32, name="turned")
-                turn_rows(bank, scaled[0][:, j, :])
-                lay_rows(slots4[0][:, j], bank[:])
-
-        def quantize_slots(i, lo=0, hi=2):
-            if i not in slots_q:
-                slots_q[i] = (
-                    work.tile([P, 2 * P], U32, name="slot_codes", align_bytes=64),
-                    work.tile([P, 2 * P], U8, name="slot_scales", align_bytes=64),
+        def quantize(store, names, src, first, tiles):
+            u, j = place(first)
+            if u not in store:
+                store[u] = (
+                    work.tile([P, UNIT * P], U32, name=names[0], align_bytes=64),
+                    work.tile([P, UNIT * P], U8, name=names[1], align_bytes=64),
                 )
-            codes, code_scales = slots_q[i]
-            cols = slice(P * lo, P * hi)
+            codes, code_scales = store[u]
+            cols = slice(P * j, P * (j + tiles))
             nc.vector.quantize_mx(
                 out=codes[:, cols].bitcast(FP8X4),
                 scales=code_scales[:, cols],
-                in_=slots4[i][:, lo:hi].rearrange("p j r t -> p (j r t)"),
+                in_=src[u][:, cols, :].rearrange("p r t -> p (r t)"),
             )
 
-        def project(w, codes, code_scales):
-            bank = proj_psum.tile([P, PACK, P], F32, name="proj")
+        def quantize_slots(first, tiles=UNIT):
+            quantize(slots_q, ("slot_codes", "slot_scales"), slots4, first, tiles)
+
+        def quantize_queries(first, tiles=UNIT):
+            quantize(query_q, ("query_codes", "query_scales"), query4, first, tiles)
+
+        def project(w, codes, code_scales, pool=proj_psum, name="proj"):
+            bank = pool.tile([P, PACK, P], F32, name=name)
             for t in range(PACK):
                 nc.tensor.matmul_mx(
                     out=bank[:, t, :],
@@ -178,39 +184,25 @@ def tile_actionbindingattention_pb_w4_kernel(
                 )
             return bank
 
-        def queries(i, tiles=(0, 1)):
-            codes, code_scales = slots_q[i]
-            for j in tiles:
+        def queries(first, tiles):
+            for i in range(first, first + tiles):
+                g, j = place(i)
+                codes, code_scales = slots_q[g]
                 cols = slice(P * j, P * (j + 1))
-                proj[i, j] = project(Q, codes[:, cols], code_scales[:, cols])
+                proj[i] = project(Q, codes[:, cols], code_scales[:, cols])
 
-        def lay_query(i, j, copy):
-            if i not in query4:
-                query4[i] = work.tile([P, 2, P, PACK], BF16, name="query4", align_bytes=64)
-            copy(out=query4[i][:, j], in_=proj[i, j][:].rearrange("p t r -> p r t"))
+        def lay_queries(first, tiles, copy):
+            for i in range(first, first + tiles):
+                u, j = place(i)
+                copy(out=query4[u][:, j * P : (j + 1) * P, :], in_=proj[i][:].rearrange("p t r -> p r t"))
 
-        def quantize_queries(i, lo=0, hi=2):
-            if i // 2 not in query_q:
-                query_q[i // 2] = (
-                    work.tile([P, 4 * P], U32, name="query_codes", align_bytes=64),
-                    work.tile([P, 4 * P], U8, name="query_scales", align_bytes=64),
-                )
-            codes, code_scales = query_q[i // 2]
-            first = 2 * (i % 2)
-            cols = slice(P * (first + lo), P * (first + hi))
-            nc.vector.quantize_mx(
-                out=codes[:, cols].bitcast(FP8X4),
-                scales=code_scales[:, cols],
-                in_=query4[i][:, lo:hi].rearrange("p j r t -> p (j r t)"),
-            )
-
-        def multiply_keys(u, pool=logit_psum, name="logits"):
-            first, tiles = UNITS[u]
-            logits[u] = pool.tile([P, 2 * tiles, SLOTS], F32, name=name)
-            codes, code_scales = query_q[first // 4]
-            cols = slice(P * (first % 4), P * (first % 4 + tiles))
+        def multiply_keys(first, tiles=UNIT, pool=logit_psum, name="logits"):
+            logits[first] = pool.tile([P, 2 * tiles, SLOTS], F32, name=name)
+            g, j = place(first)
+            codes, code_scales = query_q[g]
+            cols = slice(P * j, P * (j + tiles))
             nc.tensor.matmul_mx(
-                out=logits[u][:].rearrange("p b s -> p (b s)"),
+                out=logits[first][:].rearrange("p b s -> p (b s)"),
                 lhsT=key_codes[:].bitcast(FP8X4),
                 lhsT_scale=key_scales[:],
                 rhs=codes[:, cols].bitcast(FP8X4),
@@ -219,163 +211,156 @@ def tile_actionbindingattention_pb_w4_kernel(
                 stop=True,
             )
 
-        def find_tops(u):
-            tops[u] = soft.tile([P, 2 * UNITS[u][1]], F32, name="tops")
-            nc.vector.tensor_reduce(out=tops[u][:], in_=logits[u][:], axis=AXIS_X, op=MAX)
+        def find_tops(first):
+            tops[first] = soft.tile([P, logits[first].shape[1]], F32, name="tops")
+            nc.vector.tensor_reduce(out=tops[first][:], in_=logits[first][:], axis=AXIS_X, op=MAX)
 
-        def negate_tops(u, on_scalar):
-            biases[u] = soft.tile([P, 2 * UNITS[u][1]], F32, name="biases")
-            if on_scalar:
-                nc.scalar.activation(out=biases[u][:], in_=tops[u][:], func=COPY, scale=-LOGIT_SCALE)
-            else:
-                nc.vector.tensor_scalar(
-                    out=biases[u][:], in0=tops[u][:], scalar1=-LOGIT_SCALE, scalar2=None, op0=MULT
-                )
+        def negate_tops(first):
+            biases[first] = soft.tile([P, logits[first].shape[1]], F32, name="biases")
+            nc.vector.tensor_scalar(
+                out=biases[first][:], in0=tops[first][:], scalar1=-LOGIT_SCALE, scalar2=None, op0=MULT
+            )
 
-        def exponentiate(u, samples):
-            if u not in exps:
-                exps[u] = soft.tile([P, 2 * UNITS[u][1], SLOTS], F32, name="exps")
-                sums[u] = soft.tile([P, 2 * UNITS[u][1]], F32, name="sums")
-            for b in samples:
+        def exponentiate(first):
+            samples = logits[first].shape[1]
+            exps[first] = soft.tile([P, samples, SLOTS], F32, name="exps")
+            sums[first] = soft.tile([P, samples], F32, name="sums")
+            for b in range(samples):
                 nc.scalar.activation(
-                    out=exps[u][:, b, :],
-                    in_=logits[u][:, b, :],
+                    out=exps[first][:, b, :],
+                    in_=logits[first][:, b, :],
                     func=EXP,
-                    bias=biases[u][:, b : b + 1],
+                    bias=biases[first][:, b : b + 1],
                     scale=LOGIT_SCALE,
-                    accum_out=sums[u][:, b : b + 1],
+                    accum_out=sums[first][:, b : b + 1],
                 )
 
-        def invert_sums(u):
-            inverses[u] = soft.tile([P, 2 * UNITS[u][1]], F32, name="inverses")
-            nc.vector.reciprocal(out=inverses[u][:], in_=sums[u][:])
+        def invert_sums(first):
+            inverses[first] = soft.tile([P, logits[first].shape[1]], F32, name="inverses")
+            nc.vector.reciprocal(out=inverses[first][:], in_=sums[first][:])
 
-        def divide_and_store(u, on_scalar=False):
-            first, tiles = UNITS[u]
-            samples = 2 * tiles
+        def divide_and_store(first, engine=None):
+            samples = logits[first].shape[1]
             shares = soft.tile([P, samples, SLOTS], F32, name="shares")
-            if on_scalar:
+            if engine is None:
                 for b in range(samples):
                     nc.scalar.activation(
-                        out=shares[:, b, :], in_=exps[u][:, b, :], func=COPY, scale=inverses[u][:, b : b + 1]
+                        out=shares[:, b, :], in_=exps[first][:, b, :], func=COPY, scale=inverses[first][:, b : b + 1]
                     )
             else:
-                nc.vector.tensor_tensor(
+                engine.tensor_tensor(
                     out=shares[:],
-                    in0=exps[u][:],
-                    in1=inverses[u][:].unsqueeze(2).to_broadcast([P, samples, SLOTS]),
+                    in0=exps[first][:],
+                    in1=inverses[first][:].unsqueeze(2).to_broadcast([P, samples, SLOTS]),
                     op=MULT,
                 )
             nc.sync.dma_start(
                 out=out[2 * first : 2 * first + samples].rearrange("b n s -> n b s"), in_=shares[:]
             )
 
-        scale_bank = logit_psum.tile([P, PACK, P], F32, name="logits")
-        for t in range(PACK):
-            nc.tensor.transpose(scale_bank[:, t, :], scale4[:, t : t + 1].to_broadcast([P, P]), eye[:])
-        for j in range(2):
-            nc.scalar.copy(
-                out=scale_rows[:, j, :].rearrange("p (n t) -> p n t", t=PACK),
-                in_=scale_bank[:].rearrange("p t n -> p n t"),
-            )
         ident4 = keep.tile([P, P, PACK], BF16, name="ident4", align_bytes=64)
-        ident_bank = logit_psum.tile([P, 2, P], F32, name="logits")
-        turn_rows(ident_bank, ident_rows[:])
-        lay_rows(ident4[:], ident_bank[:])
-
-        permute_words(Q)
-        scale_slots(0)
-        turn_and_lay_first_pair()
-        permute_scales(Q)
-        scale_slots(1, (0,))
-        quantize_slots(0, 0, 1)
-        queries(0, (0,))
-        scale_slots(1, (1,))
-        quantize_slots(0, 1, 2)
-        queries(0, (1,))
-        turn_slots(1)
-
-        permute_words(K)
-        permute_scales(K)
         ident_codes = keep.tile([P, P], U32, name="ident_codes", align_bytes=64)
         ident_scales = keep.tile([P, P], U8, name="ident_scales", align_bytes=64)
-        nc.vector.quantize_mx(
-            out=ident_codes[:].bitcast(FP8X4), scales=ident_scales[:], in_=ident4[:].rearrange("p r t -> p (r t)")
-        )
-        key_bank = project(K, ident_codes[:], ident_scales[:])
-        for j in range(2):
-            lay_query(0, j, nc.scalar.copy)
-        lay_slots(1)
-        scale_slots(2)
         key4 = keep.tile([P, P, PACK], BF16, name="key4", align_bytes=64)
-        nc.scalar.copy(out=key4[:], in_=key_bank[:].rearrange("p t r -> p r t"))
         key_codes = keep.tile([P, P], U32, name="key_codes", align_bytes=64)
         key_scales = keep.tile([P, P], U8, name="key_scales", align_bytes=64)
 
-        for i in range(1, LAST):
-            u = i // 2
-            even = i % 2 == 0
-            if even and u >= 3:
-                invert_sums(u - 3)
-            if i + 2 <= LAST:
-                scale_slots(i + 2)
-            turn_slots(i + 1)
-            if even and u >= 2:
-                negate_tops(u - 2, on_scalar=True)
-            if i > 1:
-                lay_query(i - 1, 0, nc.scalar.copy)
-                lay_query(i - 1, 1, nc.scalar.copy if i + 2 <= LAST else nc.vector.tensor_copy)
-            quantize_slots(i)
-            queries(i)
-            if not even and u >= 1:
-                find_tops(u - 1)
-            quantize_queries(i - 1)
-            if i == 1:
-                nc.vector.quantize_mx(
-                    out=key_codes[:].bitcast(FP8X4), scales=key_scales[:], in_=key4[:].rearrange("p r t -> p (r t)")
-                )
-            if even:
-                multiply_keys(u - 1)
-                if u >= 2:
-                    exponentiate(u - 2, range(0, 4))
-                if u >= 3:
-                    divide_and_store(u - 3)
-            elif u >= 2:
-                exponentiate(u - 2, range(4, 8))
-            lay_slots(i + 1)
+        def quantize_keep(codes, code_scales, src):
+            nc.vector.quantize_mx(
+                out=codes[:].bitcast(FP8X4), scales=code_scales[:], in_=src[:].rearrange("p r t -> p (r t)")
+            )
 
-        quantize_slots(15)
-        find_tops(6)
-        queries(15)
-        lay_query(14, 0, nc.scalar.copy)
-        lay_query(14, 1, nc.scalar.copy)
-        lay_query(15, 0, nc.scalar.copy)
-        quantize_queries(14)
-        negate_tops(6, on_scalar=False)
-        multiply_keys(7, turn_psum, "turned")
-        lay_query(15, 1, nc.vector.tensor_copy)
-        quantize_queries(15, 0, 1)
-        find_tops(7)
-        exponentiate(5, range(4, 8))
-        quantize_queries(15, 1, 2)
-        invert_sums(5)
-        multiply_keys(8, turn_psum, "turned")
-        multiply_keys(9)
-        find_tops(8)
-        negate_tops(7, on_scalar=False)
-        exponentiate(6, range(8))
-        find_tops(9)
-        negate_tops(8, on_scalar=False)
-        divide_and_store(5)
-        exponentiate(7, range(4))
-        invert_sums(6)
-        exponentiate(8, range(2))
-        negate_tops(9, on_scalar=False)
-        invert_sums(7)
-        invert_sums(8)
-        divide_and_store(7, on_scalar=True)
-        divide_and_store(6)
-        exponentiate(9, range(2))
-        invert_sums(9)
-        divide_and_store(8)
-        divide_and_store(9)
+        def lay_ident(bank):
+            nc.scalar.copy(
+                out=ident4[:].rearrange("p r t -> p (r t)").bitcast(F32).rearrange("p (r u) -> p r u", u=2),
+                in_=bank[:].rearrange("p u r -> p r u"),
+            )
+
+        widen(0, 1, nc.vector.tensor_copy)
+        turn(0, 1)
+        widen(1, 1, nc.vector.tensor_copy)
+        turn(1, 1)
+        widen(2, 2, widen_on_scalar)
+        turn(2, 2, logit_psum, "logits")
+        widen(4, 2, nc.scalar.copy)
+        turn(4, 2, logit_psum, "logits")
+        widen(6, 2, nc.scalar.copy)
+        permute_words(Q)
+        scale_slots(0, 1)
+        permute_scales(Q)
+        scale_slots(1, 1)
+        quantize_slots(0, 1)
+        queries(0, 1)
+        quantize_slots(1, 1)
+        queries(1, 1)
+        widen(8, 2, nc.gpsimd.tensor_copy, planes[3])
+        ident_bank = turn_psum.tile([P, 2, P], F32, name="turned")
+        turn_rows(ident_bank, ident_rows[:])
+        turn(6)
+        widen(10, 2, nc.scalar.copy)
+
+        scale_slots(2)
+        lay_ident(ident_bank)
+        lay_queries(0, 2, nc.scalar.copy)
+        scale_slots(4)
+        turn(8)
+        permute_words(K)
+        permute_scales(K)
+        quantize_keep(ident_codes, ident_scales, ident4)
+        key_bank = project(K, ident_codes[:], ident_scales[:], logit_psum, "logits")
+        quantize_slots(2)
+        queries(2, 4)
+        quantize_queries(0, 2)
+        widen(STARTS[4], UNIT, nc.gpsimd.tensor_copy, planes[0])
+        widen(12, 2, nc.scalar.copy)
+        nc.scalar.copy(out=key4[:], in_=key_bank[:].rearrange("p t r -> p r t"))
+
+        for g in range(2, GROUPS):
+            i = STARTS[g]
+            for j in range(i, i + size(g), 2):
+                scale_slots(j)
+            if g + 1 < GROUPS:
+                for j in range(STARTS[g + 1], STARTS[g + 1] + size(g + 1), 2):
+                    turn(j)
+            if g >= 3:
+                find_tops(STARTS[g - 2])
+            lay_queries(STARTS[g - 1], UNIT, nc.scalar.copy)
+            if g >= 4:
+                divide_and_store(STARTS[g - 4])
+            if g == 2:
+                quantize_keep(key_codes, key_scales, key4)
+                multiply_keys(0, 2)
+            quantize_slots(i, size(g))
+            if g == 2:
+                find_tops(0)
+            queries(i, 2)
+            if g >= 3:
+                negate_tops(STARTS[g - 2])
+                invert_sums(STARTS[g - 3])
+            quantize_queries(STARTS[g - 1])
+            if g == 2:
+                negate_tops(0)
+            if g + 3 < GROUPS:
+                widen(STARTS[g + 3], size(g + 3), nc.gpsimd.tensor_copy, planes[(g - 1) % 3])
+            exponentiate(STARTS[g - 2])
+            multiply_keys(STARTS[g - 1])
+            if size(g) == UNIT:
+                queries(i + 2, 2)
+
+        lay_queries(30, 1, nc.scalar.copy)
+        lay_queries(31, 1, nc.vector.tensor_copy)
+        divide_and_store(18, nc.vector)
+        find_tops(26)
+        quantize_queries(30, 2)
+        multiply_keys(30, 2)
+        negate_tops(26)
+        invert_sums(22)
+        exponentiate(26)
+        find_tops(30)
+        divide_and_store(22, nc.vector)
+        negate_tops(30)
+        exponentiate(30)
+        invert_sums(26)
+        divide_and_store(26, nc.vector)
+        invert_sums(30)
+        divide_and_store(30, nc.vector)

@@ -13,6 +13,7 @@ FP8X4 = mybir.dt.float8_e4m3fn_x4
 FP4X4 = mybir.dt.float4_e2m1fn_x4
 MULT = mybir.AluOpType.mult
 MAX = mybir.AluOpType.max
+MIN = mybir.AluOpType.min
 AXIS_X = mybir.AxisListType.X
 COPY = mybir.ActivationFunctionType.Copy
 EXP = mybir.ActivationFunctionType.Exp
@@ -25,16 +26,17 @@ LOGIT_SCALE = float(FEATURES) ** -0.5
 
 TILES = SAMPLES * SLOTS // P
 UNIT = 4
-STARTS = [0] + list(range(2, TILES, UNIT))
+STARTS = [0, 2, 6] + list(range(12, TILES, UNIT))
 GROUPS = len(STARTS)
 
 
 def place(tile):
-    return (0, tile) if tile < 2 else ((tile + 2) // UNIT, (tile + 2) % UNIT)
+    g = max(g for g in range(GROUPS) if STARTS[g] <= tile)
+    return g, tile - STARTS[g]
 
 
 def size(g):
-    return 2 if g in (0, GROUPS - 1) else UNIT
+    return (STARTS + [TILES])[g + 1] - STARTS[g]
 
 
 Q, K = 0, 1
@@ -47,7 +49,7 @@ def tile_actionbindingattention_pb_w4_kernel(
     with ExitStack() as ctx:
         keep = ctx.enter_context(tc.tile_pool(name="keep", bufs=1))
         work = ctx.enter_context(tc.tile_pool(name="work", bufs=3))
-        soft = ctx.enter_context(tc.tile_pool(name="soft", bufs=12))
+        soft = ctx.enter_context(tc.tile_pool(name="soft", bufs=14))
         turn_psum = ctx.enter_context(tc.psum_pool(name="turn_psum", bufs=2))
         proj_psum = ctx.enter_context(tc.psum_pool(name="proj_psum", bufs=4))
         logit_psum = ctx.enter_context(tc.psum_pool(name="logit_psum", bufs=2))
@@ -83,16 +85,16 @@ def tile_actionbindingattention_pb_w4_kernel(
         ident_rows = keep.tile([P, FEATURES], BF16, name="ident_rows", align_bytes=64)
         load_slots(0, 2)
         nc.scalar.dma_start(out=scale4[:], in_=slots_scale.rearrange("a b (p t) -> p (a b t)", t=PACK))
+        nc.scalar.dma_start(out=ident_rows[:], in_=ident)
         load_slots(2, 2)
         load_words(Q, Wq_words)
         load_slots(4, 4)
         load_scales(Q, Wq_scales)
-        load_slots(8, 2)
-        nc.sync.dma_start(out=ident_rows[:], in_=ident)
+        load_slots(8, 4)
         load_words(K, Wk_words)
-        load_slots(10, 4)
+        load_slots(12, 8)
         load_scales(K, Wk_scales)
-        for g in range(4, GROUPS):
+        for g in range(5, GROUPS):
             load_slots(STARTS[g], size(g))
 
         eye = keep.tile([P, P], F32, name="eye", align_bytes=64)
@@ -111,12 +113,12 @@ def tile_actionbindingattention_pb_w4_kernel(
             )
 
         wide, turned, slots4, slots_q, proj, query4, query_q = {}, {}, {}, {}, {}, {}, {}
-        logits, tops, biases, exps, sums, inverses = {}, {}, {}, {}, {}, {}
+        logits, tops, flipped, biases, exps, sums, inverses = {}, {}, {}, {}, {}, {}, {}
 
-        planes = [keep.tile([P, UNIT * FEATURES], BF16, name="plane_%d" % n, align_bytes=64) for n in range(6)]
+        planes = [keep.tile([P, 6 * FEATURES], BF16, name="plane_%d" % n, align_bytes=64) for n in range(7)]
         for g in range(GROUPS):
             query4[g] = planes[g % 3][:].rearrange("p (r t) -> p r t", t=PACK)
-            slots4[g] = planes[3 if g == 0 else 4 + g % 2][:].rearrange("p (r t) -> p r t", t=PACK)
+            slots4[g] = planes[(3, 6)[g] if g < 2 else 4 + g % 2][:].rearrange("p (r t) -> p r t", t=PACK)
 
         def widen(first, tiles, copy, t=None):
             if t is None:
@@ -153,8 +155,8 @@ def tile_actionbindingattention_pb_w4_kernel(
             u, j = place(first)
             if u not in store:
                 store[u] = (
-                    work.tile([P, UNIT * P], U32, name=names[0], align_bytes=64),
-                    work.tile([P, UNIT * P], U8, name=names[1], align_bytes=64),
+                    work.tile([P, size(u) * P], U32, name=names[0], align_bytes=64),
+                    work.tile([P, size(u) * P], U8, name=names[1], align_bytes=64),
                 )
             codes, code_scales = store[u]
             cols = slice(P * j, P * (j + tiles))
@@ -215,23 +217,42 @@ def tile_actionbindingattention_pb_w4_kernel(
             tops[first] = soft.tile([P, logits[first].shape[1]], F32, name="tops")
             nc.vector.tensor_reduce(out=tops[first][:], in_=logits[first][:], axis=AXIS_X, op=MAX)
 
-        def negate_tops(first):
+        def negate_tops(first, on_scalar=True):
             biases[first] = soft.tile([P, logits[first].shape[1]], F32, name="biases")
-            nc.vector.tensor_scalar(
-                out=biases[first][:], in0=tops[first][:], scalar1=-LOGIT_SCALE, scalar2=None, op0=MULT
-            )
+            if on_scalar:
+                nc.scalar.activation(out=biases[first][:], in_=tops[first][:], func=COPY, scale=-LOGIT_SCALE)
+            else:
+                nc.vector.tensor_scalar(
+                    out=biases[first][:], in0=tops[first][:], scalar1=-LOGIT_SCALE, scalar2=None, op0=MULT
+                )
+
+        def flip_logits(first):
+            samples = logits[first].shape[1]
+            flipped[first] = soft.tile([P, samples, SLOTS], F32, name="flipped", bufs=3)
+            biases[first] = soft.tile([P, samples], F32, name="biases")
+            for b in range(samples):
+                nc.vector.tensor_scalar(
+                    out=flipped[first][:, b, :],
+                    in0=logits[first][:, b, :],
+                    scalar1=-LOGIT_SCALE,
+                    scalar2=None,
+                    op0=MULT,
+                    op1=MIN,
+                    accum_out=biases[first][:, b : b + 1],
+                )
 
         def exponentiate(first):
             samples = logits[first].shape[1]
+            src, factor = (flipped[first], -1.0) if first in flipped else (logits[first], LOGIT_SCALE)
             exps[first] = soft.tile([P, samples, SLOTS], F32, name="exps")
             sums[first] = soft.tile([P, samples], F32, name="sums")
             for b in range(samples):
                 nc.scalar.activation(
                     out=exps[first][:, b, :],
-                    in_=logits[first][:, b, :],
+                    in_=src[:, b, :],
                     func=EXP,
                     bias=biases[first][:, b : b + 1],
-                    scale=LOGIT_SCALE,
+                    scale=factor,
                     accum_out=sums[first][:, b : b + 1],
                 )
 
@@ -239,11 +260,16 @@ def tile_actionbindingattention_pb_w4_kernel(
             inverses[first] = soft.tile([P, logits[first].shape[1]], F32, name="inverses")
             nc.vector.reciprocal(out=inverses[first][:], in_=sums[first][:])
 
-        def divide_and_store(first, engine=None):
+        def divide_and_store(first, engine=None, room=None, between=None):
             samples = logits[first].shape[1]
-            shares = soft.tile([P, samples, SLOTS], F32, name="shares")
+            if room is None:
+                shares = soft.tile([P, samples, SLOTS], F32, name="shares")
+            else:
+                shares = room[:].bitcast(F32)[:, : samples * SLOTS].rearrange("p (b s) -> p b s", s=SLOTS)
             if engine is None:
                 for b in range(samples):
+                    if between is not None and b == samples - 3:
+                        negate_tops(between)
                     nc.scalar.activation(
                         out=shares[:, b, :], in_=exps[first][:, b, :], func=COPY, scale=inverses[first][:, b : b + 1]
                     )
@@ -271,7 +297,7 @@ def tile_actionbindingattention_pb_w4_kernel(
             )
 
         def lay_ident(bank):
-            nc.scalar.copy(
+            nc.vector.tensor_copy(
                 out=ident4[:].rearrange("p r t -> p (r t)").bitcast(F32).rearrange("p (r u) -> p r u", u=2),
                 in_=bank[:].rearrange("p u r -> p r u"),
             )
@@ -280,6 +306,8 @@ def tile_actionbindingattention_pb_w4_kernel(
         turn(0, 1)
         widen(1, 1, nc.vector.tensor_copy)
         turn(1, 1)
+        ident_bank = proj_psum.tile([P, 2, P], F32, name="proj")
+        turn_rows(ident_bank, ident_rows[:])
         widen(2, 2, widen_on_scalar)
         turn(2, 2, logit_psum, "logits")
         widen(4, 2, nc.scalar.copy)
@@ -289,78 +317,196 @@ def tile_actionbindingattention_pb_w4_kernel(
         scale_slots(0, 1)
         permute_scales(Q)
         scale_slots(1, 1)
+        lay_ident(ident_bank)
         quantize_slots(0, 1)
         queries(0, 1)
+        quantize_keep(ident_codes, ident_scales, ident4)
         quantize_slots(1, 1)
-        queries(1, 1)
-        widen(8, 2, nc.gpsimd.tensor_copy, planes[3])
-        ident_bank = turn_psum.tile([P, 2, P], F32, name="turned")
-        turn_rows(ident_bank, ident_rows[:])
+        widen(8, 3, nc.gpsimd.tensor_copy, planes[3])
         turn(6)
-        widen(10, 2, nc.scalar.copy)
+        queries(1, 1)
+        widen(11, 1, nc.scalar.copy)
 
         scale_slots(2)
-        lay_ident(ident_bank)
-        lay_queries(0, 2, nc.scalar.copy)
+        lay_queries(0, 1, nc.scalar.copy)
+        widen(17, 1, nc.scalar.copy)
+        lay_queries(1, 1, nc.scalar.copy)
         scale_slots(4)
         turn(8)
+        turn(10, 2, logit_psum, "logits")
+        quantize_slots(2, 2)
+        queries(2, 2)
         permute_words(K)
         permute_scales(K)
-        quantize_keep(ident_codes, ident_scales, ident4)
         key_bank = project(K, ident_codes[:], ident_scales[:], logit_psum, "logits")
-        quantize_slots(2)
-        queries(2, 4)
-        quantize_queries(0, 2)
-        widen(STARTS[4], UNIT, nc.gpsimd.tensor_copy, planes[0])
-        widen(12, 2, nc.scalar.copy)
+        quantize_slots(4, 2)
+        widen(12, 5, nc.gpsimd.tensor_copy, planes[6])
+        queries(4, 2)
+        widen(18, 1, nc.scalar.copy)
+
+        scale_slots(6)
+        scale_slots(8)
+        scale_slots(10)
+        lay_queries(2, 2, nc.scalar.copy)
         nc.scalar.copy(out=key4[:], in_=key_bank[:].rearrange("p t r -> p r t"))
+        lay_queries(4, 2, nc.scalar.copy)
+        widen(19, 1, nc.scalar.copy)
+        turn(12)
+        turn(14)
+        quantize_slots(6, 2)
+        queries(6, 2)
+        quantize_slots(8, 4)
+        quantize_queries(0, 2)
+        quantize_keep(key_codes, key_scales, key4)
+        quantize_queries(2)
+        widen(20, UNIT, nc.gpsimd.tensor_copy, planes[1])
+        queries(8, 2)
+        multiply_keys(0, 2)
+        multiply_keys(2)
+        lay_queries(6, 2, nc.scalar.copy)
+        queries(10, 2)
 
-        for g in range(2, GROUPS):
-            i = STARTS[g]
-            for j in range(i, i + size(g), 2):
-                scale_slots(j)
-            if g + 1 < GROUPS:
-                for j in range(STARTS[g + 1], STARTS[g + 1] + size(g + 1), 2):
-                    turn(j)
-            if g >= 3:
-                find_tops(STARTS[g - 2])
-            lay_queries(STARTS[g - 1], UNIT, nc.scalar.copy)
-            if g >= 4:
-                divide_and_store(STARTS[g - 4])
-            if g == 2:
-                quantize_keep(key_codes, key_scales, key4)
-                multiply_keys(0, 2)
-            quantize_slots(i, size(g))
-            if g == 2:
-                find_tops(0)
-            queries(i, 2)
-            if g >= 3:
-                negate_tops(STARTS[g - 2])
-                invert_sums(STARTS[g - 3])
-            quantize_queries(STARTS[g - 1])
-            if g == 2:
-                negate_tops(0)
-            if g + 3 < GROUPS:
-                widen(STARTS[g + 3], size(g + 3), nc.gpsimd.tensor_copy, planes[(g - 1) % 3])
-            exponentiate(STARTS[g - 2])
-            multiply_keys(STARTS[g - 1])
-            if size(g) == UNIT:
-                queries(i + 2, 2)
+        scale_slots(12)
+        find_tops(0)
+        scale_slots(14)
+        turn(16)
+        turn(18)
+        find_tops(2)
+        lay_queries(8, 3, nc.scalar.copy)
+        negate_tops(0)
+        lay_queries(11, 1, nc.scalar.copy)
+        exponentiate(0)
+        negate_tops(2)
+        quantize_slots(12, 2)
+        queries(12, 2)
+        quantize_slots(14, 2)
+        quantize_queries(6, 2)
+        quantize_queries(8, 4)
+        widen(24, UNIT, nc.gpsimd.tensor_copy, planes[2])
+        multiply_keys(6, 2)
+        exponentiate(2)
+        queries(14, 2)
+        multiply_keys(8, 4)
 
-        lay_queries(30, 1, nc.scalar.copy)
-        lay_queries(31, 1, nc.vector.tensor_copy)
-        divide_and_store(18, nc.vector)
-        find_tops(26)
-        quantize_queries(30, 2)
-        multiply_keys(30, 2)
-        negate_tops(26)
+        scale_slots(16)
+        find_tops(6)
+        invert_sums(0)
+        scale_slots(18)
+        turn(20)
+        turn(22)
+        find_tops(8)
+        lay_queries(12, 3, nc.scalar.copy)
+        negate_tops(6)
+        lay_queries(15, 1, nc.scalar.copy)
+        exponentiate(6)
+        divide_and_store(0, between=8)
+        quantize_slots(16, 2)
+        queries(16, 2)
+        invert_sums(2)
+        quantize_slots(18, 2)
+        quantize_queries(12)
+        widen(28, UNIT, nc.gpsimd.tensor_copy, planes[0])
+        exponentiate(8)
+        queries(18, 1)
+        multiply_keys(12)
+        queries(19, 1)
+
+        scale_slots(20)
+        invert_sums(6)
+        scale_slots(22)
+        turn(24)
+        turn(26)
+        find_tops(12)
+        lay_queries(16, UNIT, nc.scalar.copy)
+        divide_and_store(2, between=12)
+        quantize_slots(20, 2)
+        queries(20, 2)
+        invert_sums(8)
+        quantize_slots(22, 2)
+        quantize_queries(16)
+        divide_and_store(8, nc.gpsimd, planes[1])
+        divide_and_store(6, nc.gpsimd)
+        exponentiate(12)
+        multiply_keys(16)
+        queries(22, 2)
+
+        scale_slots(24)
+        turn(28)
+        lay_queries(20, 2, nc.scalar.copy)
+        find_tops(16)
+        scale_slots(26)
+        lay_queries(22, 1, nc.scalar.copy)
+        negate_tops(16)
+        lay_queries(23, 1, nc.scalar.copy)
+        quantize_queries(20, 2)
+        multiply_keys(20, 2)
+        invert_sums(12)
+        quantize_slots(24, 2)
+        queries(24, 2)
+        exponentiate(16)
+        quantize_queries(22, 2)
+        multiply_keys(22, 2)
+        find_tops(20)
+        invert_sums(16)
+        quantize_slots(26, 2)
+        divide_and_store(16, nc.gpsimd, planes[4][:, 2 * FEATURES :])
+        divide_and_store(12, between=20)
+        turn(30, 1)
+        queries(26, 2)
+
+        scale_slots(28)
+        turn(31, 1)
+        exponentiate(20)
+        lay_queries(24, 1, nc.scalar.copy)
+        find_tops(22)
+        scale_slots(30, 1)
+        lay_queries(25, 2, nc.scalar.copy)
+        negate_tops(22)
+        lay_queries(27, 1, nc.scalar.copy)
+        exponentiate(22)
+        quantize_slots(28, 2)
+        queries(28, 2)
+        scale_slots(31, 1)
+        quantize_slots(30, 1)
+        quantize_queries(24, 2)
+        quantize_slots(31, 1)
+        multiply_keys(24, 2)
+        queries(30, 2)
+        invert_sums(20)
+        quantize_queries(26, 2)
+        multiply_keys(26, 2)
+        divide_and_store(20, nc.vector)
         invert_sums(22)
-        exponentiate(26)
-        find_tops(30)
+        lay_queries(28, 1, nc.scalar.copy)
+        find_tops(24)
+        lay_queries(29, 1, nc.scalar.copy)
+        lay_queries(30, 1, nc.vector.tensor_copy)
+        negate_tops(24)
+        lay_queries(31, 1, nc.scalar.copy)
+        quantize_queries(28, 2)
+        multiply_keys(28, 2, turn_psum, "turned")
+        find_tops(26)
+        exponentiate(24)
+        quantize_queries(30, 1)
+        multiply_keys(30, 1, turn_psum, "turned")
+        negate_tops(26, False)
+        quantize_queries(31, 1)
+        multiply_keys(31, 1, proj_psum, "proj")
         divide_and_store(22, nc.vector)
-        negate_tops(30)
+        exponentiate(26)
+        flip_logits(28)
+        invert_sums(24)
+        flip_logits(30)
+        flip_logits(31)
+        exponentiate(28)
         exponentiate(30)
+        exponentiate(31)
         invert_sums(26)
-        divide_and_store(26, nc.vector)
+        invert_sums(28)
+        divide_and_store(24, nc.vector)
         invert_sums(30)
-        divide_and_store(30, nc.vector)
+        divide_and_store(26)
+        invert_sums(31)
+        divide_and_store(28, nc.vector)
+        divide_and_store(30)
+        divide_and_store(31, nc.vector)

@@ -49,7 +49,7 @@ def tile_actionbindingattention_pb_w4_kernel(
     with ExitStack() as ctx:
         keep = ctx.enter_context(tc.tile_pool(name="keep", bufs=1))
         work = ctx.enter_context(tc.tile_pool(name="work", bufs=3))
-        soft = ctx.enter_context(tc.tile_pool(name="soft", bufs=14))
+        soft = ctx.enter_context(tc.tile_pool(name="soft", bufs=15))
         turn_psum = ctx.enter_context(tc.psum_pool(name="turn_psum", bufs=2))
         proj_psum = ctx.enter_context(tc.psum_pool(name="proj_psum", bufs=4))
         logit_psum = ctx.enter_context(tc.psum_pool(name="logit_psum", bufs=2))
@@ -83,14 +83,15 @@ def tile_actionbindingattention_pb_w4_kernel(
 
         scale4 = keep.tile([P, PACK], F32, name="scale4")
         ident_rows = keep.tile([P, FEATURES], BF16, name="ident_rows", align_bytes=64)
-        load_slots(0, 2)
+        load_slots(0, 1)
         nc.scalar.dma_start(out=scale4[:], in_=slots_scale.rearrange("a b (p t) -> p (a b t)", t=PACK))
-        nc.scalar.dma_start(out=ident_rows[:], in_=ident)
+        load_slots(1, 1)
         load_slots(2, 2)
         load_words(Q, Wq_words)
         load_slots(4, 4)
         load_scales(Q, Wq_scales)
         load_slots(8, 4)
+        nc.sync.dma_start(out=ident_rows[:], in_=ident)
         load_words(K, Wk_words)
         load_slots(12, 8)
         load_scales(K, Wk_scales)
@@ -260,8 +261,8 @@ def tile_actionbindingattention_pb_w4_kernel(
             inverses[first] = soft.tile([P, logits[first].shape[1]], F32, name="inverses")
             nc.vector.reciprocal(out=inverses[first][:], in_=sums[first][:])
 
-        def divide_and_store(first, engine=None, room=None, between=None):
-            samples = logits[first].shape[1]
+        def divide_and_store(first, engine=None, room=None, between=None, part=None, queue=nc.sync):
+            lo, samples = part or (0, logits[first].shape[1])
             if room is None:
                 shares = soft.tile([P, samples, SLOTS], F32, name="shares")
             else:
@@ -271,17 +272,20 @@ def tile_actionbindingattention_pb_w4_kernel(
                     if between is not None and b == samples - 3:
                         negate_tops(between)
                     nc.scalar.activation(
-                        out=shares[:, b, :], in_=exps[first][:, b, :], func=COPY, scale=inverses[first][:, b : b + 1]
+                        out=shares[:, b, :],
+                        in_=exps[first][:, lo + b, :],
+                        func=COPY,
+                        scale=inverses[first][:, lo + b : lo + b + 1],
                     )
             else:
                 engine.tensor_tensor(
                     out=shares[:],
-                    in0=exps[first][:],
-                    in1=inverses[first][:].unsqueeze(2).to_broadcast([P, samples, SLOTS]),
+                    in0=exps[first][:, lo : lo + samples, :],
+                    in1=inverses[first][:, lo : lo + samples].unsqueeze(2).to_broadcast([P, samples, SLOTS]),
                     op=MULT,
                 )
-            nc.sync.dma_start(
-                out=out[2 * first : 2 * first + samples].rearrange("b n s -> n b s"), in_=shares[:]
+            queue.dma_start(
+                out=out[2 * first + lo : 2 * first + lo + samples].rearrange("b n s -> n b s"), in_=shares[:]
             )
 
         ident4 = keep.tile([P, P, PACK], BF16, name="ident4", align_bytes=64)
@@ -297,7 +301,7 @@ def tile_actionbindingattention_pb_w4_kernel(
             )
 
         def lay_ident(bank):
-            nc.vector.tensor_copy(
+            nc.scalar.copy(
                 out=ident4[:].rearrange("p r t -> p (r t)").bitcast(F32).rearrange("p (r u) -> p r u", u=2),
                 in_=bank[:].rearrange("p u r -> p r u"),
             )
@@ -306,8 +310,6 @@ def tile_actionbindingattention_pb_w4_kernel(
         turn(0, 1)
         widen(1, 1, nc.vector.tensor_copy)
         turn(1, 1)
-        ident_bank = proj_psum.tile([P, 2, P], F32, name="proj")
-        turn_rows(ident_bank, ident_rows[:])
         widen(2, 2, widen_on_scalar)
         turn(2, 2, logit_psum, "logits")
         widen(4, 2, nc.scalar.copy)
@@ -317,15 +319,16 @@ def tile_actionbindingattention_pb_w4_kernel(
         scale_slots(0, 1)
         permute_scales(Q)
         scale_slots(1, 1)
-        lay_ident(ident_bank)
+        ident_bank = turn_psum.tile([P, 2, P], F32, name="turned")
+        turn_rows(ident_bank, ident_rows[:])
         quantize_slots(0, 1)
         queries(0, 1)
-        quantize_keep(ident_codes, ident_scales, ident4)
         quantize_slots(1, 1)
         widen(8, 3, nc.gpsimd.tensor_copy, planes[3])
         turn(6)
         queries(1, 1)
         widen(11, 1, nc.scalar.copy)
+        lay_ident(ident_bank)
 
         scale_slots(2)
         lay_queries(0, 1, nc.scalar.copy)
@@ -338,6 +341,7 @@ def tile_actionbindingattention_pb_w4_kernel(
         queries(2, 2)
         permute_words(K)
         permute_scales(K)
+        quantize_keep(ident_codes, ident_scales, ident4)
         key_bank = project(K, ident_codes[:], ident_scales[:], logit_psum, "logits")
         quantize_slots(4, 2)
         widen(12, 5, nc.gpsimd.tensor_copy, planes[6])
@@ -352,16 +356,16 @@ def tile_actionbindingattention_pb_w4_kernel(
         lay_queries(4, 2, nc.scalar.copy)
         widen(19, 1, nc.scalar.copy)
         turn(12)
-        turn(14)
         quantize_slots(6, 2)
         queries(6, 2)
         quantize_slots(8, 4)
         quantize_queries(0, 2)
         quantize_keep(key_codes, key_scales, key4)
+        multiply_keys(0, 2)
+        turn(14)
         quantize_queries(2)
         widen(20, UNIT, nc.gpsimd.tensor_copy, planes[1])
         queries(8, 2)
-        multiply_keys(0, 2)
         multiply_keys(2)
         lay_queries(6, 2, nc.scalar.copy)
         queries(10, 2)
@@ -487,26 +491,23 @@ def tile_actionbindingattention_pb_w4_kernel(
         multiply_keys(28, 2, turn_psum, "turned")
         find_tops(26)
         exponentiate(24)
-        quantize_queries(30, 1)
-        multiply_keys(30, 1, turn_psum, "turned")
-        negate_tops(26, False)
-        quantize_queries(31, 1)
-        multiply_keys(31, 1, proj_psum, "proj")
         divide_and_store(22, nc.vector)
+        negate_tops(26)
+        quantize_queries(30, 2)
+        multiply_keys(30, 2, turn_psum, "turned")
         exponentiate(26)
-        flip_logits(28)
         invert_sums(24)
-        flip_logits(30)
-        flip_logits(31)
-        exponentiate(28)
-        exponentiate(30)
-        exponentiate(31)
-        invert_sums(26)
-        invert_sums(28)
+        find_tops(28)
         divide_and_store(24, nc.vector)
-        invert_sums(30)
-        divide_and_store(26)
-        invert_sums(31)
+        negate_tops(28)
+        find_tops(30)
+        invert_sums(26)
+        exponentiate(28)
+        negate_tops(30, False)
+        divide_and_store(26, nc.vector)
+        exponentiate(30)
+        invert_sums(28)
         divide_and_store(28, nc.vector)
-        divide_and_store(30)
-        divide_and_store(31, nc.vector)
+        invert_sums(30)
+        divide_and_store(30, nc.vector, part=(0, 2))
+        divide_and_store(30, part=(2, 2), queue=nc.scalar)

@@ -67,8 +67,8 @@ def tile_actionbindingattention_pb_w4_kernel(
 
         words_in = keep.tile([P, 2, 2 * FEATURES], U8, name="words_in", align_bytes=64)
         scales_in = keep.tile([P, 2, FEATURES], U8, name="scales_in", align_bytes=64)
-        words = keep.tile([P, 2, 2 * FEATURES], U8, name="words", align_bytes=64)
-        scales = keep.tile([P, 2, FEATURES], U8, name="scales", align_bytes=64)
+        words = keep.tile([P, 2 * FEATURES], U8, name="words", align_bytes=64)
+        scales = keep.tile([P, FEATURES], U8, name="scales", align_bytes=64)
         nc.vector.memset(scales_in[:].rearrange("p w n -> p (w n)").bitcast(I32), 0)
 
         def load_words(w, w_words):
@@ -101,16 +101,16 @@ def tile_actionbindingattention_pb_w4_kernel(
         eye = keep.tile([P, P], F32, name="eye", align_bytes=64)
         make_identity(nc, eye[:])
 
-        def permute_words(w):
+        def permute_words():
             nc.vector.tensor_copy(
-                out=words[:, w, :].bitcast(I32).rearrange("p (t g e) -> p t g e", t=PACK, e=2),
-                in_=words_in[:, w, :].bitcast(I32).rearrange("p (g t e) -> p t g e", t=PACK, e=2),
+                out=words[:].bitcast(I32).rearrange("p (t g e) -> p t g e", t=PACK, e=2),
+                in_=words_in[:, Q, :].bitcast(I32).rearrange("p (g t e) -> p t g e", t=PACK, e=2),
             )
 
-        def permute_scales(w):
+        def permute_scales():
             nc.vector.tensor_copy(
-                out=scales[:, w, :].bitcast(I32).rearrange("p (t g) -> p t g", t=PACK),
-                in_=scales_in[:, w, :].bitcast(I32).rearrange("p (g t) -> p t g", t=PACK),
+                out=scales[:].bitcast(I32).rearrange("p (t g) -> p t g", t=PACK),
+                in_=scales_in[:, Q, :].bitcast(I32).rearrange("p (g t) -> p t g", t=PACK),
             )
 
         wide, turned, slots4, slots_q, proj, query4, query_q = {}, {}, {}, {}, {}, {}, {}
@@ -173,13 +173,13 @@ def tile_actionbindingattention_pb_w4_kernel(
         def quantize_queries(first, tiles=UNIT):
             quantize(query_q, ("query_codes", "query_scales"), query4, first, tiles)
 
-        def project(w, codes, code_scales, pool=proj_psum, name="proj"):
-            bank = pool.tile([P, PACK, P], F32, name=name)
+        def project(codes, code_scales):
+            bank = proj_psum.tile([P, PACK, P], F32, name="proj")
             for t in range(PACK):
                 nc.tensor.matmul_mx(
                     out=bank[:, t, :],
-                    lhsT=words[:, w, 2 * P * t : 2 * P * (t + 1)].bitcast(FP4X4),
-                    lhsT_scale=scales[:, w, P * t : P * (t + 1)],
+                    lhsT=words[:, 2 * P * t : 2 * P * (t + 1)].bitcast(FP4X4),
+                    lhsT_scale=scales[:, P * t : P * (t + 1)],
                     rhs=codes.bitcast(FP8X4),
                     rhs_scale=code_scales,
                     start=True,
@@ -192,7 +192,7 @@ def tile_actionbindingattention_pb_w4_kernel(
                 g, j = place(i)
                 codes, code_scales = slots_q[g]
                 cols = slice(P * j, P * (j + 1))
-                proj[i] = project(Q, codes[:, cols], code_scales[:, cols])
+                proj[i] = project(codes[:, cols], code_scales[:, cols])
 
         def lay_queries(first, tiles, copy):
             for i in range(first, first + tiles):
@@ -242,12 +242,14 @@ def tile_actionbindingattention_pb_w4_kernel(
                     accum_out=biases[first][:, b : b + 1],
                 )
 
-        def exponentiate(first):
+        def exponentiate(first, between=None):
             samples = logits[first].shape[1]
             src, factor = (flipped[first], -1.0) if first in flipped else (logits[first], LOGIT_SCALE)
             exps[first] = soft.tile([P, samples, SLOTS], F32, name="exps")
             sums[first] = soft.tile([P, samples], F32, name="sums")
             for b in range(samples):
+                if between is not None and b == samples - 2:
+                    negate_tops(between)
                 nc.scalar.activation(
                     out=exps[first][:, b, :],
                     in_=src[:, b, :],
@@ -291,6 +293,7 @@ def tile_actionbindingattention_pb_w4_kernel(
         ident4 = keep.tile([P, P, PACK], BF16, name="ident4", align_bytes=64)
         ident_codes = keep.tile([P, P], U32, name="ident_codes", align_bytes=64)
         ident_scales = keep.tile([P, P], U8, name="ident_scales", align_bytes=64)
+        key_rows = keep.tile([P, FEATURES], BF16, name="key_rows", align_bytes=64)
         key4 = keep.tile([P, P, PACK], BF16, name="key4", align_bytes=64)
         key_codes = keep.tile([P, P], U32, name="key_codes", align_bytes=64)
         key_scales = keep.tile([P, P], U8, name="key_scales", align_bytes=64)
@@ -300,9 +303,25 @@ def tile_actionbindingattention_pb_w4_kernel(
                 out=codes[:].bitcast(FP8X4), scales=code_scales[:], in_=src[:].rearrange("p r t -> p (r t)")
             )
 
-        def lay_ident(bank):
+        def project_keys():
+            bank = logit_psum.tile([P, FEATURES], F32, name="logits")
+            nc.tensor.matmul_mx(
+                out=bank[:],
+                lhsT=ident_codes[:].bitcast(FP8X4),
+                lhsT_scale=ident_scales[:],
+                rhs=words_in[:, K, :].bitcast(FP4X4),
+                rhs_scale=scales_in[:, K, :],
+                start=True,
+                stop=True,
+            )
             nc.scalar.copy(
-                out=ident4[:].rearrange("p r t -> p (r t)").bitcast(F32).rearrange("p (r u) -> p r u", u=2),
+                out=key_rows[:].rearrange("p (g i t) -> p g i t", i=PACK, t=PACK),
+                in_=bank[:].rearrange("p (g t i) -> p g i t", i=PACK, t=PACK),
+            )
+
+        def lay_words(dst, bank):
+            nc.scalar.copy(
+                out=dst[:].rearrange("p r t -> p (r t)").bitcast(F32).rearrange("p (r u) -> p r u", u=2),
                 in_=bank[:].rearrange("p u r -> p r u"),
             )
 
@@ -315,36 +334,36 @@ def tile_actionbindingattention_pb_w4_kernel(
         widen(4, 2, nc.scalar.copy)
         turn(4, 2, logit_psum, "logits")
         widen(6, 2, nc.scalar.copy)
-        permute_words(Q)
+        permute_words()
         scale_slots(0, 1)
-        permute_scales(Q)
         scale_slots(1, 1)
         ident_bank = turn_psum.tile([P, 2, P], F32, name="turned")
         turn_rows(ident_bank, ident_rows[:])
         quantize_slots(0, 1)
+        permute_scales()
         queries(0, 1)
         quantize_slots(1, 1)
         widen(8, 3, nc.gpsimd.tensor_copy, planes[3])
         turn(6)
         queries(1, 1)
         widen(11, 1, nc.scalar.copy)
-        lay_ident(ident_bank)
+        lay_words(ident4, ident_bank)
 
         scale_slots(2)
         lay_queries(0, 1, nc.scalar.copy)
         widen(17, 1, nc.scalar.copy)
         lay_queries(1, 1, nc.scalar.copy)
         scale_slots(4)
+        quantize_keep(ident_codes, ident_scales, ident4)
+        project_keys()
         turn(8)
         turn(10, 2, logit_psum, "logits")
         quantize_slots(2, 2)
         queries(2, 2)
-        permute_words(K)
-        permute_scales(K)
-        quantize_keep(ident_codes, ident_scales, ident4)
-        key_bank = project(K, ident_codes[:], ident_scales[:], logit_psum, "logits")
         quantize_slots(4, 2)
         widen(12, 5, nc.gpsimd.tensor_copy, planes[6])
+        key_bank = logit_psum.tile([P, 2, P], F32, name="logits")
+        turn_rows(key_bank, key_rows[:])
         queries(4, 2)
         widen(18, 1, nc.scalar.copy)
 
@@ -352,7 +371,7 @@ def tile_actionbindingattention_pb_w4_kernel(
         scale_slots(8)
         scale_slots(10)
         lay_queries(2, 2, nc.scalar.copy)
-        nc.scalar.copy(out=key4[:], in_=key_bank[:].rearrange("p t r -> p r t"))
+        lay_words(key4, key_bank)
         lay_queries(4, 2, nc.scalar.copy)
         widen(19, 1, nc.scalar.copy)
         turn(12)
@@ -379,8 +398,7 @@ def tile_actionbindingattention_pb_w4_kernel(
         lay_queries(8, 3, nc.scalar.copy)
         negate_tops(0)
         lay_queries(11, 1, nc.scalar.copy)
-        exponentiate(0)
-        negate_tops(2)
+        exponentiate(0, between=2)
         quantize_slots(12, 2)
         queries(12, 2)
         quantize_slots(14, 2)
@@ -450,10 +468,10 @@ def tile_actionbindingattention_pb_w4_kernel(
         exponentiate(16)
         quantize_queries(22, 2)
         multiply_keys(22, 2)
+        quantize_slots(26, 2)
         find_tops(20)
         invert_sums(16)
-        quantize_slots(26, 2)
-        divide_and_store(16, nc.gpsimd, planes[4][:, 2 * FEATURES :])
+        divide_and_store(16, nc.gpsimd)
         divide_and_store(12, between=20)
         turn(30, 1)
         queries(26, 2)
@@ -476,10 +494,10 @@ def tile_actionbindingattention_pb_w4_kernel(
         quantize_slots(31, 1)
         multiply_keys(24, 2)
         queries(30, 2)
-        invert_sums(20)
         quantize_queries(26, 2)
         multiply_keys(26, 2)
-        divide_and_store(20, nc.vector)
+        invert_sums(20)
+        divide_and_store(20, nc.gpsimd)
         invert_sums(22)
         lay_queries(28, 1, nc.scalar.copy)
         find_tops(24)
@@ -491,23 +509,26 @@ def tile_actionbindingattention_pb_w4_kernel(
         multiply_keys(28, 2, turn_psum, "turned")
         find_tops(26)
         exponentiate(24)
+        quantize_queries(30, 1)
+        multiply_keys(30, 1, turn_psum, "turned")
+        quantize_queries(31, 1)
+        multiply_keys(31, 1, proj_psum, "proj")
+        negate_tops(26, False)
         divide_and_store(22, nc.vector)
-        negate_tops(26)
-        quantize_queries(30, 2)
-        multiply_keys(30, 2, turn_psum, "turned")
         exponentiate(26)
         invert_sums(24)
-        find_tops(28)
-        divide_and_store(24, nc.vector)
-        negate_tops(28)
-        find_tops(30)
-        invert_sums(26)
+        divide_and_store(24, nc.gpsimd)
+        flip_logits(28)
         exponentiate(28)
-        negate_tops(30, False)
-        divide_and_store(26, nc.vector)
+        flip_logits(30)
+        invert_sums(26)
+        flip_logits(31)
         exponentiate(30)
+        exponentiate(31)
         invert_sums(28)
-        divide_and_store(28, nc.vector)
+        divide_and_store(26, nc.vector)
         invert_sums(30)
-        divide_and_store(30, nc.vector, part=(0, 2))
-        divide_and_store(30, part=(2, 2), queue=nc.scalar)
+        divide_and_store(28, nc.vector)
+        invert_sums(31)
+        divide_and_store(30, queue=nc.scalar)
+        divide_and_store(31, nc.vector)

@@ -89,9 +89,9 @@ def tile_actionbindingattention_pb_w4_kernel(
         load_slots(2, 2)
         load_words(Q, Wq_words)
         load_slots(4, 4)
+        nc.sync.dma_start(out=ident_rows[:], in_=ident)
         load_scales(Q, Wq_scales)
         load_slots(8, 4)
-        nc.sync.dma_start(out=ident_rows[:], in_=ident)
         load_words(K, Wk_words)
         load_slots(12, 8)
         load_scales(K, Wk_scales)
@@ -294,7 +294,7 @@ def tile_actionbindingattention_pb_w4_kernel(
         ident_codes = keep.tile([P, P], U32, name="ident_codes", align_bytes=64)
         ident_scales = keep.tile([P, P], U8, name="ident_scales", align_bytes=64)
         key_rows = keep.tile([P, FEATURES], BF16, name="key_rows", align_bytes=64)
-        key4 = keep.tile([P, P, PACK], BF16, name="key4", align_bytes=64)
+        key4 = planes[1][:, UNIT * FEATURES : (UNIT + 1) * FEATURES].rearrange("p (r t) -> p r t", t=PACK)
         key_codes = keep.tile([P, P], U32, name="key_codes", align_bytes=64)
         key_scales = keep.tile([P, P], U8, name="key_scales", align_bytes=64)
 
@@ -329,23 +329,23 @@ def tile_actionbindingattention_pb_w4_kernel(
         turn(0, 1)
         widen(1, 1, nc.vector.tensor_copy)
         turn(1, 1)
-        widen(2, 2, widen_on_scalar)
+        widen(2, 1, nc.vector.tensor_copy)
+        widen(3, 1, widen_on_scalar)
         turn(2, 2, logit_psum, "logits")
         widen(4, 2, nc.scalar.copy)
+        ident_bank = proj_psum.tile([P, 2, P], F32, name="proj")
+        turn_rows(ident_bank, ident_rows[:])
         turn(4, 2, logit_psum, "logits")
         widen(6, 2, nc.scalar.copy)
         permute_words()
         scale_slots(0, 1)
         scale_slots(1, 1)
-        ident_bank = turn_psum.tile([P, 2, P], F32, name="turned")
-        turn_rows(ident_bank, ident_rows[:])
         quantize_slots(0, 1)
         permute_scales()
-        queries(0, 1)
         quantize_slots(1, 1)
         widen(8, 3, nc.gpsimd.tensor_copy, planes[3])
+        queries(0, 2)
         turn(6)
-        queries(1, 1)
         widen(11, 1, nc.scalar.copy)
         lay_words(ident4, ident_bank)
 
@@ -362,28 +362,28 @@ def tile_actionbindingattention_pb_w4_kernel(
         queries(2, 2)
         quantize_slots(4, 2)
         widen(12, 5, nc.gpsimd.tensor_copy, planes[6])
+        queries(4, 2)
         key_bank = logit_psum.tile([P, 2, P], F32, name="logits")
         turn_rows(key_bank, key_rows[:])
-        queries(4, 2)
         widen(18, 1, nc.scalar.copy)
 
         scale_slots(6)
         scale_slots(8)
         scale_slots(10)
         lay_queries(2, 2, nc.scalar.copy)
-        lay_words(key4, key_bank)
         lay_queries(4, 2, nc.scalar.copy)
+        lay_words(key4, key_bank)
         widen(19, 1, nc.scalar.copy)
         turn(12)
         quantize_slots(6, 2)
         queries(6, 2)
         quantize_slots(8, 4)
         quantize_queries(0, 2)
-        quantize_keep(key_codes, key_scales, key4)
-        multiply_keys(0, 2)
         turn(14)
         quantize_queries(2)
-        widen(20, UNIT, nc.gpsimd.tensor_copy, planes[1])
+        quantize_keep(key_codes, key_scales, key4)
+        multiply_keys(0, 2)
+        widen(20, UNIT, nc.gpsimd.tensor_copy, planes[1][:, FEATURES:])
         queries(8, 2)
         multiply_keys(2)
         lay_queries(6, 2, nc.scalar.copy)
@@ -462,6 +462,7 @@ def tile_actionbindingattention_pb_w4_kernel(
         lay_queries(23, 1, nc.scalar.copy)
         quantize_queries(20, 2)
         multiply_keys(20, 2)
+        turn(30, 1)
         invert_sums(12)
         quantize_slots(24, 2)
         queries(24, 2)
@@ -473,15 +474,15 @@ def tile_actionbindingattention_pb_w4_kernel(
         invert_sums(16)
         divide_and_store(16, nc.gpsimd)
         divide_and_store(12, between=20)
-        turn(30, 1)
-        queries(26, 2)
+        queries(26, 1)
+        turn(31, 1, proj_psum, "proj")
+        queries(27, 1)
 
         scale_slots(28)
-        turn(31, 1)
         exponentiate(20)
         lay_queries(24, 1, nc.scalar.copy)
-        find_tops(22)
         scale_slots(30, 1)
+        find_tops(22)
         lay_queries(25, 2, nc.scalar.copy)
         negate_tops(22)
         lay_queries(27, 1, nc.scalar.copy)

@@ -25,21 +25,22 @@ FLOPS = 2 * SAMPLES * SLOTS * FEATURES**2 + 2 * OBJECTS * FEATURES**2 + 2 * SAMP
 LOGIT_SCALE = float(FEATURES) ** -0.5
 
 TILES = SAMPLES * SLOTS // P
-UNIT = 4
-STARTS = [0, 2, 6] + list(range(12, TILES, UNIT))
+FULL = 4
+STARTS = [0, 2, 6] + list(range(12, TILES, FULL))
 GROUPS = len(STARTS)
+WIDEST = 6
+SOFT_BUFFERS = 15
+FLIPPED = 3
+Q, K = 0, 1
 
 
 def place(tile):
-    g = max(g for g in range(GROUPS) if STARTS[g] <= tile)
+    g = sum(start <= tile for start in STARTS) - 1
     return g, tile - STARTS[g]
 
 
-def size(g):
+def group_size(g):
     return (STARTS + [TILES])[g + 1] - STARTS[g]
-
-
-Q, K = 0, 1
 
 
 def tile_actionbindingattention_pb_w4_kernel(
@@ -49,7 +50,7 @@ def tile_actionbindingattention_pb_w4_kernel(
     with ExitStack() as ctx:
         keep = ctx.enter_context(tc.tile_pool(name="keep", bufs=1))
         work = ctx.enter_context(tc.tile_pool(name="work", bufs=3))
-        soft = ctx.enter_context(tc.tile_pool(name="soft", bufs=15))
+        soft = ctx.enter_context(tc.tile_pool(name="soft", bufs=SOFT_BUFFERS))
         turn_psum = ctx.enter_context(tc.psum_pool(name="turn_psum", bufs=2))
         proj_psum = ctx.enter_context(tc.psum_pool(name="proj_psum", bufs=4))
         logit_psum = ctx.enter_context(tc.psum_pool(name="logit_psum", bufs=2))
@@ -59,26 +60,26 @@ def tile_actionbindingattention_pb_w4_kernel(
         rows = slots_bytes.rearrange("b s k -> (b s) k")
 
         def load_slots(first, tiles):
-            t = keep.tile([P, tiles, FEATURES], U8, name="slots_%d" % first, align_bytes=64)
+            held = keep.tile([P, tiles, FEATURES], U8, name="slots_%d" % first, align_bytes=64)
             src = rows[first * P : (first + tiles) * P, :]
-            nc.sync.dma_start(out=t[:], in_=src.rearrange("(j p) k -> p j k", p=P))
+            nc.sync.dma_start(out=held[:], in_=src.rearrange("(j p) k -> p j k", p=P))
             for j in range(tiles):
-                raw_bytes[first + j] = (t, j)
+                raw_bytes[first + j] = (held, j)
 
         words_in = keep.tile([P, 2, 2 * FEATURES], U8, name="words_in", align_bytes=64)
         scales_in = keep.tile([P, 2, FEATURES], U8, name="scales_in", align_bytes=64)
-        words = keep.tile([P, 2 * FEATURES], U8, name="words", align_bytes=64)
-        scales = keep.tile([P, FEATURES], U8, name="scales", align_bytes=64)
+        wq_words = keep.tile([P, 2 * FEATURES], U8, name="wq_words", align_bytes=64)
+        wq_scales = keep.tile([P, FEATURES], U8, name="wq_scales", align_bytes=64)
         nc.vector.memset(scales_in[:].rearrange("p w n -> p (w n)").bitcast(I32), 0)
 
         def load_words(w, w_words):
             nc.sync.dma_start(out=words_in[:, w, :].bitcast(I32), in_=w_words[0].bitcast(I32))
 
         def load_scales(w, w_scales):
-            for b in range(4):
+            for a in range(4):
                 nc.sync.dma_start(
-                    out=scales_in[32 * b : 32 * b + 4, w, :].bitcast(I32),
-                    in_=w_scales[0, 4 * b : 4 * b + 4, :].bitcast(I32),
+                    out=scales_in[32 * a : 32 * a + 4, w, :].bitcast(I32),
+                    in_=w_scales[0, 4 * a : 4 * a + 4, :].bitcast(I32),
                 )
 
         scale4 = keep.tile([P, PACK], F32, name="scale4")
@@ -95,47 +96,52 @@ def tile_actionbindingattention_pb_w4_kernel(
         load_words(K, Wk_words)
         load_slots(12, 8)
         load_scales(K, Wk_scales)
-        for g in range(5, GROUPS):
-            load_slots(STARTS[g], size(g))
+        for first in range(20, TILES, FULL):
+            load_slots(first, FULL)
 
         eye = keep.tile([P, P], F32, name="eye", align_bytes=64)
         make_identity(nc, eye[:])
 
         def permute_words():
             nc.vector.tensor_copy(
-                out=words[:].bitcast(I32).rearrange("p (t g e) -> p t g e", t=PACK, e=2),
-                in_=words_in[:, Q, :].bitcast(I32).rearrange("p (g t e) -> p t g e", t=PACK, e=2),
+                out=wq_words[:].bitcast(I32).rearrange("p (t m e) -> p t m e", t=PACK, e=2),
+                in_=words_in[:, Q, :].bitcast(I32).rearrange("p (m t e) -> p t m e", t=PACK, e=2),
             )
 
         def permute_scales():
             nc.vector.tensor_copy(
-                out=scales[:].bitcast(I32).rearrange("p (t g) -> p t g", t=PACK),
-                in_=scales_in[:, Q, :].bitcast(I32).rearrange("p (g t) -> p t g", t=PACK),
+                out=wq_scales[:].bitcast(I32).rearrange("p (t m) -> p t m", t=PACK),
+                in_=scales_in[:, Q, :].bitcast(I32).rearrange("p (m t) -> p t m", t=PACK),
             )
 
         wide, turned, slots4, slots_q, proj, query4, query_q = {}, {}, {}, {}, {}, {}, {}
         logits, tops, flipped, biases, exps, sums, inverses = {}, {}, {}, {}, {}, {}, {}
 
-        planes = [keep.tile([P, 6 * FEATURES], BF16, name="plane_%d" % n, align_bytes=64) for n in range(7)]
+        rooms = [
+            keep.tile([P, WIDEST * FEATURES], BF16, name="room_%d" % index, align_bytes=64) for index in range(7)
+        ]
         for g in range(GROUPS):
-            query4[g] = planes[g % 3][:].rearrange("p (r t) -> p r t", t=PACK)
-            slots4[g] = planes[(3, 6)[g] if g < 2 else 4 + g % 2][:].rearrange("p (r t) -> p r t", t=PACK)
+            query4[g] = rooms[g % 3][:].rearrange("p (r t) -> p r t", t=PACK)
+            slots4[g] = rooms[(3, 6)[g] if g < 2 else 4 + g % 2][:].rearrange("p (r t) -> p r t", t=PACK)
 
-        def widen(first, tiles, copy, t=None):
-            if t is None:
-                t = keep.tile([P, tiles * FEATURES], BF16, name="wide_%d" % first, align_bytes=64)
-            src, j = raw_bytes[first]
-            copy(out=t[:, : tiles * FEATURES], in_=src[:, j : j + tiles, :].rearrange("p j k -> p (j k)").bitcast(FP8))
-            for i in range(tiles):
-                wide[first + i] = t[:, i * FEATURES : (i + 1) * FEATURES]
+        def widen(first, tiles, copy, room=None):
+            if room is None:
+                room = keep.tile([P, tiles * FEATURES], BF16, name="wide_%d" % first, align_bytes=64)
+            held, j = raw_bytes[first]
+            copy(
+                out=room[:, : tiles * FEATURES],
+                in_=held[:, j : j + tiles, :].rearrange("p j k -> p (j k)").bitcast(FP8),
+            )
+            for tile in range(first, first + tiles):
+                wide[tile] = room[:, (tile - first) * FEATURES : (tile - first + 1) * FEATURES]
 
-        def widen_on_scalar(out, in_):
+        def copy_by_activation(out, in_):
             nc.scalar.activation(out=out, in_=in_, func=COPY)
 
         def turn_rows(dst, src):
             src_words = src.bitcast(F32)
-            for u in range(2):
-                nc.tensor.transpose(dst[:, u, :], src_words[:, u::2], eye[:])
+            for h in range(2):
+                nc.tensor.transpose(dst[:, h, :], src_words[:, h::2], eye[:])
 
         def turn(first, tiles=2, pool=turn_psum, name="turned"):
             turned[first] = pool.tile([P, 2, tiles, P], F32, name=name)
@@ -143,63 +149,61 @@ def tile_actionbindingattention_pb_w4_kernel(
                 turn_rows(turned[first][:, :, j, :], wide[first + j])
 
         def scale_slots(first, tiles=2):
-            u, j = place(first)
+            g, j = place(first)
             n = tiles * P
+            halves = turned[first][:].rearrange("p h j r -> p h (j r)").bitcast(BF16)
             nc.vector.tensor_tensor(
-                out=slots4[u][:, j * P : j * P + n, :].rearrange("p r (h e) -> p r h e", e=2),
-                in0=turned[first][:].rearrange("p h j r -> p h (j r)").bitcast(BF16).rearrange("p h (r e) -> p r h e", e=2),
+                out=slots4[g][:, j * P : j * P + n, :].rearrange("p r (h e) -> p r h e", e=2),
+                in0=halves.rearrange("p h (r e) -> p r h e", e=2),
                 in1=scale4[:].rearrange("p (h e) -> p h e", e=2).unsqueeze(1).to_broadcast([P, n, 2, 2]),
                 op=MULT,
             )
 
-        def quantize(store, names, src, first, tiles):
-            u, j = place(first)
-            if u not in store:
-                store[u] = (
-                    work.tile([P, size(u) * P], U32, name=names[0], align_bytes=64),
-                    work.tile([P, size(u) * P], U8, name=names[1], align_bytes=64),
-                )
-            codes, code_scales = store[u]
-            cols = slice(P * j, P * (j + tiles))
+        def quantize(codes, code_scales, rows4):
             nc.vector.quantize_mx(
-                out=codes[:, cols].bitcast(FP8X4),
-                scales=code_scales[:, cols],
-                in_=src[u][:, cols, :].rearrange("p r t -> p (r t)"),
+                out=codes.bitcast(FP8X4), scales=code_scales, in_=rows4.rearrange("p r t -> p (r t)")
             )
 
-        def quantize_slots(first, tiles=UNIT):
-            quantize(slots_q, ("slot_codes", "slot_scales"), slots4, first, tiles)
-
-        def quantize_queries(first, tiles=UNIT):
-            quantize(query_q, ("query_codes", "query_scales"), query4, first, tiles)
-
-        def project(codes, code_scales):
-            bank = proj_psum.tile([P, PACK, P], F32, name="proj")
-            for t in range(PACK):
-                nc.tensor.matmul_mx(
-                    out=bank[:, t, :],
-                    lhsT=words[:, 2 * P * t : 2 * P * (t + 1)].bitcast(FP4X4),
-                    lhsT_scale=scales[:, P * t : P * (t + 1)],
-                    rhs=codes.bitcast(FP8X4),
-                    rhs_scale=code_scales,
-                    start=True,
-                    stop=True,
+        def quantize_tiles(made, names, src, first, tiles):
+            g, j = place(first)
+            if g not in made:
+                made[g] = (
+                    work.tile([P, group_size(g) * P], U32, name=names[0], align_bytes=64),
+                    work.tile([P, group_size(g) * P], U8, name=names[1], align_bytes=64),
                 )
-            return bank
+            codes, code_scales = made[g]
+            cols = slice(P * j, P * (j + tiles))
+            quantize(codes[:, cols], code_scales[:, cols], src[g][:, cols, :])
 
-        def queries(first, tiles):
-            for i in range(first, first + tiles):
-                g, j = place(i)
+        def quantize_slots(first, tiles):
+            quantize_tiles(slots_q, ("slot_codes", "slot_scales"), slots4, first, tiles)
+
+        def quantize_queries(first, tiles):
+            quantize_tiles(query_q, ("query_codes", "query_scales"), query4, first, tiles)
+
+        def project_queries(first, tiles):
+            for tile in range(first, first + tiles):
+                g, j = place(tile)
                 codes, code_scales = slots_q[g]
                 cols = slice(P * j, P * (j + 1))
-                proj[i] = project(codes[:, cols], code_scales[:, cols])
+                proj[tile] = proj_psum.tile([P, PACK, P], F32, name="proj")
+                for t in range(PACK):
+                    nc.tensor.matmul_mx(
+                        out=proj[tile][:, t, :],
+                        lhsT=wq_words[:, 2 * P * t : 2 * P * (t + 1)].bitcast(FP4X4),
+                        lhsT_scale=wq_scales[:, P * t : P * (t + 1)],
+                        rhs=codes[:, cols].bitcast(FP8X4),
+                        rhs_scale=code_scales[:, cols],
+                        start=True,
+                        stop=True,
+                    )
 
-        def lay_queries(first, tiles, copy):
-            for i in range(first, first + tiles):
-                u, j = place(i)
-                copy(out=query4[u][:, j * P : (j + 1) * P, :], in_=proj[i][:].rearrange("p t r -> p r t"))
+        def lay_queries(first, tiles, copy=nc.scalar.copy):
+            for tile in range(first, first + tiles):
+                g, j = place(tile)
+                copy(out=query4[g][:, j * P : (j + 1) * P, :], in_=proj[tile][:].rearrange("p t r -> p r t"))
 
-        def multiply_keys(first, tiles=UNIT, pool=logit_psum, name="logits"):
+        def multiply_keys(first, tiles, pool=logit_psum, name="logits"):
             logits[first] = pool.tile([P, 2 * tiles, SLOTS], F32, name=name)
             g, j = place(first)
             codes, code_scales = query_q[g]
@@ -229,7 +233,7 @@ def tile_actionbindingattention_pb_w4_kernel(
 
         def flip_logits(first):
             samples = logits[first].shape[1]
-            flipped[first] = soft.tile([P, samples, SLOTS], F32, name="flipped", bufs=3)
+            flipped[first] = soft.tile([P, samples, SLOTS], F32, name="flipped", bufs=FLIPPED)
             biases[first] = soft.tile([P, samples], F32, name="biases")
             for b in range(samples):
                 nc.vector.tensor_scalar(
@@ -242,14 +246,14 @@ def tile_actionbindingattention_pb_w4_kernel(
                     accum_out=biases[first][:, b : b + 1],
                 )
 
-        def exponentiate(first, between=None):
+        def exponentiate(first, negate=None):
             samples = logits[first].shape[1]
             src, factor = (flipped[first], -1.0) if first in flipped else (logits[first], LOGIT_SCALE)
             exps[first] = soft.tile([P, samples, SLOTS], F32, name="exps")
             sums[first] = soft.tile([P, samples], F32, name="sums")
             for b in range(samples):
-                if between is not None and b == samples - 2:
-                    negate_tops(between)
+                if negate is not None and b == samples - 2:
+                    negate_tops(negate)
                 nc.scalar.activation(
                     out=exps[first][:, b, :],
                     in_=src[:, b, :],
@@ -263,45 +267,39 @@ def tile_actionbindingattention_pb_w4_kernel(
             inverses[first] = soft.tile([P, logits[first].shape[1]], F32, name="inverses")
             nc.vector.reciprocal(out=inverses[first][:], in_=sums[first][:])
 
-        def divide_and_store(first, engine=None, room=None, between=None, part=None, queue=nc.sync):
-            lo, samples = part or (0, logits[first].shape[1])
+        def divide_and_store(first, engine=None, room=None, part=None, negate=None, queue=nc.sync):
+            start, samples = part or (0, logits[first].shape[1])
             if room is None:
                 shares = soft.tile([P, samples, SLOTS], F32, name="shares")
             else:
                 shares = room[:].bitcast(F32)[:, : samples * SLOTS].rearrange("p (b s) -> p b s", s=SLOTS)
             if engine is None:
                 for b in range(samples):
-                    if between is not None and b == samples - 3:
-                        negate_tops(between)
+                    if negate is not None and b == samples - 3:
+                        negate_tops(negate)
                     nc.scalar.activation(
                         out=shares[:, b, :],
-                        in_=exps[first][:, lo + b, :],
+                        in_=exps[first][:, start + b, :],
                         func=COPY,
-                        scale=inverses[first][:, lo + b : lo + b + 1],
+                        scale=inverses[first][:, start + b : start + b + 1],
                     )
             else:
                 engine.tensor_tensor(
                     out=shares[:],
-                    in0=exps[first][:, lo : lo + samples, :],
-                    in1=inverses[first][:, lo : lo + samples].unsqueeze(2).to_broadcast([P, samples, SLOTS]),
+                    in0=exps[first][:, start : start + samples, :],
+                    in1=inverses[first][:, start : start + samples].unsqueeze(2).to_broadcast([P, samples, SLOTS]),
                     op=MULT,
                 )
-            queue.dma_start(
-                out=out[2 * first + lo : 2 * first + lo + samples].rearrange("b n s -> n b s"), in_=shares[:]
-            )
+            sample = 2 * first + start
+            queue.dma_start(out=out[sample : sample + samples].rearrange("b n s -> n b s"), in_=shares[:])
 
         ident4 = keep.tile([P, P, PACK], BF16, name="ident4", align_bytes=64)
         ident_codes = keep.tile([P, P], U32, name="ident_codes", align_bytes=64)
         ident_scales = keep.tile([P, P], U8, name="ident_scales", align_bytes=64)
         key_rows = keep.tile([P, FEATURES], BF16, name="key_rows", align_bytes=64)
-        key4 = planes[1][:, UNIT * FEATURES : (UNIT + 1) * FEATURES].rearrange("p (r t) -> p r t", t=PACK)
+        key4 = rooms[1][:, FULL * FEATURES : (FULL + 1) * FEATURES].rearrange("p (r t) -> p r t", t=PACK)
         key_codes = keep.tile([P, P], U32, name="key_codes", align_bytes=64)
         key_scales = keep.tile([P, P], U8, name="key_scales", align_bytes=64)
-
-        def quantize_keep(codes, code_scales, src):
-            nc.vector.quantize_mx(
-                out=codes[:].bitcast(FP8X4), scales=code_scales[:], in_=src[:].rearrange("p r t -> p (r t)")
-            )
 
         def project_keys():
             bank = logit_psum.tile([P, FEATURES], F32, name="logits")
@@ -315,22 +313,23 @@ def tile_actionbindingattention_pb_w4_kernel(
                 stop=True,
             )
             nc.scalar.copy(
-                out=key_rows[:].rearrange("p (g i t) -> p g i t", i=PACK, t=PACK),
-                in_=bank[:].rearrange("p (g t i) -> p g i t", i=PACK, t=PACK),
+                out=key_rows[:].rearrange("p (m i t) -> p m i t", i=PACK, t=PACK),
+                in_=bank[:].rearrange("p (m t i) -> p m i t", i=PACK, t=PACK),
             )
 
         def lay_words(dst, bank):
             nc.scalar.copy(
-                out=dst[:].rearrange("p r t -> p (r t)").bitcast(F32).rearrange("p (r u) -> p r u", u=2),
-                in_=bank[:].rearrange("p u r -> p r u"),
+                out=dst.rearrange("p r t -> p (r t)").bitcast(F32).rearrange("p (r h) -> p r h", h=2),
+                in_=bank[:].rearrange("p h r -> p r h"),
             )
+
 
         widen(0, 1, nc.vector.tensor_copy)
         turn(0, 1)
         widen(1, 1, nc.vector.tensor_copy)
         turn(1, 1)
         widen(2, 1, nc.vector.tensor_copy)
-        widen(3, 1, widen_on_scalar)
+        widen(3, 1, copy_by_activation)
         turn(2, 2, logit_psum, "logits")
         widen(4, 2, nc.scalar.copy)
         ident_bank = proj_psum.tile([P, 2, P], F32, name="proj")
@@ -343,26 +342,26 @@ def tile_actionbindingattention_pb_w4_kernel(
         quantize_slots(0, 1)
         permute_scales()
         quantize_slots(1, 1)
-        widen(8, 3, nc.gpsimd.tensor_copy, planes[3])
-        queries(0, 2)
+        widen(8, 3, nc.gpsimd.tensor_copy, rooms[3])
+        project_queries(0, 2)
         turn(6)
         widen(11, 1, nc.scalar.copy)
-        lay_words(ident4, ident_bank)
+        lay_words(ident4[:], ident_bank)
 
         scale_slots(2)
-        lay_queries(0, 1, nc.scalar.copy)
+        lay_queries(0, 1)
         widen(17, 1, nc.scalar.copy)
-        lay_queries(1, 1, nc.scalar.copy)
+        lay_queries(1, 1)
         scale_slots(4)
-        quantize_keep(ident_codes, ident_scales, ident4)
+        quantize(ident_codes[:], ident_scales[:], ident4[:])
         project_keys()
         turn(8)
         turn(10, 2, logit_psum, "logits")
         quantize_slots(2, 2)
-        queries(2, 2)
+        project_queries(2, 2)
         quantize_slots(4, 2)
-        widen(12, 5, nc.gpsimd.tensor_copy, planes[6])
-        queries(4, 2)
+        widen(12, 5, nc.gpsimd.tensor_copy, rooms[6])
+        project_queries(4, 2)
         key_bank = logit_psum.tile([P, 2, P], F32, name="logits")
         turn_rows(key_bank, key_rows[:])
         widen(18, 1, nc.scalar.copy)
@@ -370,24 +369,24 @@ def tile_actionbindingattention_pb_w4_kernel(
         scale_slots(6)
         scale_slots(8)
         scale_slots(10)
-        lay_queries(2, 2, nc.scalar.copy)
-        lay_queries(4, 2, nc.scalar.copy)
+        lay_queries(2, 2)
+        lay_queries(4, 2)
         lay_words(key4, key_bank)
         widen(19, 1, nc.scalar.copy)
         turn(12)
         quantize_slots(6, 2)
-        queries(6, 2)
-        quantize_slots(8, 4)
+        project_queries(6, 2)
+        quantize_slots(8, FULL)
         quantize_queries(0, 2)
         turn(14)
-        quantize_queries(2)
-        quantize_keep(key_codes, key_scales, key4)
+        quantize_queries(2, FULL)
+        quantize(key_codes[:], key_scales[:], key4)
         multiply_keys(0, 2)
-        widen(20, UNIT, nc.gpsimd.tensor_copy, planes[1][:, FEATURES:])
-        queries(8, 2)
-        multiply_keys(2)
-        lay_queries(6, 2, nc.scalar.copy)
-        queries(10, 2)
+        widen(20, FULL, nc.gpsimd.tensor_copy, rooms[1][:, FEATURES:])
+        project_queries(8, 2)
+        multiply_keys(2, FULL)
+        lay_queries(6, 2)
+        project_queries(10, 2)
 
         scale_slots(12)
         find_tops(0)
@@ -395,20 +394,20 @@ def tile_actionbindingattention_pb_w4_kernel(
         turn(16)
         turn(18)
         find_tops(2)
-        lay_queries(8, 3, nc.scalar.copy)
+        lay_queries(8, 3)
         negate_tops(0)
-        lay_queries(11, 1, nc.scalar.copy)
-        exponentiate(0, between=2)
+        lay_queries(11, 1)
+        exponentiate(0, negate=2)
         quantize_slots(12, 2)
-        queries(12, 2)
+        project_queries(12, 2)
         quantize_slots(14, 2)
         quantize_queries(6, 2)
-        quantize_queries(8, 4)
-        widen(24, UNIT, nc.gpsimd.tensor_copy, planes[2])
+        quantize_queries(8, FULL)
+        widen(24, FULL, nc.gpsimd.tensor_copy, rooms[2])
         multiply_keys(6, 2)
         exponentiate(2)
-        queries(14, 2)
-        multiply_keys(8, 4)
+        project_queries(14, 2)
+        multiply_keys(8, FULL)
 
         scale_slots(16)
         find_tops(6)
@@ -417,21 +416,21 @@ def tile_actionbindingattention_pb_w4_kernel(
         turn(20)
         turn(22)
         find_tops(8)
-        lay_queries(12, 3, nc.scalar.copy)
+        lay_queries(12, 3)
         negate_tops(6)
-        lay_queries(15, 1, nc.scalar.copy)
+        lay_queries(15, 1)
         exponentiate(6)
-        divide_and_store(0, between=8)
+        divide_and_store(0, negate=8)
         quantize_slots(16, 2)
-        queries(16, 2)
+        project_queries(16, 2)
         invert_sums(2)
         quantize_slots(18, 2)
-        quantize_queries(12)
-        widen(28, UNIT, nc.gpsimd.tensor_copy, planes[0])
+        quantize_queries(12, FULL)
+        widen(28, FULL, nc.gpsimd.tensor_copy, rooms[0])
         exponentiate(8)
-        queries(18, 1)
-        multiply_keys(12)
-        queries(19, 1)
+        project_queries(18, 1)
+        multiply_keys(12, FULL)
+        project_queries(19, 1)
 
         scale_slots(20)
         invert_sums(6)
@@ -439,33 +438,34 @@ def tile_actionbindingattention_pb_w4_kernel(
         turn(24)
         turn(26)
         find_tops(12)
-        lay_queries(16, UNIT, nc.scalar.copy)
-        divide_and_store(2, between=12)
+        lay_queries(16, FULL)
+        divide_and_store(2, negate=12)
         quantize_slots(20, 2)
-        queries(20, 2)
+        project_queries(20, 2)
         invert_sums(8)
         quantize_slots(22, 2)
-        quantize_queries(16)
-        divide_and_store(8, nc.gpsimd, planes[1])
-        divide_and_store(6, nc.gpsimd)
+        quantize_queries(16, FULL)
+        divide_and_store(8, nc.gpsimd, rooms[1])
+        divide_and_store(6, nc.gpsimd, part=(0, 2))
         exponentiate(12)
-        multiply_keys(16)
-        queries(22, 2)
+        divide_and_store(6, part=(2, 2))
+        multiply_keys(16, FULL)
+        project_queries(22, 2)
 
         scale_slots(24)
         turn(28)
-        lay_queries(20, 2, nc.scalar.copy)
+        lay_queries(20, 2)
         find_tops(16)
         scale_slots(26)
-        lay_queries(22, 1, nc.scalar.copy)
+        lay_queries(22, 1)
         negate_tops(16)
-        lay_queries(23, 1, nc.scalar.copy)
+        lay_queries(23, 1)
+        turn(30, 1)
         quantize_queries(20, 2)
         multiply_keys(20, 2)
-        turn(30, 1)
         invert_sums(12)
         quantize_slots(24, 2)
-        queries(24, 2)
+        project_queries(24, 2)
         exponentiate(16)
         quantize_queries(22, 2)
         multiply_keys(22, 2)
@@ -473,39 +473,40 @@ def tile_actionbindingattention_pb_w4_kernel(
         find_tops(20)
         invert_sums(16)
         divide_and_store(16, nc.gpsimd)
-        divide_and_store(12, between=20)
-        queries(26, 1)
+        divide_and_store(12)
+        project_queries(26, 1)
         turn(31, 1, proj_psum, "proj")
-        queries(27, 1)
+        project_queries(27, 1)
 
         scale_slots(28)
+        negate_tops(20)
+        lay_queries(24, 1)
         exponentiate(20)
-        lay_queries(24, 1, nc.scalar.copy)
         scale_slots(30, 1)
         find_tops(22)
-        lay_queries(25, 2, nc.scalar.copy)
+        lay_queries(25, 2)
         negate_tops(22)
-        lay_queries(27, 1, nc.scalar.copy)
+        lay_queries(27, 1)
         exponentiate(22)
         quantize_slots(28, 2)
-        queries(28, 2)
+        project_queries(28, 2)
         scale_slots(31, 1)
         quantize_slots(30, 1)
         quantize_queries(24, 2)
         quantize_slots(31, 1)
         multiply_keys(24, 2)
-        queries(30, 2)
+        project_queries(30, 2)
         quantize_queries(26, 2)
         multiply_keys(26, 2)
         invert_sums(20)
         divide_and_store(20, nc.gpsimd)
         invert_sums(22)
-        lay_queries(28, 1, nc.scalar.copy)
+        lay_queries(28, 1)
         find_tops(24)
-        lay_queries(29, 1, nc.scalar.copy)
+        lay_queries(29, 1)
         lay_queries(30, 1, nc.vector.tensor_copy)
         negate_tops(24)
-        lay_queries(31, 1, nc.scalar.copy)
+        lay_queries(31, 1)
         quantize_queries(28, 2)
         multiply_keys(28, 2, turn_psum, "turned")
         find_tops(26)
@@ -514,8 +515,7 @@ def tile_actionbindingattention_pb_w4_kernel(
         multiply_keys(30, 1, turn_psum, "turned")
         quantize_queries(31, 1)
         multiply_keys(31, 1, proj_psum, "proj")
-        negate_tops(26, False)
-        divide_and_store(22, nc.vector)
+        divide_and_store(22, negate=26)
         exponentiate(26)
         invert_sums(24)
         divide_and_store(24, nc.gpsimd)
@@ -526,10 +526,10 @@ def tile_actionbindingattention_pb_w4_kernel(
         flip_logits(31)
         exponentiate(30)
         exponentiate(31)
-        invert_sums(28)
         divide_and_store(26, nc.vector)
         invert_sums(30)
-        divide_and_store(28, nc.vector)
-        invert_sums(31)
+        invert_sums(28)
         divide_and_store(30, queue=nc.scalar)
+        invert_sums(31)
+        divide_and_store(28, nc.vector)
         divide_and_store(31, nc.vector)

@@ -50,7 +50,7 @@ def tile_actionbindingattention_pb_w4_kernel(
     with ExitStack() as ctx:
         keep = ctx.enter_context(tc.tile_pool(name="keep", bufs=1))
         work = ctx.enter_context(tc.tile_pool(name="work", bufs=3))
-        soft = ctx.enter_context(tc.tile_pool(name="soft", bufs=SOFT_BUFFERS))
+        soft = ctx.enter_context(tc.tile_pool(name="soft", bufs=FLIPPED))
         turn_psum = ctx.enter_context(tc.psum_pool(name="turn_psum", bufs=2))
         proj_psum = ctx.enter_context(tc.psum_pool(name="proj_psum", bufs=4))
         logit_psum = ctx.enter_context(tc.psum_pool(name="logit_psum", bufs=2))
@@ -96,8 +96,9 @@ def tile_actionbindingattention_pb_w4_kernel(
         load_words(K, Wk_words)
         load_slots(12, 8)
         load_scales(K, Wk_scales)
-        for first in range(20, TILES, FULL):
-            load_slots(first, FULL)
+        load_slots(20, 4)
+        load_slots(24, 3)
+        load_slots(27, 5)
 
         eye = keep.tile([P, P], F32, name="eye", align_bytes=64)
         make_identity(nc, eye[:])
@@ -115,14 +116,15 @@ def tile_actionbindingattention_pb_w4_kernel(
             )
 
         wide, turned, slots4, slots_q, proj, query4, query_q = {}, {}, {}, {}, {}, {}, {}
-        logits, tops, flipped, biases, exps, sums, inverses = {}, {}, {}, {}, {}, {}, {}
+        logits, flipped = {}, {}
 
-        rooms = [
-            keep.tile([P, WIDEST * FEATURES], BF16, name="room_%d" % index, align_bytes=64) for index in range(7)
-        ]
+        rooms = [keep.tile([P, WIDEST * FEATURES], BF16, name="room_%d" % g, align_bytes=64) for g in range(GROUPS)]
+        early = [keep.tile([P, n * FEATURES], BF16, name="early_%d" % n, align_bytes=64) for n in (3, 8, 6)]
+        scaled = [keep.tile([P, FULL * FEATURES], BF16, name="scaled_%d" % i, align_bytes=64) for i in range(2)]
         for g in range(GROUPS):
-            query4[g] = rooms[g % 3][:].rearrange("p (r t) -> p r t", t=PACK)
-            slots4[g] = rooms[(3, 6)[g] if g < 2 else 4 + g % 2][:].rearrange("p (r t) -> p r t", t=PACK)
+            query4[g] = rooms[g][:].rearrange("p (r t) -> p r t", t=PACK)
+            held = (early[0][:], early[1][:, 4 * FEATURES :], early[2][:])[g] if g < 3 else scaled[g % 2][:]
+            slots4[g] = held.rearrange("p (r t) -> p r t", t=PACK)
 
         def widen(first, tiles, copy, room=None):
             if room is None:
@@ -218,23 +220,27 @@ def tile_actionbindingattention_pb_w4_kernel(
                 stop=True,
             )
 
-        def find_tops(first):
-            tops[first] = soft.tile([P, logits[first].shape[1]], F32, name="tops")
-            nc.vector.tensor_reduce(out=tops[first][:], in_=logits[first][:], axis=AXIS_X, op=MAX)
+        tops = keep.tile([P, SAMPLES], F32, name="tops")
+        biases = keep.tile([P, SAMPLES], F32, name="biases")
+        sums = keep.tile([P, SAMPLES], F32, name="sums")
+        inverses = keep.tile([P, SAMPLES], F32, name="inverses")
+        exps = keep.tile([P, SAMPLES, SLOTS], F32, name="exps")
+        shares = keep.tile([P, SAMPLES, SLOTS], F32, name="shares")
 
-        def negate_tops(first, on_scalar=True):
-            biases[first] = soft.tile([P, logits[first].shape[1]], F32, name="biases")
-            if on_scalar:
-                nc.scalar.activation(out=biases[first][:], in_=tops[first][:], func=COPY, scale=-LOGIT_SCALE)
-            else:
-                nc.vector.tensor_scalar(
-                    out=biases[first][:], in0=tops[first][:], scalar1=-LOGIT_SCALE, scalar2=None, op0=MULT
-                )
+        def samples_of(first):
+            return slice(2 * first, 2 * first + logits[first].shape[1])
+
+        def find_tops(first):
+            nc.vector.tensor_reduce(out=tops[:, samples_of(first)], in_=logits[first][:], axis=AXIS_X, op=MAX)
+
+        def negate_tops(first):
+            nc.scalar.activation(
+                out=biases[:, samples_of(first)], in_=tops[:, samples_of(first)], func=COPY, scale=-LOGIT_SCALE
+            )
 
         def flip_logits(first):
             samples = logits[first].shape[1]
             flipped[first] = soft.tile([P, samples, SLOTS], F32, name="flipped", bufs=FLIPPED)
-            biases[first] = soft.tile([P, samples], F32, name="biases")
             for b in range(samples):
                 nc.vector.tensor_scalar(
                     out=flipped[first][:, b, :],
@@ -243,55 +249,54 @@ def tile_actionbindingattention_pb_w4_kernel(
                     scalar2=None,
                     op0=MULT,
                     op1=MIN,
-                    accum_out=biases[first][:, b : b + 1],
+                    accum_out=biases[:, 2 * first + b : 2 * first + b + 1],
                 )
 
-        def exponentiate(first, negate=None):
-            samples = logits[first].shape[1]
+        def exponentiate(first, negate=None, part=None):
+            start, samples = part or (0, logits[first].shape[1])
             src, factor = (flipped[first], -1.0) if first in flipped else (logits[first], LOGIT_SCALE)
-            exps[first] = soft.tile([P, samples, SLOTS], F32, name="exps")
-            sums[first] = soft.tile([P, samples], F32, name="sums")
-            for b in range(samples):
-                if negate is not None and b == samples - 2:
+            for b in range(start, start + samples):
+                if negate is not None and b == start + samples - 2:
                     negate_tops(negate)
+                sample = 2 * first + b
                 nc.scalar.activation(
-                    out=exps[first][:, b, :],
+                    out=exps[:, sample, :],
                     in_=src[:, b, :],
                     func=EXP,
-                    bias=biases[first][:, b : b + 1],
+                    bias=biases[:, sample : sample + 1],
                     scale=factor,
-                    accum_out=sums[first][:, b : b + 1],
+                    accum_out=sums[:, sample : sample + 1],
                 )
 
-        def invert_sums(first):
-            inverses[first] = soft.tile([P, logits[first].shape[1]], F32, name="inverses")
-            nc.vector.reciprocal(out=inverses[first][:], in_=sums[first][:])
+        def invert_sums(first, tiles):
+            cols = slice(2 * first, 2 * (first + tiles))
+            nc.vector.reciprocal(out=inverses[:, cols], in_=sums[:, cols])
 
-        def divide_and_store(first, engine=None, room=None, part=None, negate=None, queue=nc.sync):
-            start, samples = part or (0, logits[first].shape[1])
+        def divide_and_store(first, tiles, engine=None, room=None, negate=None, queue=nc.sync):
+            start, samples = 2 * first, 2 * tiles
+            cols = slice(start, start + samples)
             if room is None:
-                shares = soft.tile([P, samples, SLOTS], F32, name="shares")
+                dst = shares[:, cols, :]
             else:
-                shares = room[:].bitcast(F32)[:, : samples * SLOTS].rearrange("p (b s) -> p b s", s=SLOTS)
+                dst = room[:].bitcast(F32)[:, : samples * SLOTS].rearrange("p (b s) -> p b s", s=SLOTS)
             if engine is None:
                 for b in range(samples):
                     if negate is not None and b == samples - 3:
                         negate_tops(negate)
                     nc.scalar.activation(
-                        out=shares[:, b, :],
-                        in_=exps[first][:, start + b, :],
+                        out=dst[:, b, :],
+                        in_=exps[:, start + b, :],
                         func=COPY,
-                        scale=inverses[first][:, start + b : start + b + 1],
+                        scale=inverses[:, start + b : start + b + 1],
                     )
             else:
                 engine.tensor_tensor(
-                    out=shares[:],
-                    in0=exps[first][:, start : start + samples, :],
-                    in1=inverses[first][:, start : start + samples].unsqueeze(2).to_broadcast([P, samples, SLOTS]),
+                    out=dst,
+                    in0=exps[:, cols, :],
+                    in1=inverses[:, cols].unsqueeze(2).to_broadcast([P, samples, SLOTS]),
                     op=MULT,
                 )
-            sample = 2 * first + start
-            queue.dma_start(out=out[sample : sample + samples].rearrange("b n s -> n b s"), in_=shares[:])
+            queue.dma_start(out=out[cols].rearrange("b n s -> n b s"), in_=dst)
 
         ident4 = keep.tile([P, P, PACK], BF16, name="ident4", align_bytes=64)
         ident_codes = keep.tile([P, P], U32, name="ident_codes", align_bytes=64)
@@ -342,16 +347,16 @@ def tile_actionbindingattention_pb_w4_kernel(
         quantize_slots(0, 1)
         permute_scales()
         quantize_slots(1, 1)
-        widen(8, 3, nc.gpsimd.tensor_copy, rooms[3])
+        widen(8, 2, nc.gpsimd.tensor_copy, early[0])
         project_queries(0, 2)
         turn(6)
-        widen(11, 1, nc.scalar.copy)
         lay_words(ident4[:], ident_bank)
+        widen(10, 2, nc.scalar.copy)
 
         scale_slots(2)
         lay_queries(0, 1)
-        widen(17, 1, nc.scalar.copy)
         lay_queries(1, 1)
+        widen(16, 4, nc.scalar.copy)
         scale_slots(4)
         quantize(ident_codes[:], ident_scales[:], ident4[:])
         project_keys()
@@ -360,19 +365,20 @@ def tile_actionbindingattention_pb_w4_kernel(
         quantize_slots(2, 2)
         project_queries(2, 2)
         quantize_slots(4, 2)
-        widen(12, 5, nc.gpsimd.tensor_copy, rooms[6])
+        widen(12, 4, nc.gpsimd.tensor_copy, early[1][:, 4 * FEATURES :])
         project_queries(4, 2)
         key_bank = logit_psum.tile([P, 2, P], F32, name="logits")
         turn_rows(key_bank, key_rows[:])
-        widen(18, 1, nc.scalar.copy)
+        widen(23, 1, nc.scalar.copy)
+        widen(27, 1, nc.scalar.copy)
 
         scale_slots(6)
         scale_slots(8)
         scale_slots(10)
         lay_queries(2, 2)
         lay_queries(4, 2)
-        lay_words(key4, key_bank)
-        widen(19, 1, nc.scalar.copy)
+        lay_words(key4[:], key_bank)
+        widen(28, 1, nc.scalar.copy)
         turn(12)
         quantize_slots(6, 2)
         project_queries(6, 2)
@@ -380,12 +386,13 @@ def tile_actionbindingattention_pb_w4_kernel(
         quantize_queries(0, 2)
         turn(14)
         quantize_queries(2, FULL)
-        quantize(key_codes[:], key_scales[:], key4)
+        quantize(key_codes[:], key_scales[:], key4[:])
         multiply_keys(0, 2)
-        widen(20, FULL, nc.gpsimd.tensor_copy, rooms[1][:, FEATURES:])
+        widen(20, 3, nc.gpsimd.tensor_copy, rooms[1][:, 2 * FEATURES :])
         project_queries(8, 2)
         multiply_keys(2, FULL)
         lay_queries(6, 2)
+        widen(29, 2, nc.scalar.copy)
         project_queries(10, 2)
 
         scale_slots(12)
@@ -403,7 +410,7 @@ def tile_actionbindingattention_pb_w4_kernel(
         quantize_slots(14, 2)
         quantize_queries(6, 2)
         quantize_queries(8, FULL)
-        widen(24, FULL, nc.gpsimd.tensor_copy, rooms[2])
+        widen(24, 3, nc.gpsimd.tensor_copy, rooms[2][:, 2 * FEATURES :])
         multiply_keys(6, 2)
         exponentiate(2)
         project_queries(14, 2)
@@ -411,7 +418,6 @@ def tile_actionbindingattention_pb_w4_kernel(
 
         scale_slots(16)
         find_tops(6)
-        invert_sums(0)
         scale_slots(18)
         turn(20)
         turn(22)
@@ -419,36 +425,33 @@ def tile_actionbindingattention_pb_w4_kernel(
         lay_queries(12, 3)
         negate_tops(6)
         lay_queries(15, 1)
-        exponentiate(6)
-        divide_and_store(0, negate=8)
+        exponentiate(6, negate=8)
         quantize_slots(16, 2)
         project_queries(16, 2)
-        invert_sums(2)
+        invert_sums(0, 6)
         quantize_slots(18, 2)
         quantize_queries(12, FULL)
-        widen(28, FULL, nc.gpsimd.tensor_copy, rooms[0])
+        divide_and_store(0, 6, nc.gpsimd, rooms[3])
         exponentiate(8)
         project_queries(18, 1)
         multiply_keys(12, FULL)
         project_queries(19, 1)
 
         scale_slots(20)
-        invert_sums(6)
         scale_slots(22)
         turn(24)
         turn(26)
         find_tops(12)
         lay_queries(16, FULL)
-        divide_and_store(2, negate=12)
+        negate_tops(12)
+        widen(31, 1, nc.scalar.copy)
         quantize_slots(20, 2)
         project_queries(20, 2)
-        invert_sums(8)
+        invert_sums(6, 6)
         quantize_slots(22, 2)
         quantize_queries(16, FULL)
-        divide_and_store(8, nc.gpsimd, rooms[1])
-        divide_and_store(6, nc.gpsimd, part=(0, 2))
+        divide_and_store(6, 6, nc.gpsimd, rooms[4])
         exponentiate(12)
-        divide_and_store(6, part=(2, 2))
         multiply_keys(16, FULL)
         project_queries(22, 2)
 
@@ -463,31 +466,31 @@ def tile_actionbindingattention_pb_w4_kernel(
         turn(30, 1)
         quantize_queries(20, 2)
         multiply_keys(20, 2)
-        invert_sums(12)
+        invert_sums(12, 4)
         quantize_slots(24, 2)
         project_queries(24, 2)
         exponentiate(16)
         quantize_queries(22, 2)
         multiply_keys(22, 2)
         quantize_slots(26, 2)
+        divide_and_store(12, 4, nc.gpsimd, scaled[0][:, 2 * FEATURES :])
         find_tops(20)
-        invert_sums(16)
-        divide_and_store(16, nc.gpsimd)
-        divide_and_store(12)
-        project_queries(26, 1)
+        invert_sums(16, 4)
         turn(31, 1, proj_psum, "proj")
-        project_queries(27, 1)
+        project_queries(26, 2)
 
         scale_slots(28)
-        negate_tops(20)
         lay_queries(24, 1)
+        negate_tops(20)
+        lay_queries(25, 1)
         exponentiate(20)
         scale_slots(30, 1)
         find_tops(22)
-        lay_queries(25, 2)
+        lay_queries(26, 1)
         negate_tops(22)
         lay_queries(27, 1)
         exponentiate(22)
+        divide_and_store(16, 4)
         quantize_slots(28, 2)
         project_queries(28, 2)
         scale_slots(31, 1)
@@ -498,9 +501,9 @@ def tile_actionbindingattention_pb_w4_kernel(
         project_queries(30, 2)
         quantize_queries(26, 2)
         multiply_keys(26, 2)
-        invert_sums(20)
-        divide_and_store(20, nc.gpsimd)
-        invert_sums(22)
+        invert_sums(20, 2)
+        divide_and_store(20, 2, nc.gpsimd)
+        invert_sums(22, 2)
         lay_queries(28, 1)
         find_tops(24)
         lay_queries(29, 1)
@@ -515,21 +518,21 @@ def tile_actionbindingattention_pb_w4_kernel(
         multiply_keys(30, 1, turn_psum, "turned")
         quantize_queries(31, 1)
         multiply_keys(31, 1, proj_psum, "proj")
-        divide_and_store(22, negate=26)
+        divide_and_store(22, 2, negate=26)
         exponentiate(26)
-        invert_sums(24)
-        divide_and_store(24, nc.gpsimd)
+        invert_sums(24, 2)
+        divide_and_store(24, 2, nc.gpsimd)
         flip_logits(28)
         exponentiate(28)
         flip_logits(30)
-        invert_sums(26)
+        invert_sums(26, 2)
         flip_logits(31)
         exponentiate(30)
         exponentiate(31)
-        divide_and_store(26, nc.vector)
-        invert_sums(30)
-        invert_sums(28)
-        divide_and_store(30, queue=nc.scalar)
-        invert_sums(31)
-        divide_and_store(28, nc.vector)
-        divide_and_store(31, nc.vector)
+        divide_and_store(26, 2, nc.vector)
+        invert_sums(30, 1)
+        invert_sums(28, 2)
+        divide_and_store(30, 1, queue=nc.scalar)
+        invert_sums(31, 1)
+        divide_and_store(28, 2, nc.vector)
+        divide_and_store(31, 1, nc.vector)

@@ -110,7 +110,7 @@ def tile_actionbindingattention_pb_w4_kernel(
             )
 
         def permute_scales():
-            nc.vector.tensor_copy(
+            nc.gpsimd.tensor_copy(
                 out=wq_scales[:].bitcast(I32).rearrange("p (t m) -> p t m", t=PACK),
                 in_=scales_in[:, Q, :].bitcast(I32).rearrange("p (m t) -> p t m", t=PACK),
             )
@@ -150,14 +150,30 @@ def tile_actionbindingattention_pb_w4_kernel(
             for j in range(tiles):
                 turn_rows(turned[first][:, :, j, :], wide[first + j])
 
-        def scale_slots(first, tiles=2):
+        def scale_slots(first, tiles=2, held=None):
             g, j = place(first)
             n = tiles * P
-            halves = turned[first][:].rearrange("p h j r -> p h (j r)").bitcast(BF16)
+            i = 0 if held is None else first - held
+            halves = turned[first - i][:, :, i : i + tiles, :].rearrange("p h j r -> p h (j r)").bitcast(BF16)
             nc.vector.tensor_tensor(
                 out=slots4[g][:, j * P : j * P + n, :].rearrange("p r (h e) -> p r h e", e=2),
                 in0=halves.rearrange("p h (r e) -> p r h e", e=2),
                 in1=scale4[:].rearrange("p (h e) -> p h e", e=2).unsqueeze(1).to_broadcast([P, n, 2, 2]),
+                op=MULT,
+            )
+
+        plain4, late4 = {}, {}
+
+        def lay_plain(first, j):
+            plain4[first + j] = keep.tile([P, P, PACK], BF16, name="plain_%d" % (first + j), align_bytes=64)
+            lay_words(plain4[first + j][:], turned[first][:, :, j, :])
+
+        def scale_plain(tile, room):
+            late4[tile] = room[:, :FEATURES].rearrange("p (r t) -> p r t", t=PACK)
+            nc.gpsimd.tensor_tensor(
+                out=late4[tile],
+                in0=plain4[tile][:],
+                in1=scale4[:].unsqueeze(1).to_broadcast([P, P, PACK]),
                 op=MULT,
             )
 
@@ -175,7 +191,7 @@ def tile_actionbindingattention_pb_w4_kernel(
                 )
             codes, code_scales = made[g]
             cols = slice(P * j, P * (j + tiles))
-            quantize(codes[:, cols], code_scales[:, cols], src[g][:, cols, :])
+            quantize(codes[:, cols], code_scales[:, cols], late4[first] if names[0] == "slot_codes" and first in late4 else src[g][:, cols, :])
 
         def quantize_slots(first, tiles):
             quantize_tiles(slots_q, ("slot_codes", "slot_scales"), slots4, first, tiles)
@@ -325,7 +341,7 @@ def tile_actionbindingattention_pb_w4_kernel(
         def lay_words(dst, bank):
             nc.scalar.copy(
                 out=dst.rearrange("p r t -> p (r t)").bitcast(F32).rearrange("p (r h) -> p r h", h=2),
-                in_=bank[:].rearrange("p h r -> p r h"),
+                in_=bank.rearrange("p h r -> p r h"),
             )
 
 
@@ -345,41 +361,40 @@ def tile_actionbindingattention_pb_w4_kernel(
         scale_slots(0, 1)
         scale_slots(1, 1)
         quantize_slots(0, 1)
-        permute_scales()
         quantize_slots(1, 1)
-        widen(8, 2, nc.gpsimd.tensor_copy, early[0])
+        permute_scales()
+        widen(8, 3, nc.gpsimd.tensor_copy, early[0])
         project_queries(0, 2)
         turn(6)
-        lay_words(ident4[:], ident_bank)
-        widen(10, 2, nc.scalar.copy)
+        lay_words(ident4[:], ident_bank[:])
+        widen(11, 1, nc.scalar.copy)
 
         scale_slots(2)
         lay_queries(0, 1)
         lay_queries(1, 1)
-        widen(16, 4, nc.scalar.copy)
+        widen(17, 3, nc.scalar.copy)
         scale_slots(4)
         quantize(ident_codes[:], ident_scales[:], ident4[:])
         project_keys()
         turn(8)
-        turn(10, 2, logit_psum, "logits")
         quantize_slots(2, 2)
         project_queries(2, 2)
+        turn(10, 2, logit_psum, "logits")
         quantize_slots(4, 2)
-        widen(12, 4, nc.gpsimd.tensor_copy, early[1][:, 4 * FEATURES :])
+        widen(12, 5, nc.gpsimd.tensor_copy, early[1][:, 3 * FEATURES :])
         project_queries(4, 2)
         key_bank = logit_psum.tile([P, 2, P], F32, name="logits")
         turn_rows(key_bank, key_rows[:])
-        widen(23, 1, nc.scalar.copy)
-        widen(27, 1, nc.scalar.copy)
+        widen(20, 4, nc.scalar.copy)
 
         scale_slots(6)
         scale_slots(8)
         scale_slots(10)
         lay_queries(2, 2)
         lay_queries(4, 2)
-        lay_words(key4[:], key_bank)
-        widen(28, 1, nc.scalar.copy)
+        lay_words(key4[:], key_bank[:])
         turn(12)
+        lay_plain(12, 1)
         quantize_slots(6, 2)
         project_queries(6, 2)
         quantize_slots(8, FULL)
@@ -388,35 +403,38 @@ def tile_actionbindingattention_pb_w4_kernel(
         quantize_queries(2, FULL)
         quantize(key_codes[:], key_scales[:], key4[:])
         multiply_keys(0, 2)
-        widen(20, 3, nc.gpsimd.tensor_copy, rooms[1][:, 2 * FEATURES :])
+        scale_plain(13, rooms[1][:, FULL * FEATURES :])
+        widen(24, 1, nc.gpsimd.tensor_copy)
         project_queries(8, 2)
         multiply_keys(2, FULL)
         lay_queries(6, 2)
-        widen(29, 2, nc.scalar.copy)
         project_queries(10, 2)
 
-        scale_slots(12)
-        find_tops(0)
+        scale_slots(12, 1)
         scale_slots(14)
+        find_tops(0)
         turn(16)
-        turn(18)
         find_tops(2)
         lay_queries(8, 3)
         negate_tops(0)
         lay_queries(11, 1)
+        lay_plain(16, 1)
         exponentiate(0, negate=2)
-        quantize_slots(12, 2)
+        quantize_slots(12, 1)
+        quantize_slots(13, 1)
         project_queries(12, 2)
+        turn(18)
         quantize_slots(14, 2)
         quantize_queries(6, 2)
         quantize_queries(8, FULL)
-        widen(24, 3, nc.gpsimd.tensor_copy, rooms[2][:, 2 * FEATURES :])
+        scale_plain(17, rooms[2][:, 2 * FEATURES :])
+        widen(25, 1, nc.gpsimd.tensor_copy)
         multiply_keys(6, 2)
         exponentiate(2)
         project_queries(14, 2)
         multiply_keys(8, FULL)
 
-        scale_slots(16)
+        scale_slots(16, 1)
         find_tops(6)
         scale_slots(18)
         turn(20)
@@ -426,13 +444,16 @@ def tile_actionbindingattention_pb_w4_kernel(
         negate_tops(6)
         lay_queries(15, 1)
         exponentiate(6, negate=8)
-        quantize_slots(16, 2)
+        quantize_slots(16, 1)
+        quantize_slots(17, 1)
         project_queries(16, 2)
         invert_sums(0, 6)
         quantize_slots(18, 2)
         quantize_queries(12, FULL)
         divide_and_store(0, 6, nc.gpsimd, rooms[3])
         exponentiate(8)
+        widen(26, 1, nc.scalar.copy)
+        widen(27, 1, nc.scalar.copy)
         project_queries(18, 1)
         multiply_keys(12, FULL)
         project_queries(19, 1)
@@ -440,11 +461,10 @@ def tile_actionbindingattention_pb_w4_kernel(
         scale_slots(20)
         scale_slots(22)
         turn(24)
-        turn(26)
         find_tops(12)
         lay_queries(16, FULL)
         negate_tops(12)
-        widen(31, 1, nc.scalar.copy)
+        widen(28, 2, nc.scalar.copy)
         quantize_slots(20, 2)
         project_queries(20, 2)
         invert_sums(6, 6)
@@ -452,7 +472,9 @@ def tile_actionbindingattention_pb_w4_kernel(
         quantize_queries(16, FULL)
         divide_and_store(6, 6, nc.gpsimd, rooms[4])
         exponentiate(12)
+        widen(30, 2, nc.scalar.copy)
         multiply_keys(16, FULL)
+        turn(26)
         project_queries(22, 2)
 
         scale_slots(24)
@@ -466,8 +488,8 @@ def tile_actionbindingattention_pb_w4_kernel(
         turn(30, 1)
         quantize_queries(20, 2)
         multiply_keys(20, 2)
-        invert_sums(12, 4)
         quantize_slots(24, 2)
+        invert_sums(12, 4)
         project_queries(24, 2)
         exponentiate(16)
         quantize_queries(22, 2)
@@ -484,8 +506,8 @@ def tile_actionbindingattention_pb_w4_kernel(
         negate_tops(20)
         lay_queries(25, 1)
         exponentiate(20)
-        scale_slots(30, 1)
         find_tops(22)
+        scale_slots(30, 1)
         lay_queries(26, 1)
         negate_tops(22)
         lay_queries(27, 1)

@@ -93,10 +93,10 @@ def tile_actionbindingattention_pb_w4_kernel(
         nc.sync.dma_start(out=ident_rows[:], in_=ident)
         load_scales(Q, Wq_scales)
         load_slots(8, 4)
+        load_slots(12, 4)
         load_words(K, Wk_words)
-        load_slots(12, 8)
         load_scales(K, Wk_scales)
-        load_slots(20, 4)
+        load_slots(16, 8)
         load_slots(24, 3)
         load_slots(27, 5)
 
@@ -363,16 +363,17 @@ def tile_actionbindingattention_pb_w4_kernel(
         quantize_slots(0, 1)
         quantize_slots(1, 1)
         permute_scales()
-        widen(8, 3, nc.gpsimd.tensor_copy, early[0])
-        project_queries(0, 2)
+        widen(8, 2, nc.gpsimd.tensor_copy, early[0])
         turn(6)
+        project_queries(0, 2)
         lay_words(ident4[:], ident_bank[:])
-        widen(11, 1, nc.scalar.copy)
+        widen(10, 2, nc.scalar.copy)
+        widen(12, 3, nc.scalar.copy)
 
         scale_slots(2)
         lay_queries(0, 1)
         lay_queries(1, 1)
-        widen(17, 3, nc.scalar.copy)
+        widen(15, 1, nc.scalar.copy)
         scale_slots(4)
         quantize(ident_codes[:], ident_scales[:], ident4[:])
         project_keys()
@@ -381,11 +382,11 @@ def tile_actionbindingattention_pb_w4_kernel(
         project_queries(2, 2)
         turn(10, 2, logit_psum, "logits")
         quantize_slots(4, 2)
-        widen(12, 5, nc.gpsimd.tensor_copy, early[1][:, 3 * FEATURES :])
+        widen(16, 5, nc.gpsimd.tensor_copy, early[1][:, 3 * FEATURES :])
         project_queries(4, 2)
         key_bank = logit_psum.tile([P, 2, P], F32, name="logits")
         turn_rows(key_bank, key_rows[:])
-        widen(20, 4, nc.scalar.copy)
+        widen(21, 3, nc.scalar.copy)
 
         scale_slots(6)
         scale_slots(8)
@@ -404,10 +405,10 @@ def tile_actionbindingattention_pb_w4_kernel(
         quantize(key_codes[:], key_scales[:], key4[:])
         multiply_keys(0, 2)
         scale_plain(13, rooms[1][:, FULL * FEATURES :])
-        widen(24, 1, nc.gpsimd.tensor_copy)
         project_queries(8, 2)
         multiply_keys(2, FULL)
         lay_queries(6, 2)
+        widen(24, 2, nc.scalar.copy)
         project_queries(10, 2)
 
         scale_slots(12, 1)
@@ -419,7 +420,8 @@ def tile_actionbindingattention_pb_w4_kernel(
         negate_tops(0)
         lay_queries(11, 1)
         lay_plain(16, 1)
-        exponentiate(0, negate=2)
+        negate_tops(2)
+        exponentiate(0)
         quantize_slots(12, 1)
         quantize_slots(13, 1)
         project_queries(12, 2)
@@ -428,7 +430,6 @@ def tile_actionbindingattention_pb_w4_kernel(
         quantize_queries(6, 2)
         quantize_queries(8, FULL)
         scale_plain(17, rooms[2][:, 2 * FEATURES :])
-        widen(25, 1, nc.gpsimd.tensor_copy)
         multiply_keys(6, 2)
         exponentiate(2)
         project_queries(14, 2)
@@ -438,15 +439,16 @@ def tile_actionbindingattention_pb_w4_kernel(
         find_tops(6)
         scale_slots(18)
         turn(20)
-        turn(22)
         find_tops(8)
         lay_queries(12, 3)
         negate_tops(6)
         lay_queries(15, 1)
-        exponentiate(6, negate=8)
+        negate_tops(8)
+        exponentiate(6)
         quantize_slots(16, 1)
         quantize_slots(17, 1)
         project_queries(16, 2)
+        turn(22)
         invert_sums(0, 6)
         quantize_slots(18, 2)
         quantize_queries(12, FULL)

@@ -31,6 +31,7 @@ GROUPS = len(STARTS)
 WIDEST = 6
 SOFT_BUFFERS = 15
 FLIPPED = 3
+BY_PRODUCT = [2, 4, 6, 8, 10, 14, 18, 20]
 Q, K = 0, 1
 
 
@@ -102,6 +103,8 @@ def tile_actionbindingattention_pb_w4_kernel(
 
         eye = keep.tile([P, P], F32, name="eye", align_bytes=64)
         make_identity(nc, eye[:])
+        eye16 = keep.tile([P, P], BF16, name="eye16", align_bytes=64)
+        nc.vector.tensor_copy(out=eye16[:], in_=eye[:])
 
         def permute_words():
             nc.vector.tensor_copy(
@@ -146,6 +149,14 @@ def tile_actionbindingattention_pb_w4_kernel(
                 nc.tensor.transpose(dst[:, h, :], src_words[:, h::2], eye[:])
 
         def turn(first, tiles=2, pool=turn_psum, name="turned"):
+            if first in BY_PRODUCT:
+                turned[first] = pool.tile([P, PACK, tiles, P], BF16, name=name)
+                for j in range(tiles):
+                    for t in range(PACK):
+                        nc.tensor.matmul(
+                            turned[first][:, t, j, :], lhsT=wide[first + j][:, t::PACK], rhs=eye16[:], start=True, stop=True
+                        )
+                return
             turned[first] = pool.tile([P, 2, tiles, P], F32, name=name)
             for j in range(tiles):
                 turn_rows(turned[first][:, :, j, :], wide[first + j])
@@ -154,6 +165,14 @@ def tile_actionbindingattention_pb_w4_kernel(
             g, j = place(first)
             n = tiles * P
             i = 0 if held is None else first - held
+            if first - i in BY_PRODUCT:
+                nc.vector.tensor_tensor(
+                    out=slots4[g][:, j * P : j * P + n, :],
+                    in0=turned[first - i][:, :, i : i + tiles, :].rearrange("p t j r -> p (j r) t"),
+                    in1=scale4[:].unsqueeze(1).to_broadcast([P, n, PACK]),
+                    op=MULT,
+                )
+                return
             halves = turned[first - i][:, :, i : i + tiles, :].rearrange("p h j r -> p h (j r)").bitcast(BF16)
             nc.vector.tensor_tensor(
                 out=slots4[g][:, j * P : j * P + n, :].rearrange("p r (h e) -> p r h e", e=2),

@@ -31,7 +31,7 @@ GROUPS = len(STARTS)
 WIDEST = 6
 SOFT_BUFFERS = 15
 FLIPPED = 3
-BY_PRODUCT = [2, 4, 6, 8, 10, 14, 18, 20]
+BY_PRODUCT = [2, 4, 6, 20, 24]
 Q, K = 0, 1
 
 
@@ -98,8 +98,7 @@ def tile_actionbindingattention_pb_w4_kernel(
         load_words(K, Wk_words)
         load_scales(K, Wk_scales)
         load_slots(16, 8)
-        load_slots(24, 3)
-        load_slots(27, 5)
+        load_slots(24, 8)
 
         eye = keep.tile([P, P], F32, name="eye", align_bytes=64)
         make_identity(nc, eye[:])
@@ -129,6 +128,22 @@ def tile_actionbindingattention_pb_w4_kernel(
             held = (early[0][:], early[1][:, 4 * FEATURES :], early[2][:])[g] if g < 3 else scaled[g % 2][:]
             slots4[g] = held.rearrange("p (r t) -> p r t", t=PACK)
 
+        ones = keep.tile([P, 1], F32, name="ones")
+        nc.vector.memset(ones[:], 1.0)
+        in_halves = set()
+
+        def widen_in_halves(tile):
+            wide[tile] = keep.tile([P, FEATURES], BF16, name="wide_%d" % tile, align_bytes=64)[:]
+            held, j = raw_bytes[tile]
+            nc.vector.tensor_scalar(
+                out=wide[tile].rearrange("p (h q e) -> p q h e", h=2, e=2),
+                in0=held[:, j, :].bitcast(FP8).rearrange("p (q h e) -> p q h e", h=2, e=2),
+                scalar1=ones[:],
+                scalar2=None,
+                op0=MULT,
+            )
+            in_halves.add(tile)
+
         def widen(first, tiles, copy, room=None):
             if room is None:
                 room = keep.tile([P, tiles * FEATURES], BF16, name="wide_%d" % first, align_bytes=64)
@@ -143,10 +158,10 @@ def tile_actionbindingattention_pb_w4_kernel(
         def copy_by_activation(out, in_):
             nc.scalar.activation(out=out, in_=in_, func=COPY)
 
-        def turn_rows(dst, src):
+        def turn_rows(dst, src, halves=False):
             src_words = src.bitcast(F32)
             for h in range(2):
-                nc.tensor.transpose(dst[:, h, :], src_words[:, h::2], eye[:])
+                nc.tensor.transpose(dst[:, h, :], src_words[:, h * P : (h + 1) * P] if halves else src_words[:, h::2], eye[:])
 
         def turn(first, tiles=2, pool=turn_psum, name="turned"):
             if first in BY_PRODUCT:
@@ -159,7 +174,7 @@ def tile_actionbindingattention_pb_w4_kernel(
                 return
             turned[first] = pool.tile([P, 2, tiles, P], F32, name=name)
             for j in range(tiles):
-                turn_rows(turned[first][:, :, j, :], wide[first + j])
+                turn_rows(turned[first][:, :, j, :], wide[first + j], first + j in in_halves)
 
         def scale_slots(first, tiles=2, held=None):
             g, j = place(first)
@@ -353,8 +368,8 @@ def tile_actionbindingattention_pb_w4_kernel(
                 stop=True,
             )
             nc.scalar.copy(
-                out=key_rows[:].rearrange("p (m i t) -> p m i t", i=PACK, t=PACK),
-                in_=bank[:].rearrange("p (m t i) -> p m i t", i=PACK, t=PACK),
+                out=key_rows[:].rearrange("p (h m i e) -> p h m i e", h=2, i=PACK, e=2),
+                in_=bank[:].rearrange("p (m h e i) -> p h m i e", h=2, i=PACK, e=2),
             )
 
         def lay_words(dst, bank):
@@ -364,9 +379,9 @@ def tile_actionbindingattention_pb_w4_kernel(
             )
 
 
-        widen(0, 1, nc.vector.tensor_copy)
+        widen_in_halves(0)
         turn(0, 1)
-        widen(1, 1, nc.vector.tensor_copy)
+        widen_in_halves(1)
         turn(1, 1)
         widen(2, 1, nc.vector.tensor_copy)
         widen(3, 1, copy_by_activation)
@@ -395,8 +410,8 @@ def tile_actionbindingattention_pb_w4_kernel(
         widen(15, 1, nc.scalar.copy)
         scale_slots(4)
         quantize(ident_codes[:], ident_scales[:], ident4[:])
-        project_keys()
         turn(8)
+        project_keys()
         quantize_slots(2, 2)
         project_queries(2, 2)
         turn(10, 2, logit_psum, "logits")
@@ -404,7 +419,7 @@ def tile_actionbindingattention_pb_w4_kernel(
         widen(16, 5, nc.gpsimd.tensor_copy, early[1][:, 3 * FEATURES :])
         project_queries(4, 2)
         key_bank = logit_psum.tile([P, 2, P], F32, name="logits")
-        turn_rows(key_bank, key_rows[:])
+        turn_rows(key_bank, key_rows[:], True)
         widen(21, 3, nc.scalar.copy)
 
         scale_slots(6)
@@ -422,9 +437,9 @@ def tile_actionbindingattention_pb_w4_kernel(
         turn(14)
         quantize_queries(2, FULL)
         quantize(key_codes[:], key_scales[:], key4[:])
-        multiply_keys(0, 2)
         scale_plain(13, rooms[1][:, FULL * FEATURES :])
         project_queries(8, 2)
+        multiply_keys(0, 2)
         multiply_keys(2, FULL)
         lay_queries(6, 2)
         widen(24, 2, nc.scalar.copy)
@@ -455,8 +470,8 @@ def tile_actionbindingattention_pb_w4_kernel(
         multiply_keys(8, FULL)
 
         scale_slots(16, 1)
-        find_tops(6)
         scale_slots(18)
+        find_tops(6)
         turn(20)
         find_tops(8)
         lay_queries(12, 3)
@@ -466,24 +481,24 @@ def tile_actionbindingattention_pb_w4_kernel(
         exponentiate(6)
         quantize_slots(16, 1)
         quantize_slots(17, 1)
-        project_queries(16, 2)
         turn(22)
+        project_queries(16, 2)
         invert_sums(0, 6)
         quantize_slots(18, 2)
         quantize_queries(12, FULL)
         divide_and_store(0, 6, nc.gpsimd, rooms[3])
         exponentiate(8)
-        widen(26, 1, nc.scalar.copy)
-        widen(27, 1, nc.scalar.copy)
-        project_queries(18, 1)
         multiply_keys(12, FULL)
+        project_queries(18, 1)
         project_queries(19, 1)
 
         scale_slots(20)
         scale_slots(22)
         turn(24)
         find_tops(12)
-        lay_queries(16, FULL)
+        lay_queries(16, 2)
+        widen(26, 2, nc.scalar.copy)
+        lay_queries(18, 2)
         negate_tops(12)
         widen(28, 2, nc.scalar.copy)
         quantize_slots(20, 2)

@@ -76,9 +76,9 @@ def tile_actionbindingattention_pb_w4_kernel(
         def load_words(w, w_words):
             nc.sync.dma_start(out=words_in[:, w, :].bitcast(I32), in_=w_words[0].bitcast(I32))
 
-        def load_scales(w, w_scales):
+        def load_scales(w, w_scales, queue):
             for a in range(4):
-                nc.sync.dma_start(
+                queue.dma_start(
                     out=scales_in[32 * a : 32 * a + 4, w, :].bitcast(I32),
                     in_=w_scales[0, 4 * a : 4 * a + 4, :].bitcast(I32),
                 )
@@ -91,14 +91,15 @@ def tile_actionbindingattention_pb_w4_kernel(
         load_slots(2, 2)
         load_words(Q, Wq_words)
         load_slots(4, 4)
+        load_scales(Q, Wq_scales, nc.sync)
         nc.sync.dma_start(out=ident_rows[:], in_=ident)
-        load_scales(Q, Wq_scales)
         load_slots(8, 4)
         load_slots(12, 4)
+        load_slots(16, 4)
         load_words(K, Wk_words)
-        load_scales(K, Wk_scales)
-        load_slots(16, 8)
-        load_slots(24, 8)
+        load_scales(K, Wk_scales, nc.sync)
+        load_slots(20, 6)
+        load_slots(26, 6)
 
         eye = keep.tile([P, P], F32, name="eye", align_bytes=64)
         make_identity(nc, eye[:])
@@ -198,16 +199,16 @@ def tile_actionbindingattention_pb_w4_kernel(
 
         plain4, late4 = {}, {}
 
-        def lay_plain(first, j):
-            plain4[first + j] = keep.tile([P, P, PACK], BF16, name="plain_%d" % (first + j), align_bytes=64)
-            lay_words(plain4[first + j][:], turned[first][:, :, j, :])
+        def lay_plain(first):
+            plain4[first] = keep.tile([P, 2 * P, PACK], BF16, name="plain_%d" % first, align_bytes=64)
+            lay_words(plain4[first][:], turned[first][:].rearrange("p h j r -> p h (j r)"))
 
         def scale_plain(tile, room):
-            late4[tile] = room[:, :FEATURES].rearrange("p (r t) -> p r t", t=PACK)
+            late4[tile] = room[:, : 2 * FEATURES].rearrange("p (r t) -> p r t", t=PACK)
             nc.gpsimd.tensor_tensor(
                 out=late4[tile],
                 in0=plain4[tile][:],
-                in1=scale4[:].unsqueeze(1).to_broadcast([P, P, PACK]),
+                in1=scale4[:].unsqueeze(1).to_broadcast([P, 2 * P, PACK]),
                 op=MULT,
             )
 
@@ -402,12 +403,12 @@ def tile_actionbindingattention_pb_w4_kernel(
         project_queries(0, 2)
         lay_words(ident4[:], ident_bank[:])
         widen(10, 2, nc.scalar.copy)
-        widen(12, 3, nc.scalar.copy)
+        widen(12, 4, nc.scalar.copy)
 
         scale_slots(2)
         lay_queries(0, 1)
         lay_queries(1, 1)
-        widen(15, 1, nc.scalar.copy)
+        widen(16, 1, nc.scalar.copy)
         scale_slots(4)
         quantize(ident_codes[:], ident_scales[:], ident4[:])
         turn(8)
@@ -416,20 +417,21 @@ def tile_actionbindingattention_pb_w4_kernel(
         project_queries(2, 2)
         turn(10, 2, logit_psum, "logits")
         quantize_slots(4, 2)
-        widen(16, 5, nc.gpsimd.tensor_copy, early[1][:, 3 * FEATURES :])
-        project_queries(4, 2)
+        widen(20, 5, nc.gpsimd.tensor_copy, early[1][:, 3 * FEATURES :])
         key_bank = logit_psum.tile([P, 2, P], F32, name="logits")
         turn_rows(key_bank, key_rows[:], True)
-        widen(21, 3, nc.scalar.copy)
+        widen(17, 3, nc.scalar.copy)
 
         scale_slots(6)
+        turn(12)
+        project_queries(4, 2)
         scale_slots(8)
         scale_slots(10)
         lay_queries(2, 2)
         lay_queries(4, 2)
         lay_words(key4[:], key_bank[:])
-        turn(12)
-        lay_plain(12, 1)
+        turn(18, 2, logit_psum, "logits")
+        lay_plain(18)
         quantize_slots(6, 2)
         project_queries(6, 2)
         quantize_slots(8, FULL)
@@ -437,15 +439,15 @@ def tile_actionbindingattention_pb_w4_kernel(
         turn(14)
         quantize_queries(2, FULL)
         quantize(key_codes[:], key_scales[:], key4[:])
-        scale_plain(13, rooms[1][:, FULL * FEATURES :])
+        scale_plain(18, rooms[1][:, FULL * FEATURES :])
         project_queries(8, 2)
         multiply_keys(0, 2)
         multiply_keys(2, FULL)
         lay_queries(6, 2)
-        widen(24, 2, nc.scalar.copy)
+        widen(25, 1, nc.scalar.copy)
         project_queries(10, 2)
 
-        scale_slots(12, 1)
+        scale_slots(12)
         scale_slots(14)
         find_tops(0)
         turn(16)
@@ -453,34 +455,29 @@ def tile_actionbindingattention_pb_w4_kernel(
         lay_queries(8, 3)
         negate_tops(0)
         lay_queries(11, 1)
-        lay_plain(16, 1)
         negate_tops(2)
         exponentiate(0)
-        quantize_slots(12, 1)
-        quantize_slots(13, 1)
+        quantize_slots(12, 2)
         project_queries(12, 2)
-        turn(18)
         quantize_slots(14, 2)
         quantize_queries(6, 2)
         quantize_queries(8, FULL)
-        scale_plain(17, rooms[2][:, 2 * FEATURES :])
+        widen(26, 2, nc.gpsimd.tensor_copy, rooms[2][:, 2 * FEATURES :])
         multiply_keys(6, 2)
         exponentiate(2)
         project_queries(14, 2)
         multiply_keys(8, FULL)
 
-        scale_slots(16, 1)
-        scale_slots(18)
+        scale_slots(16)
         find_tops(6)
         turn(20)
         find_tops(8)
         lay_queries(12, 3)
-        negate_tops(6)
         lay_queries(15, 1)
+        negate_tops(6)
         negate_tops(8)
         exponentiate(6)
-        quantize_slots(16, 1)
-        quantize_slots(17, 1)
+        quantize_slots(16, 2)
         turn(22)
         project_queries(16, 2)
         invert_sums(0, 6)
@@ -497,7 +494,6 @@ def tile_actionbindingattention_pb_w4_kernel(
         turn(24)
         find_tops(12)
         lay_queries(16, 2)
-        widen(26, 2, nc.scalar.copy)
         lay_queries(18, 2)
         negate_tops(12)
         widen(28, 2, nc.scalar.copy)

@@ -323,6 +323,10 @@ def tile_actionbindingattention_pb_w4_kernel(
             cols = slice(2 * first, 2 * (first + tiles))
             nc.vector.reciprocal(out=inverses[:, cols], in_=sums[:, cols])
 
+        def store(first, tiles, queue=nc.sync):
+            cols = slice(2 * first, 2 * (first + tiles))
+            queue.dma_start(out=out[cols].rearrange("b n s -> n b s"), in_=shares[:, cols, :])
+
         def divide_and_store(first, tiles, engine=None, room=None, negate=None, queue=nc.sync):
             start, samples = 2 * first, 2 * tiles
             cols = slice(start, start + samples)
@@ -347,7 +351,8 @@ def tile_actionbindingattention_pb_w4_kernel(
                     in1=inverses[:, cols].unsqueeze(2).to_broadcast([P, samples, SLOTS]),
                     op=MULT,
                 )
-            queue.dma_start(out=out[cols].rearrange("b n s -> n b s"), in_=dst)
+            if queue is not None:
+                queue.dma_start(out=out[cols].rearrange("b n s -> n b s"), in_=dst)
 
         ident4 = keep.tile([P, P, PACK], BF16, name="ident4", align_bytes=64)
         ident_codes = keep.tile([P, P], U32, name="ident_codes", align_bytes=64)
@@ -586,7 +591,8 @@ def tile_actionbindingattention_pb_w4_kernel(
         divide_and_store(26, 2, nc.vector)
         invert_sums(30, 1)
         invert_sums(28, 2)
-        divide_and_store(30, 1, queue=nc.scalar)
+        divide_and_store(30, 1, queue=None)
         invert_sums(31, 1)
-        divide_and_store(28, 2, nc.vector)
-        divide_and_store(31, 1, nc.vector)
+        divide_and_store(28, 2, nc.vector, queue=None)
+        divide_and_store(31, 1, nc.vector, queue=None)
+        store(28, 4)

@@ -31,7 +31,7 @@ GROUPS = len(STARTS)
 WIDEST = 6
 SOFT_BUFFERS = 15
 FLIPPED = 3
-BY_PRODUCT = [2, 4, 6, 20, 24]
+BY_PRODUCT = [2, 4, 6, 16, 20, 24]
 Q, K = 0, 1
 
 
@@ -98,10 +98,15 @@ def tile_actionbindingattention_pb_w4_kernel(
         load_slots(16, 4)
         load_words(K, Wk_words)
         load_scales(K, Wk_scales, nc.sync)
-        load_slots(20, 6)
-        load_slots(26, 6)
+        load_slots(20, 5)
+        load_slots(25, 7)
 
         eye = keep.tile([P, P], F32, name="eye", align_bytes=64)
+        zeros = keep.tile([P, FEATURES], BF16, name="zeros", align_bytes=64)
+        nc.vector.memset(zeros[:], 0.0)
+        warm_bank = proj_psum.tile([P, FEATURES], F32, name="proj")
+        for i in range(3):
+            nc.tensor.matmul(warm_bank[:], lhsT=zeros[:, :P], rhs=zeros[:], start=True, stop=True)
         make_identity(nc, eye[:])
         eye16 = keep.tile([P, P], BF16, name="eye16", align_bytes=64)
         nc.vector.tensor_copy(out=eye16[:], in_=eye[:])
@@ -323,9 +328,9 @@ def tile_actionbindingattention_pb_w4_kernel(
             cols = slice(2 * first, 2 * (first + tiles))
             nc.vector.reciprocal(out=inverses[:, cols], in_=sums[:, cols])
 
-        def store(first, tiles, queue=nc.sync):
+        def store(first, tiles):
             cols = slice(2 * first, 2 * (first + tiles))
-            queue.dma_start(out=out[cols].rearrange("b n s -> n b s"), in_=shares[:, cols, :])
+            nc.sync.dma_start(out=out[cols].rearrange("b n s -> n b s"), in_=shares[:, cols, :])
 
         def divide_and_store(first, tiles, engine=None, room=None, negate=None, queue=nc.sync):
             start, samples = 2 * first, 2 * tiles
@@ -422,7 +427,7 @@ def tile_actionbindingattention_pb_w4_kernel(
         project_queries(2, 2)
         turn(10, 2, logit_psum, "logits")
         quantize_slots(4, 2)
-        widen(20, 5, nc.gpsimd.tensor_copy, early[1][:, 3 * FEATURES :])
+        widen(20, 4, nc.gpsimd.tensor_copy, early[1][:, 4 * FEATURES :])
         key_bank = logit_psum.tile([P, 2, P], F32, name="logits")
         turn_rows(key_bank, key_rows[:], True)
         widen(17, 3, nc.scalar.copy)
@@ -449,7 +454,7 @@ def tile_actionbindingattention_pb_w4_kernel(
         multiply_keys(0, 2)
         multiply_keys(2, FULL)
         lay_queries(6, 2)
-        widen(25, 1, nc.scalar.copy)
+        widen(24, 1, nc.scalar.copy)
         project_queries(10, 2)
 
         scale_slots(12)
@@ -467,7 +472,7 @@ def tile_actionbindingattention_pb_w4_kernel(
         quantize_slots(14, 2)
         quantize_queries(6, 2)
         quantize_queries(8, FULL)
-        widen(26, 2, nc.gpsimd.tensor_copy, rooms[2][:, 2 * FEATURES :])
+        widen(25, 3, nc.gpsimd.tensor_copy, rooms[2][:, 3 * FEATURES :])
         multiply_keys(6, 2)
         exponentiate(2)
         project_queries(14, 2)

@@ -328,10 +328,6 @@ def tile_actionbindingattention_pb_w4_kernel(
             cols = slice(2 * first, 2 * (first + tiles))
             nc.vector.reciprocal(out=inverses[:, cols], in_=sums[:, cols])
 
-        def store(first, tiles):
-            cols = slice(2 * first, 2 * (first + tiles))
-            nc.sync.dma_start(out=out[cols].rearrange("b n s -> n b s"), in_=shares[:, cols, :])
-
         def divide_and_store(first, tiles, engine=None, room=None, negate=None, queue=nc.sync):
             start, samples = 2 * first, 2 * tiles
             cols = slice(start, start + samples)
@@ -356,8 +352,7 @@ def tile_actionbindingattention_pb_w4_kernel(
                     in1=inverses[:, cols].unsqueeze(2).to_broadcast([P, samples, SLOTS]),
                     op=MULT,
                 )
-            if queue is not None:
-                queue.dma_start(out=out[cols].rearrange("b n s -> n b s"), in_=dst)
+            queue.dma_start(out=out[cols].rearrange("b n s -> n b s"), in_=dst)
 
         ident4 = keep.tile([P, P, PACK], BF16, name="ident4", align_bytes=64)
         ident_codes = keep.tile([P, P], U32, name="ident_codes", align_bytes=64)
@@ -596,8 +591,7 @@ def tile_actionbindingattention_pb_w4_kernel(
         divide_and_store(26, 2, nc.vector)
         invert_sums(30, 1)
         invert_sums(28, 2)
-        divide_and_store(30, 1, queue=None)
+        divide_and_store(30, 1, queue=nc.scalar)
         invert_sums(31, 1)
-        divide_and_store(28, 2, nc.vector, queue=None)
-        divide_and_store(31, 1, nc.vector, queue=None)
-        store(28, 4)
+        divide_and_store(28, 2, nc.vector)
+        divide_and_store(31, 1, nc.vector)

@@ -102,11 +102,6 @@ def tile_actionbindingattention_pb_w4_kernel(
         load_slots(25, 7)
 
         eye = keep.tile([P, P], F32, name="eye", align_bytes=64)
-        zeros = keep.tile([P, FEATURES], BF16, name="zeros", align_bytes=64)
-        nc.vector.memset(zeros[:], 0.0)
-        warm_bank = proj_psum.tile([P, FEATURES], F32, name="proj")
-        for i in range(3):
-            nc.tensor.matmul(warm_bank[:], lhsT=zeros[:, :P], rhs=zeros[:], start=True, stop=True)
         make_identity(nc, eye[:])
         eye16 = keep.tile([P, P], BF16, name="eye16", align_bytes=64)
         nc.vector.tensor_copy(out=eye16[:], in_=eye[:])

from contextlib import ExitStack

import concourse.mybir as mybir
from concourse.masks import make_identity

F32 = mybir.dt.float32
BF16 = mybir.dt.bfloat16
I32 = mybir.dt.int32
U32 = mybir.dt.uint32
U8 = mybir.dt.uint8
FP8 = mybir.dt.float8_e4m3fn
FP8X4 = mybir.dt.float8_e4m3fn_x4
FP4X4 = mybir.dt.float4_e2m1fn_x4
MULT = mybir.AluOpType.mult
MAX = mybir.AluOpType.max
MIN = mybir.AluOpType.min
AXIS_X = mybir.AxisListType.X
COPY = mybir.ActivationFunctionType.Copy
EXP = mybir.ActivationFunctionType.Exp

P = 128
PACK = 4
SAMPLES, SLOTS, FEATURES, OBJECTS = 64, 64, 512, 128
FLOPS = 2 * SAMPLES * SLOTS * FEATURES**2 + 2 * OBJECTS * FEATURES**2 + 2 * SAMPLES * OBJECTS * SLOTS * FEATURES
LOGIT_SCALE = float(FEATURES) ** -0.5

TILES = SAMPLES * SLOTS // P
FULL = 4
STARTS = [0, 2, 6] + list(range(12, TILES, FULL))
GROUPS = len(STARTS)
WIDEST = 6
SOFT_BUFFERS = 15
FLIPPED = 3
BY_PRODUCT = [2, 4, 6, 16, 20, 24]
Q, K = 0, 1


def place(tile):
    g = sum(start <= tile for start in STARTS) - 1
    return g, tile - STARTS[g]


def group_size(g):
    return (STARTS + [TILES])[g + 1] - STARTS[g]


def tile_actionbindingattention_pb_w4_kernel(
    tc, slots_bytes, slots_scale, ident, Wq_words, Wq_scales, Wk_words, Wk_scales, out
):
    nc = tc.nc
    with ExitStack() as ctx:
        keep = ctx.enter_context(tc.tile_pool(name="keep", bufs=1))
        work = ctx.enter_context(tc.tile_pool(name="work", bufs=3))
        soft = ctx.enter_context(tc.tile_pool(name="soft", bufs=FLIPPED))
        turn_psum = ctx.enter_context(tc.psum_pool(name="turn_psum", bufs=2))
        proj_psum = ctx.enter_context(tc.psum_pool(name="proj_psum", bufs=4))
        logit_psum = ctx.enter_context(tc.psum_pool(name="logit_psum", bufs=2))
        ctx.enter_context(tc.manual_schedule())

        raw_bytes = {}
        rows = slots_bytes.rearrange("b s k -> (b s) k")

        def load_slots(first, tiles):
            held = keep.tile([P, tiles, FEATURES], U8, name="slots_%d" % first, align_bytes=64)
            src = rows[first * P : (first + tiles) * P, :]
            nc.sync.dma_start(out=held[:], in_=src.rearrange("(j p) k -> p j k", p=P))
            for j in range(tiles):
                raw_bytes[first + j] = (held, j)

        words_in = keep.tile([P, 2, 2 * FEATURES], U8, name="words_in", align_bytes=64)
        scales_in = keep.tile([P, 2, FEATURES], U8, name="scales_in", align_bytes=64)
        wq_words = keep.tile([P, 2 * FEATURES], U8, name="wq_words", align_bytes=64)
        wq_scales = keep.tile([P, FEATURES], U8, name="wq_scales", align_bytes=64)
        nc.vector.memset(scales_in[:].rearrange("p w n -> p (w n)").bitcast(I32), 0)

        def load_words(w, w_words):
            nc.sync.dma_start(out=words_in[:, w, :].bitcast(I32), in_=w_words[0].bitcast(I32))

        def load_scales(w, w_scales, queue):
            for a in range(4):
                queue.dma_start(
                    out=scales_in[32 * a : 32 * a + 4, w, :].bitcast(I32),
                    in_=w_scales[0, 4 * a : 4 * a + 4, :].bitcast(I32),
                )

        scale4 = keep.tile([P, PACK], F32, name="scale4")
        ident_rows = keep.tile([P, FEATURES], BF16, name="ident_rows", align_bytes=64)
        load_slots(0, 1)
        nc.scalar.dma_start(out=scale4[:], in_=slots_scale.rearrange("a b (p t) -> p (a b t)", t=PACK))
        load_slots(1, 1)
        load_slots(2, 2)
        load_words(Q, Wq_words)
        load_slots(4, 4)
        load_scales(Q, Wq_scales, nc.sync)
        nc.sync.dma_start(out=ident_rows[:], in_=ident)
        load_slots(8, 4)
        load_slots(12, 4)
        load_slots(16, 4)
        load_words(K, Wk_words)
        load_scales(K, Wk_scales, nc.sync)
        load_slots(20, 5)
        load_slots(25, 7)

        eye = keep.tile([P, P], F32, name="eye", align_bytes=64)
        make_identity(nc, eye[:])
        eye16 = keep.tile([P, P], BF16, name="eye16", align_bytes=64)
        nc.vector.tensor_copy(out=eye16[:], in_=eye[:])

        def permute_words():
            nc.vector.tensor_copy(
                out=wq_words[:].bitcast(I32).rearrange("p (t m e) -> p t m e", t=PACK, e=2),
                in_=words_in[:, Q, :].bitcast(I32).rearrange("p (m t e) -> p t m e", t=PACK, e=2),
            )

        def permute_scales():
            nc.gpsimd.tensor_copy(
                out=wq_scales[:].bitcast(I32).rearrange("p (t m) -> p t m", t=PACK),
                in_=scales_in[:, Q, :].bitcast(I32).rearrange("p (m t) -> p t m", t=PACK),
            )

        wide, turned, slots4, slots_q, proj, query4, query_q = {}, {}, {}, {}, {}, {}, {}
        logits, flipped = {}, {}

        rooms = [keep.tile([P, WIDEST * FEATURES], BF16, name="room_%d" % g, align_bytes=64) for g in range(GROUPS)]
        early = [keep.tile([P, n * FEATURES], BF16, name="early_%d" % n, align_bytes=64) for n in (3, 8, 6)]
        scaled = [keep.tile([P, FULL * FEATURES], BF16, name="scaled_%d" % i, align_bytes=64) for i in range(2)]
        for g in range(GROUPS):
            query4[g] = rooms[g][:].rearrange("p (r t) -> p r t", t=PACK)
            held = (early[0][:], early[1][:, 4 * FEATURES :], early[2][:])[g] if g < 3 else scaled[g % 2][:]
            slots4[g] = held.rearrange("p (r t) -> p r t", t=PACK)

        ones = keep.tile([P, 1], F32, name="ones")
        nc.vector.memset(ones[:], 1.0)
        in_halves = set()

        def widen_in_halves(tile):
            wide[tile] = keep.tile([P, FEATURES], BF16, name="wide_%d" % tile, align_bytes=64)[:]
            held, j = raw_bytes[tile]
            nc.vector.tensor_scalar(
                out=wide[tile].rearrange("p (h q e) -> p q h e", h=2, e=2),
                in0=held[:, j, :].bitcast(FP8).rearrange("p (q h e) -> p q h e", h=2, e=2),
                scalar1=ones[:],
                scalar2=None,
                op0=MULT,
            )
            in_halves.add(tile)

        def widen(first, tiles, copy, room=None):
            if room is None:
                room = keep.tile([P, tiles * FEATURES], BF16, name="wide_%d" % first, align_bytes=64)
            held, j = raw_bytes[first]
            copy(
                out=room[:, : tiles * FEATURES],
                in_=held[:, j : j + tiles, :].rearrange("p j k -> p (j k)").bitcast(FP8),
            )
            for tile in range(first, first + tiles):
                wide[tile] = room[:, (tile - first) * FEATURES : (tile - first + 1) * FEATURES]

        def copy_by_activation(out, in_):
            nc.scalar.activation(out=out, in_=in_, func=COPY)

        def turn_rows(dst, src, halves=False):
            src_words = src.bitcast(F32)
            for h in range(2):
                nc.tensor.transpose(dst[:, h, :], src_words[:, h * P : (h + 1) * P] if halves else src_words[:, h::2], eye[:])

        def turn(first, tiles=2, pool=turn_psum, name="turned"):
            if first in BY_PRODUCT:
                turned[first] = pool.tile([P, PACK, tiles, P], BF16, name=name)
                for j in range(tiles):
                    for t in range(PACK):
                        nc.tensor.matmul(
                            turned[first][:, t, j, :], lhsT=wide[first + j][:, t::PACK], rhs=eye16[:], start=True, stop=True
                        )
                return
            turned[first] = pool.tile([P, 2, tiles, P], F32, name=name)
            for j in range(tiles):
                turn_rows(turned[first][:, :, j, :], wide[first + j], first + j in in_halves)

        def scale_slots(first, tiles=2, held=None):
            g, j = place(first)
            n = tiles * P
            i = 0 if held is None else first - held
            if first - i in BY_PRODUCT:
                nc.vector.tensor_tensor(
                    out=slots4[g][:, j * P : j * P + n, :],
                    in0=turned[first - i][:, :, i : i + tiles, :].rearrange("p t j r -> p (j r) t"),
                    in1=scale4[:].unsqueeze(1).to_broadcast([P, n, PACK]),
                    op=MULT,
                )
                return
            halves = turned[first - i][:, :, i : i + tiles, :].rearrange("p h j r -> p h (j r)").bitcast(BF16)
            nc.vector.tensor_tensor(
                out=slots4[g][:, j * P : j * P + n, :].rearrange("p r (h e) -> p r h e", e=2),
                in0=halves.rearrange("p h (r e) -> p r h e", e=2),
                in1=scale4[:].rearrange("p (h e) -> p h e", e=2).unsqueeze(1).to_broadcast([P, n, 2, 2]),
                op=MULT,
            )

        plain4, late4 = {}, {}

        def lay_plain(first):
            plain4[first] = keep.tile([P, 2 * P, PACK], BF16, name="plain_%d" % first, align_bytes=64)
            lay_words(plain4[first][:], turned[first][:].rearrange("p h j r -> p h (j r)"))

        def scale_plain(tile, room):
            late4[tile] = room[:, : 2 * FEATURES].rearrange("p (r t) -> p r t", t=PACK)
            nc.gpsimd.tensor_tensor(
                out=late4[tile],
                in0=plain4[tile][:],
                in1=scale4[:].unsqueeze(1).to_broadcast([P, 2 * P, PACK]),
                op=MULT,
            )

        def quantize(codes, code_scales, rows4):
            nc.vector.quantize_mx(
                out=codes.bitcast(FP8X4), scales=code_scales, in_=rows4.rearrange("p r t -> p (r t)")
            )

        def quantize_tiles(made, names, src, first, tiles):
            g, j = place(first)
            if g not in made:
                made[g] = (
                    work.tile([P, group_size(g) * P], U32, name=names[0], align_bytes=64),
                    work.tile([P, group_size(g) * P], U8, name=names[1], align_bytes=64),
                )
            codes, code_scales = made[g]
            cols = slice(P * j, P * (j + tiles))
            quantize(codes[:, cols], code_scales[:, cols], late4[first] if names[0] == "slot_codes" and first in late4 else src[g][:, cols, :])

        def quantize_slots(first, tiles):
            quantize_tiles(slots_q, ("slot_codes", "slot_scales"), slots4, first, tiles)

        def quantize_queries(first, tiles):
            quantize_tiles(query_q, ("query_codes", "query_scales"), query4, first, tiles)

        def project_queries(first, tiles):
            for tile in range(first, first + tiles):
                g, j = place(tile)
                codes, code_scales = slots_q[g]
                cols = slice(P * j, P * (j + 1))
                proj[tile] = proj_psum.tile([P, PACK, P], F32, name="proj")
                for t in range(PACK):
                    nc.tensor.matmul_mx(
                        out=proj[tile][:, t, :],
                        lhsT=wq_words[:, 2 * P * t : 2 * P * (t + 1)].bitcast(FP4X4),
                        lhsT_scale=wq_scales[:, P * t : P * (t + 1)],
                        rhs=codes[:, cols].bitcast(FP8X4),
                        rhs_scale=code_scales[:, cols],
                        start=True,
                        stop=True,
                    )

        def lay_queries(first, tiles, copy=nc.scalar.copy):
            for tile in range(first, first + tiles):
                g, j = place(tile)
                copy(out=query4[g][:, j * P : (j + 1) * P, :], in_=proj[tile][:].rearrange("p t r -> p r t"))

        def multiply_keys(first, tiles, pool=logit_psum, name="logits"):
            logits[first] = pool.tile([P, 2 * tiles, SLOTS], F32, name=name)
            g, j = place(first)
            codes, code_scales = query_q[g]
            cols = slice(P * j, P * (j + tiles))
            nc.tensor.matmul_mx(
                out=logits[first][:].rearrange("p b s -> p (b s)"),
                lhsT=key_codes[:].bitcast(FP8X4),
                lhsT_scale=key_scales[:],
                rhs=codes[:, cols].bitcast(FP8X4),
                rhs_scale=code_scales[:, cols],
                start=True,
                stop=True,
            )

        tops = keep.tile([P, SAMPLES], F32, name="tops")
        biases = keep.tile([P, SAMPLES], F32, name="biases")
        sums = keep.tile([P, SAMPLES], F32, name="sums")
        inverses = keep.tile([P, SAMPLES], F32, name="inverses")
        exps = keep.tile([P, SAMPLES, SLOTS], F32, name="exps")
        shares = keep.tile([P, SAMPLES, SLOTS], F32, name="shares")

        def samples_of(first):
            return slice(2 * first, 2 * first + logits[first].shape[1])

        def find_tops(first):
            nc.vector.tensor_reduce(out=tops[:, samples_of(first)], in_=logits[first][:], axis=AXIS_X, op=MAX)

        def negate_tops(first):
            nc.scalar.activation(
                out=biases[:, samples_of(first)], in_=tops[:, samples_of(first)], func=COPY, scale=-LOGIT_SCALE
            )

        def flip_logits(first):
            samples = logits[first].shape[1]
            flipped[first] = soft.tile([P, samples, SLOTS], F32, name="flipped", bufs=FLIPPED)
            for b in range(samples):
                nc.vector.tensor_scalar(
                    out=flipped[first][:, b, :],
                    in0=logits[first][:, b, :],
                    scalar1=-LOGIT_SCALE,
                    scalar2=None,
                    op0=MULT,
                    op1=MIN,
                    accum_out=biases[:, 2 * first + b : 2 * first + b + 1],
                )

        def exponentiate(first, negate=None, part=None):
            start, samples = part or (0, logits[first].shape[1])
            src, factor = (flipped[first], -1.0) if first in flipped else (logits[first], LOGIT_SCALE)
            for b in range(start, start + samples):
                if negate is not None and b == start + samples - 2:
                    negate_tops(negate)
                sample = 2 * first + b
                nc.scalar.activation(
                    out=exps[:, sample, :],
                    in_=src[:, b, :],
                    func=EXP,
                    bias=biases[:, sample : sample + 1],
                    scale=factor,
                    accum_out=sums[:, sample : sample + 1],
                )

        def invert_sums(first, tiles):
            cols = slice(2 * first, 2 * (first + tiles))
            nc.vector.reciprocal(out=inverses[:, cols], in_=sums[:, cols])

        def divide_and_store(first, tiles, engine=None, room=None, negate=None, queue=nc.sync):
            start, samples = 2 * first, 2 * tiles
            cols = slice(start, start + samples)
            if room is None:
                dst = shares[:, cols, :]
            else:
                dst = room[:].bitcast(F32)[:, : samples * SLOTS].rearrange("p (b s) -> p b s", s=SLOTS)
            if engine is None:
                for b in range(samples):
                    if negate is not None and b == samples - 3:
                        negate_tops(negate)
                    nc.scalar.activation(
                        out=dst[:, b, :],
                        in_=exps[:, start + b, :],
                        func=COPY,
                        scale=inverses[:, start + b : start + b + 1],
                    )
            else:
                engine.tensor_tensor(
                    out=dst,
                    in0=exps[:, cols, :],
                    in1=inverses[:, cols].unsqueeze(2).to_broadcast([P, samples, SLOTS]),
                    op=MULT,
                )
            queue.dma_start(out=out[cols].rearrange("b n s -> n b s"), in_=dst)

        ident4 = keep.tile([P, P, PACK], BF16, name="ident4", align_bytes=64)
        ident_codes = keep.tile([P, P], U32, name="ident_codes", align_bytes=64)
        ident_scales = keep.tile([P, P], U8, name="ident_scales", align_bytes=64)
        key_rows = keep.tile([P, FEATURES], BF16, name="key_rows", align_bytes=64)
        key4 = rooms[1][:, FULL * FEATURES : (FULL + 1) * FEATURES].rearrange("p (r t) -> p r t", t=PACK)
        key_codes = keep.tile([P, P], U32, name="key_codes", align_bytes=64)
        key_scales = keep.tile([P, P], U8, name="key_scales", align_bytes=64)

        def project_keys():
            bank = logit_psum.tile([P, FEATURES], F32, name="logits")
            nc.tensor.matmul_mx(
                out=bank[:],
                lhsT=ident_codes[:].bitcast(FP8X4),
                lhsT_scale=ident_scales[:],
                rhs=words_in[:, K, :].bitcast(FP4X4),
                rhs_scale=scales_in[:, K, :],
                start=True,
                stop=True,
            )
            nc.scalar.copy(
                out=key_rows[:].rearrange("p (h m i e) -> p h m i e", h=2, i=PACK, e=2),
                in_=bank[:].rearrange("p (m h e i) -> p h m i e", h=2, i=PACK, e=2),
            )

        def lay_words(dst, bank):
            nc.scalar.copy(
                out=dst.rearrange("p r t -> p (r t)").bitcast(F32).rearrange("p (r h) -> p r h", h=2),
                in_=bank.rearrange("p h r -> p r h"),
            )


        widen_in_halves(0)
        turn(0, 1)
        widen_in_halves(1)
        turn(1, 1)
        widen(2, 1, nc.vector.tensor_copy)
        widen(3, 1, copy_by_activation)
        turn(2, 2, logit_psum, "logits")
        widen(4, 2, nc.scalar.copy)
        ident_bank = proj_psum.tile([P, 2, P], F32, name="proj")
        turn_rows(ident_bank, ident_rows[:])
        turn(4, 2, logit_psum, "logits")
        widen(6, 2, nc.scalar.copy)
        permute_words()
        scale_slots(0, 1)
        scale_slots(1, 1)
        quantize_slots(0, 1)
        quantize_slots(1, 1)
        permute_scales()
        widen(8, 2, nc.gpsimd.tensor_copy, early[0])
        turn(6)
        project_queries(0, 2)
        lay_words(ident4[:], ident_bank[:])
        widen(10, 2, nc.scalar.copy)
        widen(12, 4, nc.scalar.copy)

        scale_slots(2)
        lay_queries(0, 1)
        lay_queries(1, 1)
        widen(16, 1, nc.scalar.copy)
        scale_slots(4)
        quantize(ident_codes[:], ident_scales[:], ident4[:])
        turn(8)
        project_keys()
        quantize_slots(2, 2)
        project_queries(2, 2)
        turn(10, 2, logit_psum, "logits")
        quantize_slots(4, 2)
        widen(20, 4, nc.gpsimd.tensor_copy, early[1][:, 4 * FEATURES :])
        key_bank = logit_psum.tile([P, 2, P], F32, name="logits")
        turn_rows(key_bank, key_rows[:], True)
        widen(17, 3, nc.scalar.copy)

        scale_slots(6)
        turn(12)
        project_queries(4, 2)
        scale_slots(8)
        scale_slots(10)
        lay_queries(2, 2)
        lay_queries(4, 2)
        lay_words(key4[:], key_bank[:])
        turn(18, 2, logit_psum, "logits")
        lay_plain(18)
        quantize_slots(6, 2)
        project_queries(6, 2)
        quantize_slots(8, FULL)
        quantize_queries(0, 2)
        turn(14)
        quantize_queries(2, FULL)
        quantize(key_codes[:], key_scales[:], key4[:])
        scale_plain(18, rooms[1][:, FULL * FEATURES :])
        project_queries(8, 2)
        multiply_keys(0, 2)
        multiply_keys(2, FULL)
        lay_queries(6, 2)
        widen(24, 1, nc.scalar.copy)
        project_queries(10, 2)

        scale_slots(12)
        scale_slots(14)
        find_tops(0)
        turn(16)
        find_tops(2)
        lay_queries(8, 3)
        negate_tops(0)
        lay_queries(11, 1)
        negate_tops(2)
        exponentiate(0)
        quantize_slots(12, 2)
        project_queries(12, 2)
        quantize_slots(14, 2)
        quantize_queries(6, 2)
        quantize_queries(8, FULL)
        widen(25, 3, nc.gpsimd.tensor_copy, rooms[2][:, 3 * FEATURES :])
        multiply_keys(6, 2)
        exponentiate(2)
        project_queries(14, 2)
        multiply_keys(8, FULL)

        scale_slots(16)
        find_tops(6)
        turn(20)
        find_tops(8)
        lay_queries(12, 3)
        lay_queries(15, 1)
        negate_tops(6)
        negate_tops(8)
        exponentiate(6)
        quantize_slots(16, 2)
        turn(22)
        project_queries(16, 2)
        invert_sums(0, 6)
        quantize_slots(18, 2)
        quantize_queries(12, FULL)
        divide_and_store(0, 6, nc.gpsimd, rooms[3])
        exponentiate(8)
        multiply_keys(12, FULL)
        project_queries(18, 1)
        project_queries(19, 1)

        scale_slots(20)
        scale_slots(22)
        turn(24)
        find_tops(12)
        lay_queries(16, 2)
        lay_queries(18, 2)
        negate_tops(12)
        widen(28, 2, nc.scalar.copy)
        quantize_slots(20, 2)
        project_queries(20, 2)
        invert_sums(6, 6)
        quantize_slots(22, 2)
        quantize_queries(16, FULL)
        divide_and_store(6, 6, nc.gpsimd, rooms[4])
        exponentiate(12)
        widen(30, 2, nc.scalar.copy)
        multiply_keys(16, FULL)
        turn(26)
        project_queries(22, 2)

        scale_slots(24)
        turn(28)
        lay_queries(20, 2)
        find_tops(16)
        scale_slots(26)
        lay_queries(22, 1)
        negate_tops(16)
        lay_queries(23, 1)
        turn(30, 1)
        quantize_queries(20, 2)
        multiply_keys(20, 2)
        quantize_slots(24, 2)
        invert_sums(12, 4)
        project_queries(24, 2)
        exponentiate(16)
        quantize_queries(22, 2)
        multiply_keys(22, 2)
        quantize_slots(26, 2)
        divide_and_store(12, 4, nc.gpsimd, scaled[0][:, 2 * FEATURES :])
        find_tops(20)
        invert_sums(16, 4)
        turn(31, 1, proj_psum, "proj")
        project_queries(26, 2)

        scale_slots(28)
        lay_queries(24, 1)
        negate_tops(20)
        lay_queries(25, 1)
        exponentiate(20)
        find_tops(22)
        scale_slots(30, 1)
        lay_queries(26, 1)
        negate_tops(22)
        lay_queries(27, 1)
        exponentiate(22)
        divide_and_store(16, 4)
        quantize_slots(28, 2)
        project_queries(28, 2)
        scale_slots(31, 1)
        quantize_slots(30, 1)
        quantize_queries(24, 2)
        quantize_slots(31, 1)
        multiply_keys(24, 2)
        project_queries(30, 2)
        quantize_queries(26, 2)
        multiply_keys(26, 2)
        invert_sums(20, 2)
        divide_and_store(20, 2, nc.gpsimd)
        invert_sums(22, 2)
        lay_queries(28, 1)
        find_tops(24)
        lay_queries(29, 1)
        lay_queries(30, 1, nc.vector.tensor_copy)
        negate_tops(24)
        lay_queries(31, 1)
        quantize_queries(28, 2)
        multiply_keys(28, 2, turn_psum, "turned")
        find_tops(26)
        exponentiate(24)
        quantize_queries(30, 1)
        multiply_keys(30, 1, turn_psum, "turned")
        quantize_queries(31, 1)
        multiply_keys(31, 1, proj_psum, "proj")
        divide_and_store(22, 2, negate=26)
        exponentiate(26)
        invert_sums(24, 2)
        divide_and_store(24, 2, nc.gpsimd)
        flip_logits(28)
        exponentiate(28)
        flip_logits(30)
        invert_sums(26, 2)
        flip_logits(31)
        exponentiate(30)
        exponentiate(31)
        divide_and_store(26, 2, nc.vector)
        invert_sums(30, 1)
        invert_sums(28, 2)
        divide_and_store(30, 1, queue=nc.scalar)
        invert_sums(31, 1)
        divide_and_store(28, 2, nc.vector)
        divide_and_store(31, 1, nc.vector)
